import numpy as np
import ml_dtypes

BF16 = ml_dtypes.bfloat16


def bf(x):
    return np.asarray(x, np.float32).astype(BF16)


def f32(x):
    return np.asarray(x, np.float32)


def f64(x):
    return np.asarray(x).astype(np.float64)


def striped(idx):
    return np.tile(idx.reshape(-1, 16).T, (8, 1))


B, L, D, NH, HD, S, T, N = 4, 512, 512, 8, 64, 4096, 128, 2048
EPS = 1e-12


def five(z):
    nxt = np.roll(z, -1, axis=3)
    first = np.broadcast_to(z[:, :, :, :1], z.shape).copy()
    first[:, :, :, 0] = z[:, :, :, -1]
    relay = np.broadcast_to(z.mean(axis=3, keepdims=True), z.shape)
    return np.stack([nxt, z, first, z, relay])


def setup_inputs():
    r = np.random.standard_normal
    return {
        "table": f32(r((D, S)) + 0.5 * r((D, 1))),
        "qw": bf(r((D, D)) / np.sqrt(D)),
        "qb": f32(0.1 * r((D, 1))),
        "kw": bf(r((D, D)) / np.sqrt(D)),
        "vw": bf(r((D, D)) / np.sqrt(D)),
        "vb": f32(0.1 * r((D, 1))),
        "ow": bf(r((D, D)) / np.sqrt(D)),
        "ob": f32(0.1 * r((D, 1))),
        "ln_w": f32(1.0 + 0.1 * r((D, 1))),
        "ln_b": f32(0.1 * r((D, 1))),
        "ofc_w": bf(r((D, T)) / np.sqrt(D)),
        "ofc_b": f32(0.1 * r((T, 1))),
        "offs": striped(np.random.permutation(S)[:N]),
    }


def reference(table, qw, qb, kw, vw, vb, ow, ob, ln_w, ln_b, ofc_w, ofc_b, offs):
    idx = offs[:16].T.reshape(-1)
    e = f64(table)[:, idx]
    q = (f64(qw).T @ e + f64(qb)).reshape(NH, HD, B, L)
    k = (f64(kw).T @ e).reshape(NH, HD, B, L)
    v = (f64(vw).T @ e + f64(vb)).reshape(NH, HD, B, L)
    k5, v5 = five(k), five(v)
    sc = (q[None] * k5).sum(axis=2) / np.sqrt(HD)
    p = np.exp(sc - sc.max(axis=0))
    p = p / p.sum(axis=0)
    ctx = (p[:, :, None] * v5).sum(axis=0).reshape(D, N)
    a = np.maximum(f64(ow).T @ ctx + f64(ob), 0.0)
    u = a.mean(axis=0)
    var = ((a - u) ** 2).mean(axis=0)
    y = f64(ln_w) * (a - u) / np.sqrt(var + EPS) + f64(ln_b)
    return f64(ofc_w).T @ y + f64(ofc_b)

@@ -1,0 +1,257 @@
+from contextlib import ExitStack
+
+import concourse.mybir as mybir
+from concourse.masks import make_identity
+
+F32 = mybir.dt.float32
+BF16 = mybir.dt.bfloat16
+U16 = mybir.dt.uint16
+ALU = mybir.AluOpType
+ACT = mybir.ActivationFunctionType
+AX = mybir.AxisListType
+
+P = 128
+D = 512
+KB = D // P
+S = 4096
+N = 2048
+L = 512
+B = N // L
+LQ = L // 4
+T = 128
+EPS = 1e-12
+NEXT, SELF, FIRST, RELAY = 0, 1, 2, 3
+
+FLOPS = 2 * N * (4 * D * D + D * T)
+
+
+def tile_ner_b_kernel(tc, table, qw, qb, kw, vw, vb, ow, ob, ln_w, ln_b, ofc_w, ofc_b, offs, out):
+    nc = tc.nc
+    with ExitStack() as ctx:
+        held = ctx.enter_context(tc.tile_pool(name="held", bufs=1))
+        qk_pool = ctx.enter_context(tc.tile_pool(name="qk", bufs=2))
+        v_pool = ctx.enter_context(tc.tile_pool(name="v", bufs=3))
+        score_pool = ctx.enter_context(tc.tile_pool(name="score", bufs=2))
+        small = ctx.enter_context(tc.tile_pool(name="small", bufs=4))
+        proj_ps = ctx.enter_context(tc.psum_pool(name="proj_ps", bufs=3))
+        sc_ps_pool = ctx.enter_context(tc.psum_pool(name="sc_ps", bufs=1))
+        bc_ps = ctx.enter_context(tc.psum_pool(name="bc_ps", bufs=2))
+        tr_ps = ctx.enter_context(tc.psum_pool(name="tr_ps", bufs=2))
+
+        offsets = held.tile([P, N // 16], U16, name="offsets")
+        nc.sync.dma_start(offsets[:], offs)
+
+        e16 = [held.tile([P, N], BF16, name=f"e16_{cb}") for cb in range(KB)]
+
+        def dealt(vec, name):
+            t = held.tile([P, KB], F32, name=name)
+            nc.scalar.dma_start(t[:], vec.rearrange("(p i) o -> p (i o)", i=KB))
+            return t
+
+        qb_t = dealt(qb, "qb_t")
+        vb_t = dealt(vb, "vb_t")
+        lnw_t = dealt(ln_w, "lnw_t")
+        lnb_t = dealt(ln_b, "lnb_t")
+        ofcb_t = held.tile([P, 1], F32, name="ofcb_t")
+        nc.scalar.dma_start(ofcb_t[:], ofc_b)
+        ob_bc = held.tile([P, D], F32, name="ob_bc")
+        nc.scalar.dma_start(ob_bc[:], ob.rearrange("m o -> (m o)").partition_broadcast(P))
+
+        with tc.tile_pool(name="table", bufs=1) as table_pool, tc.tile_pool(name="e32", bufs=4) as e32_pool:
+            tables = []
+            for cb in range(KB):
+                t = table_pool.tile([P, S], F32, name=f"table_{cb}")
+                nc.sync.dma_start(t[:], table[cb * P:(cb + 1) * P, :])
+                tables.append(t)
+
+            wk = held.tile([P, KB, D], BF16, name="wk")
+            wq = held.tile([P, KB, D], BF16, name="wq")
+            wv = held.tile([P, KB, D], BF16, name="wv")
+            for w_t, w in ((wk, kw), (wq, qw), (wv, vw)):
+                nc.sync.dma_start(w_t[:], w.rearrange("(k p) m -> p k m", p=P))
+            wo = held.tile([P, KB, D], BF16, name="wo")
+            nc.sync.dma_start(wo[:], ow.rearrange("(p i) m -> p i m", i=KB))
+            wf = held.tile([P, KB, T], BF16, name="wf")
+            nc.sync.dma_start(wf[:], ofc_w.rearrange("(p i) t -> p i t", i=KB))
+
+            ident = held.tile([P, P], F32, name="ident")
+            make_identity(nc, ident[:])
+            headsum = held.tile([P, 4, P], F32, name="headsum")
+            nc.gpsimd.memset(headsum[:], 0.125)
+            nc.gpsimd.affine_select(out=headsum[:], in_=headsum[:], compare_op=ALU.is_ge, fill=0.0,
+                                    base=0, pattern=[[512, 4], [-16, P]], channel_multiplier=1)
+            nc.gpsimd.affine_select(out=headsum[:], in_=headsum[:], compare_op=ALU.is_ge, fill=0.0,
+                                    base=15, pattern=[[-512, 4], [16, P]], channel_multiplier=-1)
+            spread = held.tile([P, 4, P], F32, name="spread")
+            nc.gpsimd.memset(spread[:], 1.0)
+            nc.gpsimd.affine_select(out=spread[:], in_=spread[:], compare_op=ALU.is_ge, fill=0.0,
+                                    base=0, pattern=[[512, 4], [1, P]], channel_multiplier=-16)
+            nc.gpsimd.affine_select(out=spread[:], in_=spread[:], compare_op=ALU.is_ge, fill=0.0,
+                                    base=15, pattern=[[-512, 4], [-1, P]], channel_multiplier=16)
+            neghalf = held.tile([P, 4], F32, name="neghalf")
+            nc.gpsimd.memset(neghalf[:], -0.5)
+
+            for cb in range(KB):
+                for b in range(B):
+                    e32 = e32_pool.tile([P, L], F32, name="e32")
+                    nc.scalar.activation(e32[:], tables[cb][:].indirect(offsets[:, b * (L // 16):(b + 1) * (L // 16)]), ACT.Copy)
+                    nc.vector.tensor_copy(e16[cb][:, b * L:(b + 1) * L], e32[:])
+
+        ctx_pool = ctx.enter_context(tc.tile_pool(name="ctx", bufs=2))
+        ln_pool = ctx.enter_context(tc.tile_pool(name="ln", bufs=2))
+
+        def project(w_t, b, i):
+            ps = proj_ps.tile([P, L], F32, name="ps")
+            cols = w_t.rearrange("p k (j i) -> p k i j", i=KB)
+            for cb in range(KB):
+                nc.tensor.matmul(ps[:], cols[:, cb, i, :], e16[cb][:, b * L:(b + 1) * L],
+                                 start=(cb == 0), stop=(cb == KB - 1))
+            return ps
+
+        kt, qt, vt, kr, vr, prob, ctx16 = {}, {}, {}, {}, {}, {}, {}
+
+        def project_kq(b):
+            kt[b] = qk_pool.tile([P, KB, L + 1], F32, name="kt")
+            ksum = small.tile([P, KB], F32, name="ksum")
+            for i in range(KB):
+                ps = project(wk, b, i)
+                nc.scalar.activation(kt[b][:, i, 0:L], ps[:], ACT.Copy, accum_out=ksum[:, i:i + 1])
+            nc.gpsimd.tensor_copy(kt[b][:, :, L:L + 1], kt[b][:, :, 0:1])
+            kr[b] = small.tile([P, KB], F32, name="kr")
+            nc.vector.tensor_scalar_mul(kr[b][:], ksum[:], 1.0 / L)
+            qt[b] = qk_pool.tile([P, KB, L], F32, name="qt")
+            for i in range(KB):
+                ps = project(wq, b, i)
+                nc.scalar.activation(qt[b][:, i, :], ps[:], ACT.Identity, bias=qb_t[:, i:i + 1])
+
+        def project_v(b):
+            vt[b] = v_pool.tile([P, KB, L + 1], F32, name="vt")
+            vsum = small.tile([P, KB], F32, name="vsum")
+            for i in range(KB):
+                ps = project(wv, b, i)
+                nc.scalar.activation(vt[b][:, i, 0:L], ps[:], ACT.Identity, bias=vb_t[:, i:i + 1],
+                                     accum_out=vsum[:, i:i + 1])
+            nc.gpsimd.tensor_copy(vt[b][:, :, L:L + 1], vt[b][:, :, 0:1])
+            vr[b] = small.tile([P, KB], F32, name="vr")
+            nc.vector.tensor_scalar_mul(vr[b][:], vsum[:], 1.0 / L)
+
+        def scores(b):
+            q, k = qt[b], kt[b]
+            part = score_pool.tile([P, 4, L], F32, name="part")
+            for kind, shift in ((SELF, 0), (NEXT, 1)):
+                prod = score_pool.tile([P, KB, L], F32, name="prod")
+                nc.vector.tensor_tensor(prod[:], q[:], k[:, :, shift:shift + L], ALU.mult)
+                half = score_pool.tile([P, 2, L], F32, name="half")
+                nc.gpsimd.tensor_tensor(half[:], prod[:, 0:2, :], prod[:, 2:4, :], ALU.add)
+                nc.gpsimd.tensor_tensor(part[:, kind, :], half[:, 0, :], half[:, 1, :], ALU.add)
+            nc.vector.tensor_scalar_mul(part[:, FIRST, 1:L], q[:, 0, 1:L], k[:, 0, 0:1])
+            nc.vector.tensor_scalar_mul(part[:, RELAY, :], q[:, 0, :], kr[b][:, 0:1])
+            for i in range(1, KB):
+                nc.vector.scalar_tensor_tensor(part[:, FIRST, 1:L], q[:, i, 1:L], k[:, i, 0:1], part[:, FIRST, 1:L],
+                                               ALU.mult, ALU.add)
+                nc.vector.scalar_tensor_tensor(part[:, RELAY, :], q[:, i, :], kr[b][:, i:i + 1], part[:, RELAY, :],
+                                               ALU.mult, ALU.add)
+            t0 = small.tile([P, KB, 1], F32, name="t0")
+            nc.vector.tensor_tensor(t0[:], q[:, :, 0:1], k[:, :, L - 1:L], ALU.mult)
+            nc.vector.reduce_sum(part[:, FIRST, 0:1], t0.rearrange("p i o -> p (i o)"), axis=AX.X)
+
+            sc = sc_ps_pool.tile([P, 4, LQ], F32, name="sc")
+            for qr in range(4):
+                nc.tensor.matmul(sc[:], headsum[:, qr, :], part[:, :, qr * LQ:(qr + 1) * LQ],
+                                 start=(qr == 0), stop=(qr == 3))
+            top = small.tile([P, LQ], F32, name="top")
+            nc.vector.tensor_reduce(top[:], sc.rearrange("p k t -> p t k"), axis=AX.X, op=ALU.max)
+            ex = small.tile([P, 4, LQ], F32, name="ex")
+            nc.vector.tensor_tensor(ex[:], sc[:], top[:].unsqueeze(1).to_broadcast([P, 4, LQ]), ALU.subtract)
+            nc.scalar.activation(ex[:], ex[:], ACT.Exp)
+            nc.vector.tensor_scalar_mul(ex[:, SELF, :], ex[:, SELF, :], 2.0)
+            den = small.tile([P, LQ], F32, name="den")
+            nc.vector.tensor_reduce(den[:], ex.rearrange("p k t -> p t k"), axis=AX.X, op=ALU.add)
+            nc.vector.reciprocal(den[:], den[:])
+            prob[b] = small.tile([P, 4, LQ], F32, name="prob")
+            nc.vector.tensor_tensor(prob[b][:], ex[:], den[:].unsqueeze(1).to_broadcast([P, 4, LQ]), ALU.mult)
+
+        def spread_prob(b, kind):
+            ps = bc_ps.tile([P, L], F32, name="pb")
+            for qr in range(4):
+                nc.tensor.matmul(ps[:, qr * LQ:(qr + 1) * LQ], spread[:, qr, :], prob[b][:, kind, :],
+                                 start=True, stop=True)
+            return ps
+
+        def context(b):
+            v = vt[b]
+            own = ctx_pool.tile([P, KB, L], F32, name="own")
+            nxt = ctx_pool.tile([P, KB, L], F32, name="nxt")
+            pb = spread_prob(b, SELF)
+            for i in range(KB):
+                nc.vector.tensor_tensor(own[:, i, :], pb[:], v[:, i, 0:L], ALU.mult)
+            pb = spread_prob(b, NEXT)
+            for i in range(KB):
+                nc.vector.tensor_tensor(nxt[:, i, :], pb[:], v[:, i, 1:L + 1], ALU.mult)
+            pb = spread_prob(b, FIRST)
+            for i in range(KB):
+                nc.vector.scalar_tensor_tensor(own[:, i, 1:L], pb[:, 1:L], v[:, i, 0:1], own[:, i, 1:L], ALU.mult, ALU.add)
+                nc.vector.scalar_tensor_tensor(own[:, i, 0:1], pb[:, 0:1], v[:, i, L - 1:L], own[:, i, 0:1], ALU.mult, ALU.add)
+            pb = spread_prob(b, RELAY)
+            for i in range(KB):
+                nc.vector.scalar_tensor_tensor(nxt[:, i, :], pb[:], vr[b][:, i:i + 1], nxt[:, i, :], ALU.mult, ALU.add)
+            ctx16[b] = ctx_pool.tile([P, KB, L], BF16, name="ctx16")
+            nc.gpsimd.tensor_tensor(ctx16[b][:], own[:], nxt[:], ALU.add)
+
+        def tagger(b):
+            a = ln_pool.tile([P, 4, D], F32, name="a")
+            asum = small.tile([P, 4], F32, name="asum")
+            for tb in range(4):
+                ps = proj_ps.tile([P, D], F32, name="ps")
+                for i in range(KB):
+                    nc.tensor.matmul(ps[:], ctx16[b][:, i, tb * P:(tb + 1) * P], wo[:, i, :],
+                                     start=(i == 0), stop=(i == KB - 1))
+                nc.vector.tensor_tensor(a[:, tb, :], ps[:], ob_bc[:], ALU.add)
+                nc.scalar.activation(a[:, tb, :], a[:, tb, :], ACT.Relu, accum_out=asum[:, tb:tb + 1])
+            negu = small.tile([P, 4], F32, name="negu")
+            nc.vector.tensor_scalar_mul(negu[:], asum[:], -1.0 / D)
+            ssq = small.tile([P, 4], F32, name="ssq")
+            for tb in range(4):
+                sq = ln_pool.tile([P, D], F32, name="sq")
+                nc.scalar.activation(sq[:], a[:, tb, :], ACT.Square, bias=negu[:, tb:tb + 1], accum_out=ssq[:, tb:tb + 1])
+            rstd = small.tile([P, 4], F32, name="rstd")
+            nc.vector.tensor_scalar(rstd[:], ssq[:], 1.0 / D, EPS, ALU.mult, ALU.add)
+            nc.gpsimd.tensor_tensor(rstd[:], rstd[:], neghalf[:], ALU.pow)
+            y16 = ln_pool.tile([P, KB, L], BF16, name="y16")
+            for tb in range(4):
+                z = ln_pool.tile([P, D], F32, name="z")
+                nc.vector.tensor_scalar(z[:], a[:, tb, :], negu[:, tb:tb + 1], rstd[:, tb:tb + 1], ALU.add, ALU.mult)
+                zt = tr_ps.tile([P, KB, P], F32, name="zt")
+                dealt_z = z.rearrange("t (j i) -> t i j", i=KB)
+                for i in range(KB):
+                    nc.tensor.transpose(zt[:, i, :], dealt_z[:, i, :], ident[:])
+                for i in range(KB):
+                    nc.scalar.activation(y16[:, i, tb * P:(tb + 1) * P], zt[:, i, :], ACT.Identity,
+                                         bias=lnb_t[:, i:i + 1], scale=lnw_t[:, i:i + 1])
+            ps = proj_ps.tile([T, L], F32, name="ps")
+            for i in range(KB):
+                nc.tensor.matmul(ps[:], wf[:, i, :], y16[:, i, :], start=(i == 0), stop=(i == KB - 1))
+            logits = ln_pool.tile([T, L], F32, name="logits")
+            nc.scalar.activation(logits[:], ps[:], ACT.Identity, bias=ofcb_t[:, 0:1])
+            nc.sync.dma_start(out[:, b * L:(b + 1) * L], logits[:])
+
+        project_kq(0)
+        project_kq(1)
+        project_v(0)
+        scores(0)
+        project_v(1)
+        context(0)
+        project_kq(2)
+        scores(1)
+        tagger(0)
+        context(1)
+        project_v(2)
+        project_kq(3)
+        scores(2)
+        tagger(1)
+        context(2)
+        project_v(3)
+        scores(3)
+        tagger(2)
+        context(3)
+        tagger(3)

@@ -17,8 +17,12 @@ S = 4096
 N = 2048
 L = 512
 B = N // L
-LQ = L // 4
+QN = L // P
 T = 128
+NH = 8
+HP = P // NH
+G = QN * NH
+ROWS = 3 * G
 EPS = 1e-12
 NEXT, SELF, FIRST, RELAY = 0, 1, 2, 3
 
@@ -27,16 +31,17 @@ FLOPS = 2 * N * (4 * D * D + D * T)
 
 def tile_ner_b_kernel(tc, table, qw, qb, kw, vw, vb, ow, ob, ln_w, ln_b, ofc_w, ofc_b, offs, out):
     nc = tc.nc
-    with ExitStack() as ctx:
-        held = ctx.enter_context(tc.tile_pool(name="held", bufs=1))
-        qk_pool = ctx.enter_context(tc.tile_pool(name="qk", bufs=2))
-        v_pool = ctx.enter_context(tc.tile_pool(name="v", bufs=3))
-        score_pool = ctx.enter_context(tc.tile_pool(name="score", bufs=2))
-        small = ctx.enter_context(tc.tile_pool(name="small", bufs=4))
-        proj_ps = ctx.enter_context(tc.psum_pool(name="proj_ps", bufs=3))
-        sc_ps_pool = ctx.enter_context(tc.psum_pool(name="sc_ps", bufs=1))
-        bc_ps = ctx.enter_context(tc.psum_pool(name="bc_ps", bufs=2))
-        tr_ps = ctx.enter_context(tc.psum_pool(name="tr_ps", bufs=2))
+    with ExitStack() as stack:
+        held = stack.enter_context(tc.tile_pool(name="held", bufs=1))
+        k_pool = stack.enter_context(tc.tile_pool(name="k", bufs=2))
+        v_pool = stack.enter_context(tc.tile_pool(name="v", bufs=2))
+        part_pool = stack.enter_context(tc.tile_pool(name="part", bufs=2))
+        prod_pool = stack.enter_context(tc.tile_pool(name="prod", bufs=3))
+        small = stack.enter_context(tc.tile_pool(name="small", bufs=3))
+        q_ps = stack.enter_context(tc.psum_pool(name="q_ps", bufs=2))
+        kvt_ps = stack.enter_context(tc.psum_pool(name="kvt_ps", bufs=3))
+        sm_ps = stack.enter_context(tc.psum_pool(name="sm_ps", bufs=1))
+        pb_ps = stack.enter_context(tc.psum_pool(name="pb_ps", bufs=2))
 
         offsets = held.tile([P, N // 16], U16, name="offsets")
         nc.sync.dma_start(offsets[:], offs)
@@ -54,10 +59,15 @@ def tile_ner_b_kernel(tc, table, qw, qb, kw, vw, vb, ow, ob, ln_w, ln_b, ofc_w, 
         lnb_t = dealt(ln_b, "lnb_t")
         ofcb_t = held.tile([P, 1], F32, name="ofcb_t")
         nc.scalar.dma_start(ofcb_t[:], ofc_b)
-        ob_bc = held.tile([P, D], F32, name="ob_bc")
-        nc.scalar.dma_start(ob_bc[:], ob.rearrange("m o -> (m o)").partition_broadcast(P))
 
-        with tc.tile_pool(name="table", bufs=1) as table_pool, tc.tile_pool(name="e32", bufs=4) as e32_pool:
+        def split3(src, hi, mid, lo, rest):
+            nc.vector.tensor_copy(hi, src)
+            nc.vector.tensor_tensor(rest, src, hi, ALU.subtract)
+            nc.vector.tensor_copy(mid, rest)
+            nc.vector.tensor_tensor(rest, rest, mid, ALU.subtract)
+            nc.vector.tensor_copy(lo, rest)
+
+        with tc.tile_pool(name="table", bufs=1) as table_pool, tc.tile_pool(name="start", bufs=1) as start_pool:
             tables = []
             for cb in range(KB):
                 t = table_pool.tile([P, S], F32, name=f"table_{cb}")
@@ -76,182 +86,237 @@ def tile_ner_b_kernel(tc, table, qw, qb, kw, vw, vb, ow, ob, ln_w, ln_b, ofc_w, 
 
             ident = held.tile([P, P], F32, name="ident")
             make_identity(nc, ident[:])
-            headsum = held.tile([P, 4, P], F32, name="headsum")
-            nc.gpsimd.memset(headsum[:], 0.125)
-            nc.gpsimd.affine_select(out=headsum[:], in_=headsum[:], compare_op=ALU.is_ge, fill=0.0,
-                                    base=0, pattern=[[512, 4], [-16, P]], channel_multiplier=1)
-            nc.gpsimd.affine_select(out=headsum[:], in_=headsum[:], compare_op=ALU.is_ge, fill=0.0,
-                                    base=15, pattern=[[-512, 4], [16, P]], channel_multiplier=-1)
-            spread = held.tile([P, 4, P], F32, name="spread")
-            nc.gpsimd.memset(spread[:], 1.0)
-            nc.gpsimd.affine_select(out=spread[:], in_=spread[:], compare_op=ALU.is_ge, fill=0.0,
-                                    base=0, pattern=[[512, 4], [1, P]], channel_multiplier=-16)
-            nc.gpsimd.affine_select(out=spread[:], in_=spread[:], compare_op=ALU.is_ge, fill=0.0,
-                                    base=15, pattern=[[-512, 4], [-1, P]], channel_multiplier=16)
-            neghalf = held.tile([P, 4], F32, name="neghalf")
+            ident16 = held.tile([P, P], BF16, name="ident16")
+            nc.gpsimd.tensor_copy(ident16[:], ident[:])
+            headsel = held.tile([P, NH], F32, name="headsel")
+            nc.gpsimd.memset(headsel[:], 0.125)
+            nc.gpsimd.affine_select(out=headsel[:], in_=headsel[:], compare_op=ALU.is_ge, fill=0.0,
+                                    base=0, pattern=[[-HP, NH]], channel_multiplier=1)
+            nc.gpsimd.affine_select(out=headsel[:], in_=headsel[:], compare_op=ALU.is_ge, fill=0.0,
+                                    base=HP - 1, pattern=[[HP, NH]], channel_multiplier=-1)
+            sel32 = start_pool.tile([ROWS, QN, P], F32, name="sel32")
+            nc.gpsimd.memset(sel32[:], 1.0)
+            nc.gpsimd.affine_select(out=sel32[:], in_=sel32[:], compare_op=ALU.is_ge, fill=0.0,
+                                    base=0, pattern=[[-3 * NH, QN], [-3, NH], [0, HP]], channel_multiplier=1)
+            nc.gpsimd.affine_select(out=sel32[:], in_=sel32[:], compare_op=ALU.is_ge, fill=0.0,
+                                    base=2, pattern=[[3 * NH, QN], [3, NH], [0, HP]], channel_multiplier=-1)
+            sel16 = held.tile([ROWS, QN, P], BF16, name="sel16")
+            nc.gpsimd.tensor_copy(sel16[:], sel32[:])
+            neghalf = held.tile([P, 1], F32, name="neghalf")
             nc.gpsimd.memset(neghalf[:], -0.5)
+
+            ones16 = held.tile([P, P], BF16, name="ones16")
+            nc.gpsimd.memset(ones16[:], 1.0)
+            ob3 = start_pool.tile([P, D], F32, name="ob3")
+            nc.gpsimd.memset(ob3[:], 0.0)
+            for row in (0, 32, 64):
+                nc.scalar.dma_start(ob3[row:row + 1, :], ob.rearrange("m o -> o m"))
+            ob_parts = start_pool.tile([P, 3, D], BF16, name="ob_parts")
+            ob_rest = start_pool.tile([P, D], F32, name="ob_rest")
+            split3(ob3[:], ob_parts[:, 0, :], ob_parts[:, 1, :], ob_parts[:, 2, :], ob_rest[:])
+            ob16 = held.tile([P, D], BF16, name="ob16")
+            nc.vector.tensor_copy(ob16[0:32, :], ob_parts[0:32, 0, :])
+            nc.vector.tensor_copy(ob16[32:64, :], ob_parts[32:64, 1, :])
+            nc.vector.tensor_copy(ob16[64:128, :], ob_parts[64:128, 2, :])
 
             for cb in range(KB):
                 for b in range(B):
-                    e32 = e32_pool.tile([P, L], F32, name="e32")
-                    nc.scalar.activation(e32[:], tables[cb][:].indirect(offsets[:, b * (L // 16):(b + 1) * (L // 16)]), ACT.Copy)
+                    e32 = start_pool.tile([P, L], F32, name="e32", bufs=4)
+                    piece = offsets[:, b * (L // 16):(b + 1) * (L // 16)]
+                    nc.scalar.activation(e32[:], tables[cb][:].indirect(piece), ACT.Copy)
                     nc.vector.tensor_copy(e16[cb][:, b * L:(b + 1) * L], e32[:])
 
-        ctx_pool = ctx.enter_context(tc.tile_pool(name="ctx", bufs=2))
-        ln_pool = ctx.enter_context(tc.tile_pool(name="ln", bufs=2))
+        ctx_pool = stack.enter_context(tc.tile_pool(name="ctx", bufs=2))
+        ln_pool = stack.enter_context(tc.tile_pool(name="ln", bufs=QN))
+        y_pool = stack.enter_context(tc.tile_pool(name="y", bufs=2))
 
-        def project(w_t, b, i):
-            ps = proj_ps.tile([P, L], F32, name="ps")
+        def project(pool, w_t, b, i):
+            ps = pool.tile([P, L], F32, name="ps")
             cols = w_t.rearrange("p k (j i) -> p k i j", i=KB)
             for cb in range(KB):
                 nc.tensor.matmul(ps[:], cols[:, cb, i, :], e16[cb][:, b * L:(b + 1) * L],
                                  start=(cb == 0), stop=(cb == KB - 1))
             return ps
 
-        kt, qt, vt, kr, vr, prob, ctx16 = {}, {}, {}, {}, {}, {}, {}
+        kt, ksum, kfix, cfix = {}, {}, {}, {}
+        vt, vsum, vr = {}, {}, {}
+        part, tok0, pr_t, probs = {}, {}, {}, {}
+        own_t, nxt_t, ctx16, z_t, y_t = {}, {}, {}, {}, {}
 
-        def project_kq(b):
-            kt[b] = qk_pool.tile([P, KB, L + 1], F32, name="kt")
-            ksum = small.tile([P, KB], F32, name="ksum")
-            for i in range(KB):
-                ps = project(wk, b, i)
-                nc.scalar.activation(kt[b][:, i, 0:L], ps[:], ACT.Copy, accum_out=ksum[:, i:i + 1])
-            nc.gpsimd.tensor_copy(kt[b][:, :, L:L + 1], kt[b][:, :, 0:1])
-            kr[b] = small.tile([P, KB], F32, name="kr")
-            nc.vector.tensor_scalar_mul(kr[b][:], ksum[:], 1.0 / L)
-            qt[b] = qk_pool.tile([P, KB, L], F32, name="qt")
-            for i in range(KB):
-                ps = project(wq, b, i)
-                nc.scalar.activation(qt[b][:, i, :], ps[:], ACT.Identity, bias=qb_t[:, i:i + 1])
+        def key_block(b, i):
+            if i == 0:
+                kt[b] = k_pool.tile([P, KB, L + 1], F32, name="kt")
+                ksum[b] = small.tile([P, KB], F32, name="ksum")
+            ps = project(kvt_ps, wk, b, i)
+            nc.scalar.activation(kt[b][:, i, 0:L], ps[:], ACT.Copy, accum_out=ksum[b][:, i:i + 1])
+            if i == KB - 1:
+                k = kt[b]
+                nc.gpsimd.tensor_copy(k[:, :, L:L + 1], k[:, :, 0:1])
+                fix = small.tile([P, 2, KB], F32, name="kfix")
+                nc.vector.tensor_copy(fix[:, 0, :], k[:, :, 0:1].rearrange("p i o -> p (i o)"))
+                nc.vector.tensor_scalar_mul(fix[:, 1, :], ksum[b][:], 1.0 / L)
+                qbk = small.tile([P, 2, KB], F32, name="qbk")
+                nc.vector.tensor_tensor(qbk[:], fix[:], qb_t[:].unsqueeze(1).to_broadcast([P, 2, KB]), ALU.mult)
+                cfix[b] = small.tile([P, 2], F32, name="cfix")
+                nc.vector.reduce_sum(cfix[b][:], qbk[:], axis=AX.X)
+                kfix[b] = fix
 
-        def project_v(b):
-            vt[b] = v_pool.tile([P, KB, L + 1], F32, name="vt")
-            vsum = small.tile([P, KB], F32, name="vsum")
-            for i in range(KB):
-                ps = project(wv, b, i)
-                nc.scalar.activation(vt[b][:, i, 0:L], ps[:], ACT.Identity, bias=vb_t[:, i:i + 1],
-                                     accum_out=vsum[:, i:i + 1])
-            nc.gpsimd.tensor_copy(vt[b][:, :, L:L + 1], vt[b][:, :, 0:1])
-            vr[b] = small.tile([P, KB], F32, name="vr")
-            nc.vector.tensor_scalar_mul(vr[b][:], vsum[:], 1.0 / L)
+        def value_block(b, i):
+            if i == 0:
+                vt[b] = v_pool.tile([P, KB, L + 1], F32, name="vt")
+                vsum[b] = small.tile([P, KB], F32, name="vsum")
+            ps = project(kvt_ps, wv, b, i)
+            nc.scalar.activation(vt[b][:, i, 0:L], ps[:], ACT.Identity, bias=vb_t[:, i:i + 1],
+                                 accum_out=vsum[b][:, i:i + 1])
+            if i == KB - 1:
+                nc.gpsimd.tensor_copy(vt[b][:, :, L:L + 1], vt[b][:, :, 0:1])
+                vr[b] = small.tile([P, KB], F32, name="vr")
+                nc.vector.tensor_scalar_mul(vr[b][:], vsum[b][:], 1.0 / L)
 
-        def scores(b):
-            q, k = qt[b], kt[b]
-            part = score_pool.tile([P, 4, L], F32, name="part")
+        def product_block(b, i):
+            if i == 0:
+                part[b] = part_pool.tile([P, 4, L], F32, name="part")
+                tok0[b] = small.tile([P, KB], F32, name="tok0")
+            k, fix, c, pt = kt[b], kfix[b], cfix[b], part[b]
+            ps = project(q_ps, wq, b, i)
+            bias = qb_t[:, i:i + 1]
             for kind, shift in ((SELF, 0), (NEXT, 1)):
-                prod = score_pool.tile([P, KB, L], F32, name="prod")
-                nc.vector.tensor_tensor(prod[:], q[:], k[:, :, shift:shift + L], ALU.mult)
-                half = score_pool.tile([P, 2, L], F32, name="half")
-                nc.gpsimd.tensor_tensor(half[:], prod[:, 0:2, :], prod[:, 2:4, :], ALU.add)
-                nc.gpsimd.tensor_tensor(part[:, kind, :], half[:, 0, :], half[:, 1, :], ALU.add)
-            nc.vector.tensor_scalar_mul(part[:, FIRST, 1:L], q[:, 0, 1:L], k[:, 0, 0:1])
-            nc.vector.tensor_scalar_mul(part[:, RELAY, :], q[:, 0, :], kr[b][:, 0:1])
-            for i in range(1, KB):
-                nc.vector.scalar_tensor_tensor(part[:, FIRST, 1:L], q[:, i, 1:L], k[:, i, 0:1], part[:, FIRST, 1:L],
-                                               ALU.mult, ALU.add)
-                nc.vector.scalar_tensor_tensor(part[:, RELAY, :], q[:, i, :], kr[b][:, i:i + 1], part[:, RELAY, :],
-                                               ALU.mult, ALU.add)
-            t0 = small.tile([P, KB, 1], F32, name="t0")
-            nc.vector.tensor_tensor(t0[:], q[:, :, 0:1], k[:, :, L - 1:L], ALU.mult)
-            nc.vector.reduce_sum(part[:, FIRST, 0:1], t0.rearrange("p i o -> p (i o)"), axis=AX.X)
+                if i == 0:
+                    nc.vector.scalar_tensor_tensor(pt[:, kind, :], ps[:], bias, k[:, i, shift:shift + L], ALU.add, ALU.mult)
+                else:
+                    prod = prod_pool.tile([P, L], F32, name=f"prod{kind}")
+                    nc.vector.scalar_tensor_tensor(prod[:], ps[:], bias, k[:, i, shift:shift + L], ALU.add, ALU.mult)
+                    nc.gpsimd.tensor_tensor(pt[:, kind, :], pt[:, kind, :], prod[:], ALU.add)
+            if i == 0:
+                nc.vector.tensor_scalar(pt[:, FIRST, 1:L], ps[:, 1:L], fix[:, 0, 0:1], c[:, 0:1], ALU.mult, ALU.add)
+                nc.vector.tensor_scalar(pt[:, RELAY, :], ps[:], fix[:, 1, 0:1], c[:, 1:2], ALU.mult, ALU.add)
+            else:
+                nc.vector.scalar_tensor_tensor(pt[:, FIRST, 1:L], ps[:, 1:L], fix[:, 0, i:i + 1], pt[:, FIRST, 1:L], ALU.mult, ALU.add)
+                nc.vector.scalar_tensor_tensor(pt[:, RELAY, :], ps[:], fix[:, 1, i:i + 1], pt[:, RELAY, :], ALU.mult, ALU.add)
+            nc.vector.scalar_tensor_tensor(tok0[b][:, i:i + 1], ps[:, 0:1], bias, k[:, i, L - 1:L], ALU.add, ALU.mult)
+            if i == KB - 1:
+                nc.vector.reduce_sum(pt[:, FIRST, 0:1], tok0[b][:], axis=AX.X)
 
-            sc = sc_ps_pool.tile([P, 4, LQ], F32, name="sc")
-            for qr in range(4):
-                nc.tensor.matmul(sc[:], headsum[:, qr, :], part[:, :, qr * LQ:(qr + 1) * LQ],
-                                 start=(qr == 0), stop=(qr == 3))
-            top = small.tile([P, LQ], F32, name="top")
-            nc.vector.tensor_reduce(top[:], sc.rearrange("p k t -> p t k"), axis=AX.X, op=ALU.max)
-            ex = small.tile([P, 4, LQ], F32, name="ex")
-            nc.vector.tensor_tensor(ex[:], sc[:], top[:].unsqueeze(1).to_broadcast([P, 4, LQ]), ALU.subtract)
-            nc.scalar.activation(ex[:], ex[:], ACT.Exp)
-            nc.vector.tensor_scalar_mul(ex[:, SELF, :], ex[:, SELF, :], 2.0)
-            den = small.tile([P, LQ], F32, name="den")
-            nc.vector.tensor_reduce(den[:], ex.rearrange("p k t -> p t k"), axis=AX.X, op=ALU.add)
+        def softmax_head(b):
+            sc = sm_ps.tile([P, 4, G], F32, name="sm")
+            for kind in range(4):
+                for c in range(QN):
+                    nc.tensor.matmul(sc[:, kind, c * NH:(c + 1) * NH], part[b][:, kind, c * P:(c + 1) * P], headsel[:],
+                                     start=True, stop=True)
+            top = small.tile([P, G], F32, name="top")
+            nc.vector.tensor_reduce(top[:], sc.rearrange("t k g -> t g k"), axis=AX.X, op=ALU.max)
+            pr = small.tile([P, 4, G], F32, name="pr")
+            nc.vector.tensor_tensor(pr[:], sc[:], top[:].unsqueeze(1).to_broadcast([P, 4, G]), ALU.subtract)
+            nc.scalar.activation(pr[:], pr[:], ACT.Exp)
+            pr_t[b] = pr
+
+        def softmax_tail(b):
+            pr = pr_t[b]
+            nc.vector.tensor_scalar_mul(pr[:, SELF, :], pr[:, SELF, :], 2.0)
+            den = small.tile([P, G], F32, name="den")
+            nc.vector.tensor_reduce(den[:], pr.rearrange("t k g -> t g k"), axis=AX.X, op=ALU.add)
             nc.vector.reciprocal(den[:], den[:])
-            prob[b] = small.tile([P, 4, LQ], F32, name="prob")
-            nc.vector.tensor_tensor(prob[b][:], ex[:], den[:].unsqueeze(1).to_broadcast([P, 4, LQ]), ALU.mult)
+            nc.vector.tensor_tensor(pr[:], pr[:], den[:].unsqueeze(1).to_broadcast([P, 4, G]), ALU.mult)
+            three = small.tile([P, 4, G, 3], BF16, name="three")
+            rest = small.tile([P, 4, G], F32, name="rest")
+            split3(pr[:], three[:, :, :, 0], three[:, :, :, 1], three[:, :, :, 2], rest[:])
+            flipped = sm_ps.tile([ROWS, 4, P], BF16, name="sm")
+            for kind in range(4):
+                nc.tensor.transpose(flipped[:, kind, :], three[:, kind, :, :].rearrange("t g j -> t (g j)"), ident16[:])
+            probs[b] = small.tile([ROWS, 4, P], BF16, name="probs")
+            nc.scalar.copy(probs[b][:], flipped[:])
 
-        def spread_prob(b, kind):
-            ps = bc_ps.tile([P, L], F32, name="pb")
-            for qr in range(4):
-                nc.tensor.matmul(ps[:, qr * LQ:(qr + 1) * LQ], spread[:, qr, :], prob[b][:, kind, :],
-                                 start=True, stop=True)
-            return ps
+        def context_kind(b, kind):
+            if kind == SELF:
+                own_t[b] = ctx_pool.tile([P, KB, L], F32, name="own")
+                nxt_t[b] = ctx_pool.tile([P, KB, L], F32, name="nxt")
+                ctx16[b] = ctx_pool.tile([P, KB, L], BF16, name="ctx16")
+            v, own, nxt = vt[b], own_t[b], nxt_t[b]
+            pb = pb_ps.tile([P, L], F32, name="pb")
+            for c in range(QN):
+                nc.tensor.matmul(pb[:, c * P:(c + 1) * P], sel16[:, c, :], probs[b][:, kind, :], start=True, stop=True)
+            for i in range(KB):
+                if kind == SELF:
+                    nc.vector.tensor_tensor(own[:, i, :], pb[:], v[:, i, 0:L], ALU.mult)
+                elif kind == NEXT:
+                    nc.vector.tensor_tensor(nxt[:, i, :], pb[:], v[:, i, 1:L + 1], ALU.mult)
+                elif kind == FIRST:
+                    nc.vector.scalar_tensor_tensor(own[:, i, 1:L], pb[:, 1:L], v[:, i, 0:1], own[:, i, 1:L], ALU.mult, ALU.add)
+                    nc.vector.scalar_tensor_tensor(own[:, i, 0:1], pb[:, 0:1], v[:, i, L - 1:L], own[:, i, 0:1], ALU.mult, ALU.add)
+                else:
+                    nc.vector.scalar_tensor_tensor(nxt[:, i, :], pb[:], vr[b][:, i:i + 1], nxt[:, i, :], ALU.mult, ALU.add)
+                    nc.gpsimd.tensor_tensor(ctx16[b][:, i, :], own[:, i, :], nxt[:, i, :], ALU.add)
 
-        def context(b):
-            v = vt[b]
-            own = ctx_pool.tile([P, KB, L], F32, name="own")
-            nxt = ctx_pool.tile([P, KB, L], F32, name="nxt")
-            pb = spread_prob(b, SELF)
+        def norm_block(b, tb):
+            ps = kvt_ps.tile([P, D], F32, name="ps")
             for i in range(KB):
-                nc.vector.tensor_tensor(own[:, i, :], pb[:], v[:, i, 0:L], ALU.mult)
-            pb = spread_prob(b, NEXT)
-            for i in range(KB):
-                nc.vector.tensor_tensor(nxt[:, i, :], pb[:], v[:, i, 1:L + 1], ALU.mult)
-            pb = spread_prob(b, FIRST)
-            for i in range(KB):
-                nc.vector.scalar_tensor_tensor(own[:, i, 1:L], pb[:, 1:L], v[:, i, 0:1], own[:, i, 1:L], ALU.mult, ALU.add)
-                nc.vector.scalar_tensor_tensor(own[:, i, 0:1], pb[:, 0:1], v[:, i, L - 1:L], own[:, i, 0:1], ALU.mult, ALU.add)
-            pb = spread_prob(b, RELAY)
-            for i in range(KB):
-                nc.vector.scalar_tensor_tensor(nxt[:, i, :], pb[:], vr[b][:, i:i + 1], nxt[:, i, :], ALU.mult, ALU.add)
-            ctx16[b] = ctx_pool.tile([P, KB, L], BF16, name="ctx16")
-            nc.gpsimd.tensor_tensor(ctx16[b][:], own[:], nxt[:], ALU.add)
-
-        def tagger(b):
-            a = ln_pool.tile([P, 4, D], F32, name="a")
-            asum = small.tile([P, 4], F32, name="asum")
-            for tb in range(4):
-                ps = proj_ps.tile([P, D], F32, name="ps")
-                for i in range(KB):
-                    nc.tensor.matmul(ps[:], ctx16[b][:, i, tb * P:(tb + 1) * P], wo[:, i, :],
-                                     start=(i == 0), stop=(i == KB - 1))
-                nc.vector.tensor_tensor(a[:, tb, :], ps[:], ob_bc[:], ALU.add)
-                nc.scalar.activation(a[:, tb, :], a[:, tb, :], ACT.Relu, accum_out=asum[:, tb:tb + 1])
-            negu = small.tile([P, 4], F32, name="negu")
-            nc.vector.tensor_scalar_mul(negu[:], asum[:], -1.0 / D)
-            ssq = small.tile([P, 4], F32, name="ssq")
-            for tb in range(4):
-                sq = ln_pool.tile([P, D], F32, name="sq")
-                nc.scalar.activation(sq[:], a[:, tb, :], ACT.Square, bias=negu[:, tb:tb + 1], accum_out=ssq[:, tb:tb + 1])
-            rstd = small.tile([P, 4], F32, name="rstd")
-            nc.vector.tensor_scalar(rstd[:], ssq[:], 1.0 / D, EPS, ALU.mult, ALU.add)
+                nc.tensor.matmul(ps[:], ctx16[b][:, i, tb * P:(tb + 1) * P], wo[:, i, :], start=(i == 0), stop=False)
+            nc.tensor.matmul(ps[:], ones16[:], ob16[:], start=False, stop=True)
+            a = ln_pool.tile([P, D], F32, name="a")
+            asum = ln_pool.tile([P, 1], F32, name="asum")
+            nc.scalar.activation(a[:], ps[:], ACT.Relu, accum_out=asum[:])
+            negu = ln_pool.tile([P, 1], F32, name="negu")
+            nc.scalar.mul(negu[:], asum[:], -1.0 / D)
+            sq = ln_pool.tile([P, D], F32, name="sq")
+            ssq = ln_pool.tile([P, 1], F32, name="ssq")
+            nc.scalar.activation(sq[:], a[:], ACT.Square, bias=negu[:], accum_out=ssq[:])
+            rstd = ln_pool.tile([P, 1], F32, name="rstd")
+            nc.gpsimd.tensor_scalar(rstd[:], ssq[:], 1.0 / D, EPS, ALU.mult, ALU.add)
             nc.gpsimd.tensor_tensor(rstd[:], rstd[:], neghalf[:], ALU.pow)
-            y16 = ln_pool.tile([P, KB, L], BF16, name="y16")
-            for tb in range(4):
-                z = ln_pool.tile([P, D], F32, name="z")
-                nc.vector.tensor_scalar(z[:], a[:, tb, :], negu[:, tb:tb + 1], rstd[:, tb:tb + 1], ALU.add, ALU.mult)
-                zt = tr_ps.tile([P, KB, P], F32, name="zt")
-                dealt_z = z.rearrange("t (j i) -> t i j", i=KB)
-                for i in range(KB):
-                    nc.tensor.transpose(zt[:, i, :], dealt_z[:, i, :], ident[:])
-                for i in range(KB):
-                    nc.scalar.activation(y16[:, i, tb * P:(tb + 1) * P], zt[:, i, :], ACT.Identity,
-                                         bias=lnb_t[:, i:i + 1], scale=lnw_t[:, i:i + 1])
-            ps = proj_ps.tile([T, L], F32, name="ps")
-            for i in range(KB):
-                nc.tensor.matmul(ps[:], wf[:, i, :], y16[:, i, :], start=(i == 0), stop=(i == KB - 1))
-            logits = ln_pool.tile([T, L], F32, name="logits")
-            nc.scalar.activation(logits[:], ps[:], ACT.Identity, bias=ofcb_t[:, 0:1])
-            nc.sync.dma_start(out[:, b * L:(b + 1) * L], logits[:])
+            shift = ln_pool.tile([P, 1], F32, name="shift")
+            nc.gpsimd.tensor_tensor(shift[:], negu[:], rstd[:], ALU.mult)
+            z = ln_pool.tile([P, D], F32, name="z")
+            nc.scalar.activation(z[:], a[:], ACT.Identity, bias=shift[:], scale=rstd[:])
+            z_t[b, tb] = z
 
-        project_kq(0)
-        project_kq(1)
-        project_v(0)
-        scores(0)
-        project_v(1)
-        context(0)
-        project_kq(2)
-        scores(1)
-        tagger(0)
-        context(1)
-        project_v(2)
-        project_kq(3)
-        scores(2)
-        tagger(1)
-        context(2)
-        project_v(3)
-        scores(3)
-        tagger(2)
-        context(3)
-        tagger(3)
+        def flip_block(b, tb):
+            if tb == 0:
+                y_t[b] = y_pool.tile([P, KB, L], BF16, name="y16")
+            zt = kvt_ps.tile([P, KB, P], F32, name="ps")
+            dealt_z = z_t[b, tb].rearrange("t (j i) -> t i j", i=KB)
+            for i in range(KB):
+                nc.tensor.transpose(zt[:, i, :], dealt_z[:, i, :], ident[:])
+            for i in range(KB):
+                nc.scalar.activation(y_t[b][:, i, tb * P:(tb + 1) * P], zt[:, i, :], ACT.Identity,
+                                     bias=lnb_t[:, i:i + 1], scale=lnw_t[:, i:i + 1])
+
+        def logits(b):
+            ps = kvt_ps.tile([T, L], F32, name="ps")
+            for i in range(KB):
+                nc.tensor.matmul(ps[:], wf[:, i, :], y_t[b][:, i, :], start=(i == 0), stop=(i == KB - 1))
+            res = y_pool.tile([T, L], F32, name="res")
+            nc.scalar.activation(res[:], ps[:], ACT.Identity, bias=ofcb_t[:, 0:1])
+            nc.sync.dma_start(out[:, b * L:(b + 1) * L], res[:])
+
+        for i in range(KB):
+            key_block(0, i)
+        for step in range(4 * B + 11):
+            b, i = divmod(step, 4)
+            if 0 <= b - 3 < B:
+                if i < 2:
+                    flip_block(b - 3, 2 * i)
+                    flip_block(b - 3, 2 * i + 1)
+                elif i == 2:
+                    logits(b - 3)
+            if 0 <= b - 2 < B:
+                if i == 0:
+                    context_kind(b - 2, FIRST)
+                elif i == 1:
+                    context_kind(b - 2, RELAY)
+                else:
+                    norm_block(b - 2, 2 * i - 4)
+                    norm_block(b - 2, 2 * i - 3)
+            if 0 <= b - 1 < B:
+                if i == 0:
+                    softmax_head(b - 1)
+                elif i == 1:
+                    softmax_tail(b - 1)
+                elif i == 2:
+                    context_kind(b - 1, SELF)
+                else:
+                    context_kind(b - 1, NEXT)
+            if b < B:
+                product_block(b, i)
+                if b + 1 < B:
+                    key_block(b + 1, i)
+                value_block(b, i)

@@ -22,6 +22,7 @@ T = 128
 NH = 8
 HP = P // NH
 G = QN * NH
+GA = B * G
 ROWS = 3 * G
 EPS = 1e-12
 NEXT, SELF, FIRST, RELAY = 0, 1, 2, 3
@@ -34,14 +35,11 @@ def tile_ner_b_kernel(tc, table, qw, qb, kw, vw, vb, ow, ob, ln_w, ln_b, ofc_w, 
     with ExitStack() as stack:
         held = stack.enter_context(tc.tile_pool(name="held", bufs=1))
         k_pool = stack.enter_context(tc.tile_pool(name="k", bufs=2))
-        v_pool = stack.enter_context(tc.tile_pool(name="v", bufs=2))
+        v_pool = stack.enter_context(tc.tile_pool(name="v", bufs=B))
         part_pool = stack.enter_context(tc.tile_pool(name="part", bufs=2))
-        prod_pool = stack.enter_context(tc.tile_pool(name="prod", bufs=3))
-        small = stack.enter_context(tc.tile_pool(name="small", bufs=3))
-        q_ps = stack.enter_context(tc.psum_pool(name="q_ps", bufs=2))
-        kvt_ps = stack.enter_context(tc.psum_pool(name="kvt_ps", bufs=3))
+        prod_pool = stack.enter_context(tc.tile_pool(name="prod", bufs=4))
+        small = stack.enter_context(tc.tile_pool(name="small", bufs=2))
         sm_ps = stack.enter_context(tc.psum_pool(name="sm_ps", bufs=1))
-        pb_ps = stack.enter_context(tc.psum_pool(name="pb_ps", bufs=2))
 
         offsets = held.tile([P, N // 16], U16, name="offsets")
         nc.sync.dma_start(offsets[:], offs)
@@ -102,7 +100,7 @@ def tile_ner_b_kernel(tc, table, qw, qb, kw, vw, vb, ow, ob, ln_w, ln_b, ofc_w, 
                                     base=2, pattern=[[3 * NH, QN], [3, NH], [0, HP]], channel_multiplier=-1)
             sel16 = held.tile([ROWS, QN, P], BF16, name="sel16")
             nc.gpsimd.tensor_copy(sel16[:], sel32[:])
-            neghalf = held.tile([P, 1], F32, name="neghalf")
+            neghalf = held.tile([P, QN], F32, name="neghalf")
             nc.gpsimd.memset(neghalf[:], -0.5)
 
             ones16 = held.tile([P, P], BF16, name="ones16")
@@ -127,7 +125,7 @@ def tile_ner_b_kernel(tc, table, qw, qb, kw, vw, vb, ow, ob, ln_w, ln_b, ofc_w, 
                     nc.vector.tensor_copy(e16[cb][:, b * L:(b + 1) * L], e32[:])
 
         ctx_pool = stack.enter_context(tc.tile_pool(name="ctx", bufs=2))
-        ln_pool = stack.enter_context(tc.tile_pool(name="ln", bufs=QN))
+        ln_pool = stack.enter_context(tc.tile_pool(name="ln", bufs=2))
         y_pool = stack.enter_context(tc.tile_pool(name="y", bufs=2))
 
         def project(pool, w_t, b, i):
@@ -138,185 +136,169 @@ def tile_ner_b_kernel(tc, table, qw, qb, kw, vw, vb, ow, ob, ln_w, ln_b, ofc_w, 
                                  start=(cb == 0), stop=(cb == KB - 1))
             return ps
 
-        kt, ksum, kfix, cfix = {}, {}, {}, {}
-        vt, vsum, vr = {}, {}, {}
-        part, tok0, pr_t, probs = {}, {}, {}, {}
-        own_t, nxt_t, ctx16, z_t, y_t = {}, {}, {}, {}, {}
+        kt, kfix, cfix, vt, vr, ctx16, z_t = {}, {}, {}, {}, {}, {}, {}
 
-        def key_block(b, i):
-            if i == 0:
-                kt[b] = k_pool.tile([P, KB, L + 1], F32, name="kt")
-                ksum[b] = small.tile([P, KB], F32, name="ksum")
-            ps = project(kvt_ps, wk, b, i)
-            nc.scalar.activation(kt[b][:, i, 0:L], ps[:], ACT.Copy, accum_out=ksum[b][:, i:i + 1])
-            if i == KB - 1:
-                k = kt[b]
-                nc.gpsimd.tensor_copy(k[:, :, L:L + 1], k[:, :, 0:1])
-                fix = small.tile([P, 2, KB], F32, name="kfix")
-                nc.vector.tensor_copy(fix[:, 0, :], k[:, :, 0:1].rearrange("p i o -> p (i o)"))
-                nc.vector.tensor_scalar_mul(fix[:, 1, :], ksum[b][:], 1.0 / L)
-                qbk = small.tile([P, 2, KB], F32, name="qbk")
-                nc.vector.tensor_tensor(qbk[:], fix[:], qb_t[:].unsqueeze(1).to_broadcast([P, 2, KB]), ALU.mult)
-                cfix[b] = small.tile([P, 2], F32, name="cfix")
-                nc.vector.reduce_sum(cfix[b][:], qbk[:], axis=AX.X)
-                kfix[b] = fix
+        def keys(b):
+            k = k_pool.tile([P, KB, L + 1], F32, name="kt")
+            ksum = small.tile([P, KB], F32, name="ksum")
+            for i in range(KB):
+                ps = project(kv_ps, wk, b, i)
+                nc.scalar.activation(k[:, i, 0:L], ps[:], ACT.Copy, accum_out=ksum[:, i:i + 1])
+            nc.gpsimd.tensor_copy(k[:, :, L:L + 1], k[:, :, 0:1])
+            fix = small.tile([P, 2, KB], F32, name="kfix")
+            nc.vector.tensor_copy(fix[:, 0, :], k[:, :, 0:1].rearrange("p i o -> p (i o)"))
+            nc.vector.tensor_scalar_mul(fix[:, 1, :], ksum[:], 1.0 / L)
+            qbk = small.tile([P, 2, KB], F32, name="qbk")
+            nc.vector.tensor_tensor(qbk[:], fix[:], qb_t[:].unsqueeze(1).to_broadcast([P, 2, KB]), ALU.mult)
+            cfix[b] = small.tile([P, 2], F32, name="cfix")
+            nc.vector.reduce_sum(cfix[b][:], qbk[:], axis=AX.X)
+            kt[b], kfix[b] = k, fix
 
-        def value_block(b, i):
-            if i == 0:
-                vt[b] = v_pool.tile([P, KB, L + 1], F32, name="vt")
-                vsum[b] = small.tile([P, KB], F32, name="vsum")
-            ps = project(kvt_ps, wv, b, i)
-            nc.scalar.activation(vt[b][:, i, 0:L], ps[:], ACT.Identity, bias=vb_t[:, i:i + 1],
-                                 accum_out=vsum[b][:, i:i + 1])
-            if i == KB - 1:
-                nc.gpsimd.tensor_copy(vt[b][:, :, L:L + 1], vt[b][:, :, 0:1])
-                vr[b] = small.tile([P, KB], F32, name="vr")
-                nc.vector.tensor_scalar_mul(vr[b][:], vsum[b][:], 1.0 / L)
+        def values(b):
+            v = v_pool.tile([P, KB, L + 1], F32, name="vt")
+            vsum = small.tile([P, KB], F32, name="vsum")
+            for i in range(KB):
+                ps = project(kv_ps, wv, b, i)
+                nc.scalar.activation(v[:, i, 0:L], ps[:], ACT.Identity, bias=vb_t[:, i:i + 1],
+                                     accum_out=vsum[:, i:i + 1])
+            nc.gpsimd.tensor_copy(v[:, :, L:L + 1], v[:, :, 0:1])
+            vr[b] = held.tile([P, KB], F32, name=f"vr{b}")
+            nc.vector.tensor_scalar_mul(vr[b][:], vsum[:], 1.0 / L)
+            vt[b] = v
 
-        def product_block(b, i):
-            if i == 0:
-                part[b] = part_pool.tile([P, 4, L], F32, name="part")
-                tok0[b] = small.tile([P, KB], F32, name="tok0")
-            k, fix, c, pt = kt[b], kfix[b], cfix[b], part[b]
-            ps = project(q_ps, wq, b, i)
-            bias = qb_t[:, i:i + 1]
-            for kind, shift in ((SELF, 0), (NEXT, 1)):
+        sc = sm_ps.tile([P, 4, GA], F32, name="sm")
+
+        def scores(b):
+            k, fix, c = kt[b], kfix[b], cfix[b]
+            pt = part_pool.tile([P, 4, L], F32, name="part")
+            tok0 = small.tile([P, KB], F32, name="tok0")
+            for i in range(KB):
+                ps = project(q_ps, wq, b, i)
+                bias = qb_t[:, i:i + 1]
+                nc.vector.scalar_tensor_tensor(tok0[:, i:i + 1], ps[:, 0:1], bias, k[:, i, L - 1:L], ALU.add, ALU.mult)
+                for kind, shift in ((SELF, 0), (NEXT, 1)):
+                    if i == 0:
+                        nc.vector.scalar_tensor_tensor(pt[:, kind, :], ps[:], bias, k[:, i, shift:shift + L], ALU.add, ALU.mult)
+                    else:
+                        prod = prod_pool.tile([P, L], F32, name=f"prod{kind}")
+                        nc.vector.scalar_tensor_tensor(prod[:], ps[:], bias, k[:, i, shift:shift + L], ALU.add, ALU.mult)
+                        nc.gpsimd.tensor_tensor(pt[:, kind, :], pt[:, kind, :], prod[:], ALU.add)
                 if i == 0:
-                    nc.vector.scalar_tensor_tensor(pt[:, kind, :], ps[:], bias, k[:, i, shift:shift + L], ALU.add, ALU.mult)
+                    nc.vector.tensor_scalar(pt[:, FIRST, 1:L], ps[:, 1:L], fix[:, 0, 0:1], c[:, 0:1], ALU.mult, ALU.add)
+                    nc.vector.tensor_scalar(pt[:, RELAY, :], ps[:], fix[:, 1, 0:1], c[:, 1:2], ALU.mult, ALU.add)
                 else:
-                    prod = prod_pool.tile([P, L], F32, name=f"prod{kind}")
-                    nc.vector.scalar_tensor_tensor(prod[:], ps[:], bias, k[:, i, shift:shift + L], ALU.add, ALU.mult)
-                    nc.gpsimd.tensor_tensor(pt[:, kind, :], pt[:, kind, :], prod[:], ALU.add)
-            if i == 0:
-                nc.vector.tensor_scalar(pt[:, FIRST, 1:L], ps[:, 1:L], fix[:, 0, 0:1], c[:, 0:1], ALU.mult, ALU.add)
-                nc.vector.tensor_scalar(pt[:, RELAY, :], ps[:], fix[:, 1, 0:1], c[:, 1:2], ALU.mult, ALU.add)
-            else:
-                nc.vector.scalar_tensor_tensor(pt[:, FIRST, 1:L], ps[:, 1:L], fix[:, 0, i:i + 1], pt[:, FIRST, 1:L], ALU.mult, ALU.add)
-                nc.vector.scalar_tensor_tensor(pt[:, RELAY, :], ps[:], fix[:, 1, i:i + 1], pt[:, RELAY, :], ALU.mult, ALU.add)
-            nc.vector.scalar_tensor_tensor(tok0[b][:, i:i + 1], ps[:, 0:1], bias, k[:, i, L - 1:L], ALU.add, ALU.mult)
-            if i == KB - 1:
-                nc.vector.reduce_sum(pt[:, FIRST, 0:1], tok0[b][:], axis=AX.X)
-
-        def softmax_head(b):
-            sc = sm_ps.tile([P, 4, G], F32, name="sm")
+                    nc.vector.scalar_tensor_tensor(pt[:, FIRST, 1:L], ps[:, 1:L], fix[:, 0, i:i + 1], pt[:, FIRST, 1:L], ALU.mult, ALU.add)
+                    nc.vector.scalar_tensor_tensor(pt[:, RELAY, :], ps[:], fix[:, 1, i:i + 1], pt[:, RELAY, :], ALU.mult, ALU.add)
+            nc.vector.reduce_sum(pt[:, FIRST, 0:1], tok0[:], axis=AX.X)
             for kind in range(4):
-                for c in range(QN):
-                    nc.tensor.matmul(sc[:, kind, c * NH:(c + 1) * NH], part[b][:, kind, c * P:(c + 1) * P], headsel[:],
-                                     start=True, stop=True)
-            top = small.tile([P, G], F32, name="top")
-            nc.vector.tensor_reduce(top[:], sc.rearrange("t k g -> t g k"), axis=AX.X, op=ALU.max)
-            pr = small.tile([P, 4, G], F32, name="pr")
-            nc.vector.tensor_tensor(pr[:], sc[:], top[:].unsqueeze(1).to_broadcast([P, 4, G]), ALU.subtract)
-            nc.scalar.activation(pr[:], pr[:], ACT.Exp)
-            pr_t[b] = pr
+                for c4 in range(QN):
+                    g = b * G + c4 * NH
+                    nc.tensor.matmul(sc[:, kind, g:g + NH], pt[:, kind, c4 * P:(c4 + 1) * P], headsel[:], start=True, stop=True)
 
-        def softmax_tail(b):
-            pr = pr_t[b]
+        probs = held.tile([ROWS, B, 4, P], BF16, name="probs")
+
+        def softmax():
+            top = small.tile([P, GA], F32, name="top")
+            nc.vector.tensor_reduce(top[:], sc.rearrange("t k g -> t g k"), axis=AX.X, op=ALU.max)
+            pr = small.tile([P, 4, GA], F32, name="pr")
+            nc.vector.tensor_tensor(pr[:], sc[:], top[:].unsqueeze(1).to_broadcast([P, 4, GA]), ALU.subtract)
+            nc.scalar.activation(pr[:], pr[:], ACT.Exp)
             nc.vector.tensor_scalar_mul(pr[:, SELF, :], pr[:, SELF, :], 2.0)
-            den = small.tile([P, G], F32, name="den")
+            den = small.tile([P, GA], F32, name="den")
             nc.vector.tensor_reduce(den[:], pr.rearrange("t k g -> t g k"), axis=AX.X, op=ALU.add)
             nc.vector.reciprocal(den[:], den[:])
-            nc.vector.tensor_tensor(pr[:], pr[:], den[:].unsqueeze(1).to_broadcast([P, 4, G]), ALU.mult)
-            three = small.tile([P, 4, G, 3], BF16, name="three")
-            rest = small.tile([P, 4, G], F32, name="rest")
+            nc.vector.tensor_tensor(pr[:], pr[:], den[:].unsqueeze(1).to_broadcast([P, 4, GA]), ALU.mult)
+            three = small.tile([P, 4, GA, 3], BF16, name="three")
+            rest = small.tile([P, 4, GA], F32, name="rest")
             split3(pr[:], three[:, :, :, 0], three[:, :, :, 1], three[:, :, :, 2], rest[:])
-            flipped = sm_ps.tile([ROWS, 4, P], BF16, name="sm")
-            for kind in range(4):
-                nc.tensor.transpose(flipped[:, kind, :], three[:, kind, :, :].rearrange("t g j -> t (g j)"), ident16[:])
-            probs[b] = small.tile([ROWS, 4, P], BF16, name="probs")
-            nc.scalar.copy(probs[b][:], flipped[:])
+            for pair in range(B // 2):
+                flipped = sm_ps.tile([ROWS, 2, 4, P], BF16, name="sm")
+                for b2 in range(2):
+                    b = 2 * pair + b2
+                    for kind in range(4):
+                        nc.tensor.transpose(flipped[:, b2, kind, :],
+                                            three[:, kind, b * G:(b + 1) * G, :].rearrange("t g j -> t (g j)"), ident16[:])
+                nc.scalar.copy(probs[:, 2 * pair:2 * pair + 2, :, :], flipped[:])
 
-        def context_kind(b, kind):
-            if kind == SELF:
-                own_t[b] = ctx_pool.tile([P, KB, L], F32, name="own")
-                nxt_t[b] = ctx_pool.tile([P, KB, L], F32, name="nxt")
-                ctx16[b] = ctx_pool.tile([P, KB, L], BF16, name="ctx16")
-            v, own, nxt = vt[b], own_t[b], nxt_t[b]
+        def spread(b, kind):
             pb = pb_ps.tile([P, L], F32, name="pb")
             for c in range(QN):
-                nc.tensor.matmul(pb[:, c * P:(c + 1) * P], sel16[:, c, :], probs[b][:, kind, :], start=True, stop=True)
-            for i in range(KB):
-                if kind == SELF:
-                    nc.vector.tensor_tensor(own[:, i, :], pb[:], v[:, i, 0:L], ALU.mult)
-                elif kind == NEXT:
-                    nc.vector.tensor_tensor(nxt[:, i, :], pb[:], v[:, i, 1:L + 1], ALU.mult)
-                elif kind == FIRST:
-                    nc.vector.scalar_tensor_tensor(own[:, i, 1:L], pb[:, 1:L], v[:, i, 0:1], own[:, i, 1:L], ALU.mult, ALU.add)
-                    nc.vector.scalar_tensor_tensor(own[:, i, 0:1], pb[:, 0:1], v[:, i, L - 1:L], own[:, i, 0:1], ALU.mult, ALU.add)
-                else:
-                    nc.vector.scalar_tensor_tensor(nxt[:, i, :], pb[:], vr[b][:, i:i + 1], nxt[:, i, :], ALU.mult, ALU.add)
-                    nc.gpsimd.tensor_tensor(ctx16[b][:, i, :], own[:, i, :], nxt[:, i, :], ALU.add)
+                nc.tensor.matmul(pb[:, c * P:(c + 1) * P], sel16[:, c, :], probs[:, b, kind, :], start=True, stop=True)
+            return pb
 
-        def norm_block(b, tb):
-            ps = kvt_ps.tile([P, D], F32, name="ps")
+        def context(b):
+            v = vt[b]
+            own = ctx_pool.tile([P, KB, L], F32, name="own")
+            nxt = ctx_pool.tile([P, KB, L], F32, name="nxt")
+            ctx16[b] = ctx_pool.tile([P, KB, L], BF16, name="ctx16")
+            pb = spread(b, SELF)
             for i in range(KB):
-                nc.tensor.matmul(ps[:], ctx16[b][:, i, tb * P:(tb + 1) * P], wo[:, i, :], start=(i == 0), stop=False)
-            nc.tensor.matmul(ps[:], ones16[:], ob16[:], start=False, stop=True)
-            a = ln_pool.tile([P, D], F32, name="a")
-            asum = ln_pool.tile([P, 1], F32, name="asum")
-            nc.scalar.activation(a[:], ps[:], ACT.Relu, accum_out=asum[:])
-            negu = ln_pool.tile([P, 1], F32, name="negu")
+                nc.vector.tensor_tensor(own[:, i, :], pb[:], v[:, i, 0:L], ALU.mult)
+            pb = spread(b, NEXT)
+            for i in range(KB):
+                nc.vector.tensor_tensor(nxt[:, i, :], pb[:], v[:, i, 1:L + 1], ALU.mult)
+            pb = spread(b, FIRST)
+            for i in range(KB):
+                nc.vector.scalar_tensor_tensor(own[:, i, 1:L], pb[:, 1:L], v[:, i, 0:1], own[:, i, 1:L], ALU.mult, ALU.add)
+                nc.vector.scalar_tensor_tensor(own[:, i, 0:1], pb[:, 0:1], v[:, i, L - 1:L], own[:, i, 0:1], ALU.mult, ALU.add)
+            pb = spread(b, RELAY)
+            for i in range(KB):
+                nc.vector.scalar_tensor_tensor(nxt[:, i, :], pb[:], vr[b][:, i:i + 1], nxt[:, i, :], ALU.mult, ALU.add)
+                nc.gpsimd.tensor_tensor(ctx16[b][:, i, :], own[:, i, :], nxt[:, i, :], ALU.add)
+
+        def norm(b):
+            a = ln_pool.tile([P, QN, D], F32, name="a")
+            asum = ln_pool.tile([P, QN], F32, name="asum")
+            for tb in range(QN):
+                ps = a_ps.tile([P, D], F32, name="a_ps")
+                for i in range(KB):
+                    nc.tensor.matmul(ps[:], ctx16[b][:, i, tb * P:(tb + 1) * P], wo[:, i, :], start=(i == 0), stop=False)
+                nc.tensor.matmul(ps[:], ones16[:], ob16[:], start=False, stop=True)
+                nc.scalar.activation(a[:, tb, :], ps[:], ACT.Relu, accum_out=asum[:, tb:tb + 1])
+            negu = ln_pool.tile([P, QN], F32, name="negu")
             nc.scalar.mul(negu[:], asum[:], -1.0 / D)
-            sq = ln_pool.tile([P, D], F32, name="sq")
-            ssq = ln_pool.tile([P, 1], F32, name="ssq")
-            nc.scalar.activation(sq[:], a[:], ACT.Square, bias=negu[:], accum_out=ssq[:])
-            rstd = ln_pool.tile([P, 1], F32, name="rstd")
+            ssq = ln_pool.tile([P, QN], F32, name="ssq")
+            for tb in range(QN):
+                sq = ln_pool.tile([P, D], F32, name="sq")
+                nc.scalar.activation(sq[:], a[:, tb, :], ACT.Square, bias=negu[:, tb:tb + 1], accum_out=ssq[:, tb:tb + 1])
+            rstd = ln_pool.tile([P, QN], F32, name="rstd")
             nc.gpsimd.tensor_scalar(rstd[:], ssq[:], 1.0 / D, EPS, ALU.mult, ALU.add)
             nc.gpsimd.tensor_tensor(rstd[:], rstd[:], neghalf[:], ALU.pow)
-            shift = ln_pool.tile([P, 1], F32, name="shift")
-            nc.gpsimd.tensor_tensor(shift[:], negu[:], rstd[:], ALU.mult)
-            z = ln_pool.tile([P, D], F32, name="z")
-            nc.scalar.activation(z[:], a[:], ACT.Identity, bias=shift[:], scale=rstd[:])
-            z_t[b, tb] = z
+            z = ln_pool.tile([P, QN, D], F32, name="z")
+            for tb in range(QN):
+                nc.gpsimd.tensor_scalar(z[:, tb, :], a[:, tb, :], negu[:, tb:tb + 1], rstd[:, tb:tb + 1], ALU.add, ALU.mult)
+            z_t[b] = z
 
-        def flip_block(b, tb):
-            if tb == 0:
-                y_t[b] = y_pool.tile([P, KB, L], BF16, name="y16")
-            zt = kvt_ps.tile([P, KB, P], F32, name="ps")
-            dealt_z = z_t[b, tb].rearrange("t (j i) -> t i j", i=KB)
+        def tags(b):
+            dealt_z = z_t[b].rearrange("t q (j i) -> t q i j", i=KB)
+            y16 = y_pool.tile([P, KB, L], BF16, name="y16")
             for i in range(KB):
-                nc.tensor.transpose(zt[:, i, :], dealt_z[:, i, :], ident[:])
+                zt = zt_ps.tile([P, L], F32, name="zt")
+                for tb in range(QN):
+                    nc.tensor.transpose(zt[:, tb * P:(tb + 1) * P], dealt_z[:, tb, i, :], ident[:])
+                nc.scalar.activation(y16[:, i, :], zt[:], ACT.Identity, bias=lnb_t[:, i:i + 1], scale=lnw_t[:, i:i + 1])
+            ps = zt_ps.tile([T, L], F32, name="zt")
             for i in range(KB):
-                nc.scalar.activation(y_t[b][:, i, tb * P:(tb + 1) * P], zt[:, i, :], ACT.Identity,
-                                     bias=lnb_t[:, i:i + 1], scale=lnw_t[:, i:i + 1])
-
-        def logits(b):
-            ps = kvt_ps.tile([T, L], F32, name="ps")
-            for i in range(KB):
-                nc.tensor.matmul(ps[:], wf[:, i, :], y_t[b][:, i, :], start=(i == 0), stop=(i == KB - 1))
+                nc.tensor.matmul(ps[:], wf[:, i, :], y16[:, i, :], start=(i == 0), stop=(i == KB - 1))
             res = y_pool.tile([T, L], F32, name="res")
             nc.scalar.activation(res[:], ps[:], ACT.Identity, bias=ofcb_t[:, 0:1])
             nc.sync.dma_start(out[:, b * L:(b + 1) * L], res[:])
 
-        for i in range(KB):
-            key_block(0, i)
-        for step in range(4 * B + 11):
-            b, i = divmod(step, 4)
-            if 0 <= b - 3 < B:
-                if i < 2:
-                    flip_block(b - 3, 2 * i)
-                    flip_block(b - 3, 2 * i + 1)
-                elif i == 2:
-                    logits(b - 3)
-            if 0 <= b - 2 < B:
-                if i == 0:
-                    context_kind(b - 2, FIRST)
-                elif i == 1:
-                    context_kind(b - 2, RELAY)
-                else:
-                    norm_block(b - 2, 2 * i - 4)
-                    norm_block(b - 2, 2 * i - 3)
-            if 0 <= b - 1 < B:
-                if i == 0:
-                    softmax_head(b - 1)
-                elif i == 1:
-                    softmax_tail(b - 1)
-                elif i == 2:
-                    context_kind(b - 1, SELF)
-                else:
-                    context_kind(b - 1, NEXT)
-            if b < B:
-                product_block(b, i)
+        with tc.psum_pool(name="q_ps", bufs=3) as q_ps, tc.psum_pool(name="kv_ps", bufs=4) as kv_ps:
+            keys(0)
+            for b in range(B):
                 if b + 1 < B:
-                    key_block(b + 1, i)
-                value_block(b, i)
+                    keys(b + 1)
+                scores(b)
+            for b in range(B):
+                values(b)
+        softmax()
+        with tc.psum_pool(name="pb_ps", bufs=2) as pb_ps, tc.psum_pool(name="a_ps", bufs=2) as a_ps, \
+                tc.psum_pool(name="zt_ps", bufs=2) as zt_ps:
+            for step in range(B + 2):
+                if step < B:
+                    context(step)
+                if 0 <= step - 1 < B:
+                    norm(step - 1)
+                if 0 <= step - 2 < B:
+                    tags(step - 2)

@@ -144,7 +144,7 @@ def tile_ner_b_kernel(tc, table, qw, qb, kw, vw, vb, ow, ob, ln_w, ln_b, ofc_w, 
             for i in range(KB):
                 ps = project(kv_ps, wk, b, i)
                 nc.scalar.activation(k[:, i, 0:L], ps[:], ACT.Copy, accum_out=ksum[:, i:i + 1])
-            nc.gpsimd.tensor_copy(k[:, :, L:L + 1], k[:, :, 0:1])
+            nc.vector.tensor_copy(k[:, :, L:L + 1], k[:, :, 0:1])
             fix = small.tile([P, 2, KB], F32, name="kfix")
             nc.vector.tensor_copy(fix[:, 0, :], k[:, :, 0:1].rearrange("p i o -> p (i o)"))
             nc.vector.tensor_scalar_mul(fix[:, 1, :], ksum[:], 1.0 / L)
@@ -161,7 +161,7 @@ def tile_ner_b_kernel(tc, table, qw, qb, kw, vw, vb, ow, ob, ln_w, ln_b, ofc_w, 
                 ps = project(kv_ps, wv, b, i)
                 nc.scalar.activation(v[:, i, 0:L], ps[:], ACT.Identity, bias=vb_t[:, i:i + 1],
                                      accum_out=vsum[:, i:i + 1])
-            nc.gpsimd.tensor_copy(v[:, :, L:L + 1], v[:, :, 0:1])
+            nc.vector.tensor_copy(v[:, :, L:L + 1], v[:, :, 0:1])
             vr[b] = held.tile([P, KB], F32, name=f"vr{b}")
             nc.vector.tensor_scalar_mul(vr[b][:], vsum[:], 1.0 / L)
             vt[b] = v
@@ -182,7 +182,7 @@ def tile_ner_b_kernel(tc, table, qw, qb, kw, vw, vb, ow, ob, ln_w, ln_b, ofc_w, 
                     else:
                         prod = prod_pool.tile([P, L], F32, name=f"prod{kind}")
                         nc.vector.scalar_tensor_tensor(prod[:], ps[:], bias, k[:, i, shift:shift + L], ALU.add, ALU.mult)
-                        nc.gpsimd.tensor_tensor(pt[:, kind, :], pt[:, kind, :], prod[:], ALU.add)
+                        nc.vector.tensor_tensor(pt[:, kind, :], pt[:, kind, :], prod[:], ALU.add)
                 if i == 0:
                     nc.vector.tensor_scalar(pt[:, FIRST, 1:L], ps[:, 1:L], fix[:, 0, 0:1], c[:, 0:1], ALU.mult, ALU.add)
                     nc.vector.tensor_scalar(pt[:, RELAY, :], ps[:], fix[:, 1, 0:1], c[:, 1:2], ALU.mult, ALU.add)
@@ -244,7 +244,7 @@ def tile_ner_b_kernel(tc, table, qw, qb, kw, vw, vb, ow, ob, ln_w, ln_b, ofc_w, 
             pb = spread(b, RELAY)
             for i in range(KB):
                 nc.vector.scalar_tensor_tensor(nxt[:, i, :], pb[:], vr[b][:, i:i + 1], nxt[:, i, :], ALU.mult, ALU.add)
-                nc.gpsimd.tensor_tensor(ctx16[b][:, i, :], own[:, i, :], nxt[:, i, :], ALU.add)
+                nc.vector.tensor_tensor(ctx16[b][:, i, :], own[:, i, :], nxt[:, i, :], ALU.add)
 
         def norm(b):
             a = ln_pool.tile([P, QN, D], F32, name="a")
@@ -264,9 +264,11 @@ def tile_ner_b_kernel(tc, table, qw, qb, kw, vw, vb, ow, ob, ln_w, ln_b, ofc_w, 
             rstd = ln_pool.tile([P, QN], F32, name="rstd")
             nc.gpsimd.tensor_scalar(rstd[:], ssq[:], 1.0 / D, EPS, ALU.mult, ALU.add)
             nc.gpsimd.tensor_tensor(rstd[:], rstd[:], neghalf[:], ALU.pow)
+            shift = ln_pool.tile([P, QN], F32, name="shift")
+            nc.gpsimd.tensor_tensor(shift[:], negu[:], rstd[:], ALU.mult)
             z = ln_pool.tile([P, QN, D], F32, name="z")
             for tb in range(QN):
-                nc.gpsimd.tensor_scalar(z[:, tb, :], a[:, tb, :], negu[:, tb:tb + 1], rstd[:, tb:tb + 1], ALU.add, ALU.mult)
+                nc.scalar.activation(z[:, tb, :], a[:, tb, :], ACT.Identity, bias=shift[:, tb:tb + 1], scale=rstd[:, tb:tb + 1])
             z_t[b] = z
 
         def tags(b):

@@ -22,7 +22,7 @@ T = 128
 NH = 8
 HP = P // NH
 G = QN * NH
-GA = B * G
+GP = 2 * G
 ROWS = 3 * G
 EPS = 1e-12
 NEXT, SELF, FIRST, RELAY = 0, 1, 2, 3
@@ -39,7 +39,7 @@ def tile_ner_b_kernel(tc, table, qw, qb, kw, vw, vb, ow, ob, ln_w, ln_b, ofc_w, 
         part_pool = stack.enter_context(tc.tile_pool(name="part", bufs=2))
         prod_pool = stack.enter_context(tc.tile_pool(name="prod", bufs=4))
         small = stack.enter_context(tc.tile_pool(name="small", bufs=2))
-        sm_ps = stack.enter_context(tc.psum_pool(name="sm_ps", bufs=1))
+        sm_ps = stack.enter_context(tc.psum_pool(name="sm_ps", bufs=2))
 
         offsets = held.tile([P, N // 16], U16, name="offsets")
         nc.sync.dma_start(offsets[:], offs)
@@ -100,6 +100,8 @@ def tile_ner_b_kernel(tc, table, qw, qb, kw, vw, vb, ow, ob, ln_w, ln_b, ofc_w, 
                                     base=2, pattern=[[3 * NH, QN], [3, NH], [0, HP]], channel_multiplier=-1)
             sel16 = held.tile([ROWS, QN, P], BF16, name="sel16")
             nc.gpsimd.tensor_copy(sel16[:], sel32[:])
+            zeros = held.tile([P, GP], F32, name="zeros")
+            nc.gpsimd.memset(zeros[:], 0.0)
             neghalf = held.tile([P, QN], F32, name="neghalf")
             nc.gpsimd.memset(neghalf[:], -0.5)
 
@@ -136,41 +138,47 @@ def tile_ner_b_kernel(tc, table, qw, qb, kw, vw, vb, ow, ob, ln_w, ln_b, ofc_w, 
                                  start=(cb == 0), stop=(cb == KB - 1))
             return ps
 
-        kt, kfix, cfix, vt, vr, ctx16, z_t = {}, {}, {}, {}, {}, {}, {}
+        kt, cfix, vt, vneg, vends, vr, ctx16, z_t = {}, {}, {}, {}, {}, {}, {}, {}
+
+        def project_all(pool, w_t, b, name):
+            x = pool.tile([P, KB, L + 1], F32, name=name)
+            xsum = small.tile([P, KB], F32, name=name + "_sum")
+            for i in range(KB):
+                ps = project(kv_ps, w_t, b, i)
+                nc.scalar.activation(x[:, i, 0:L], ps[:], ACT.Copy, accum_out=xsum[:, i:i + 1])
+            negmean = held.tile([P, KB], F32, name=f"{name}_negmean{b}")
+            nc.scalar.mul(negmean[:], xsum[:], -1.0 / L)
+            return x, negmean
 
         def keys(b):
-            k = k_pool.tile([P, KB, L + 1], F32, name="kt")
-            ksum = small.tile([P, KB], F32, name="ksum")
+            k, negmean = project_all(k_pool, wk, b, "kt")
             for i in range(KB):
-                ps = project(kv_ps, wk, b, i)
-                nc.scalar.activation(k[:, i, 0:L], ps[:], ACT.Copy, accum_out=ksum[:, i:i + 1])
+                nc.scalar.activation(k[:, i, 0:L], k[:, i, 0:L], ACT.Identity, bias=negmean[:, i:i + 1])
             nc.vector.tensor_copy(k[:, :, L:L + 1], k[:, :, 0:1])
-            fix = small.tile([P, 2, KB], F32, name="kfix")
-            nc.vector.tensor_copy(fix[:, 0, :], k[:, :, 0:1].rearrange("p i o -> p (i o)"))
-            nc.vector.tensor_scalar_mul(fix[:, 1, :], ksum[:], 1.0 / L)
-            qbk = small.tile([P, 2, KB], F32, name="qbk")
-            nc.vector.tensor_tensor(qbk[:], fix[:], qb_t[:].unsqueeze(1).to_broadcast([P, 2, KB]), ALU.mult)
-            cfix[b] = small.tile([P, 2], F32, name="cfix")
+            qbk = small.tile([P, KB], F32, name="qbk")
+            nc.vector.tensor_tensor(qbk[:], k[:, :, 0:1].rearrange("p i o -> p (i o)"), qb_t[:], ALU.mult)
+            cfix[b] = small.tile([P, 1], F32, name="cfix")
             nc.vector.reduce_sum(cfix[b][:], qbk[:], axis=AX.X)
-            kt[b], kfix[b] = k, fix
+            kt[b] = k
 
         def values(b):
-            v = v_pool.tile([P, KB, L + 1], F32, name="vt")
-            vsum = small.tile([P, KB], F32, name="vsum")
-            for i in range(KB):
-                ps = project(kv_ps, wv, b, i)
-                nc.scalar.activation(v[:, i, 0:L], ps[:], ACT.Identity, bias=vb_t[:, i:i + 1],
-                                     accum_out=vsum[:, i:i + 1])
+            v, negmean = project_all(v_pool, wv, b, "vt")
             nc.vector.tensor_copy(v[:, :, L:L + 1], v[:, :, 0:1])
-            vr[b] = held.tile([P, KB], F32, name=f"vr{b}")
-            nc.vector.tensor_scalar_mul(vr[b][:], vsum[:], 1.0 / L)
-            vt[b] = v
+            ends = held.tile([P, 2, KB], F32, name=f"ends{b}")
+            nc.vector.tensor_tensor(ends[:, 0, :], v[:, :, 0:1].rearrange("p i o -> p (i o)"), negmean[:], ALU.add)
+            nc.vector.tensor_tensor(ends[:, 1, :], v[:, :, L - 1:L].rearrange("p i o -> p (i o)"), negmean[:], ALU.add)
+            relay = held.tile([P, KB], F32, name=f"relay{b}")
+            nc.vector.tensor_tensor(relay[:], vb_t[:], negmean[:], ALU.subtract)
+            vt[b], vneg[b], vends[b], vr[b] = v, negmean, ends, relay
 
-        sc = sm_ps.tile([P, 4, GA], F32, name="sm")
+        sc, pr_t = {}, {}
 
         def scores(b):
-            k, fix, c = kt[b], kfix[b], cfix[b]
-            pt = part_pool.tile([P, 4, L], F32, name="part")
+            k = kt[b]
+            if b % 2 == 0:
+                sc[b // 2] = sm_ps.tile([P, 4, GP], F32, name="sm")
+                nc.tensor.matmul(sc[b // 2][:, RELAY, :], ident[:], zeros[:], start=True, stop=True)
+            pt = part_pool.tile([P, 3, L], F32, name="part")
             tok0 = small.tile([P, KB], F32, name="tok0")
             for i in range(KB):
                 ps = project(q_ps, wq, b, i)
@@ -184,41 +192,42 @@ def tile_ner_b_kernel(tc, table, qw, qb, kw, vw, vb, ow, ob, ln_w, ln_b, ofc_w, 
                         nc.vector.scalar_tensor_tensor(prod[:], ps[:], bias, k[:, i, shift:shift + L], ALU.add, ALU.mult)
                         nc.vector.tensor_tensor(pt[:, kind, :], pt[:, kind, :], prod[:], ALU.add)
                 if i == 0:
-                    nc.vector.tensor_scalar(pt[:, FIRST, 1:L], ps[:, 1:L], fix[:, 0, 0:1], c[:, 0:1], ALU.mult, ALU.add)
-                    nc.vector.tensor_scalar(pt[:, RELAY, :], ps[:], fix[:, 1, 0:1], c[:, 1:2], ALU.mult, ALU.add)
+                    nc.vector.tensor_scalar(pt[:, FIRST, 1:L], ps[:, 1:L], k[:, i, 0:1], cfix[b][:], ALU.mult, ALU.add)
                 else:
-                    nc.vector.scalar_tensor_tensor(pt[:, FIRST, 1:L], ps[:, 1:L], fix[:, 0, i:i + 1], pt[:, FIRST, 1:L], ALU.mult, ALU.add)
-                    nc.vector.scalar_tensor_tensor(pt[:, RELAY, :], ps[:], fix[:, 1, i:i + 1], pt[:, RELAY, :], ALU.mult, ALU.add)
+                    nc.vector.scalar_tensor_tensor(pt[:, FIRST, 1:L], ps[:, 1:L], k[:, i, 0:1], pt[:, FIRST, 1:L], ALU.mult, ALU.add)
             nc.vector.reduce_sum(pt[:, FIRST, 0:1], tok0[:], axis=AX.X)
-            for kind in range(4):
+            for kind in (NEXT, SELF, FIRST):
                 for c4 in range(QN):
-                    g = b * G + c4 * NH
-                    nc.tensor.matmul(sc[:, kind, g:g + NH], pt[:, kind, c4 * P:(c4 + 1) * P], headsel[:], start=True, stop=True)
+                    g = (b % 2) * G + c4 * NH
+                    nc.tensor.matmul(sc[b // 2][:, kind, g:g + NH], pt[:, kind, c4 * P:(c4 + 1) * P], headsel[:],
+                                     start=True, stop=True)
 
-        probs = held.tile([ROWS, B, 4, P], BF16, name="probs")
+        probs = held.tile([ROWS, B, 3, P], BF16, name="probs")
 
-        def softmax():
-            top = small.tile([P, GA], F32, name="top")
-            nc.vector.tensor_reduce(top[:], sc.rearrange("t k g -> t g k"), axis=AX.X, op=ALU.max)
-            pr = small.tile([P, 4, GA], F32, name="pr")
-            nc.vector.tensor_tensor(pr[:], sc[:], top[:].unsqueeze(1).to_broadcast([P, 4, GA]), ALU.subtract)
+        def softmax_exp(half):
+            top = small.tile([P, GP], F32, name="top")
+            nc.vector.tensor_reduce(top[:], sc[half].rearrange("t k g -> t g k"), axis=AX.X, op=ALU.max)
+            pr = small.tile([P, 4, GP], F32, name="pr")
+            nc.vector.tensor_tensor(pr[:], sc[half][:], top[:].unsqueeze(1).to_broadcast([P, 4, GP]), ALU.subtract)
             nc.scalar.activation(pr[:], pr[:], ACT.Exp)
+            pr_t[half] = pr
+
+        def softmax_norm(half):
+            pr = pr_t[half]
             nc.vector.tensor_scalar_mul(pr[:, SELF, :], pr[:, SELF, :], 2.0)
-            den = small.tile([P, GA], F32, name="den")
+            den = small.tile([P, GP], F32, name="den")
             nc.vector.tensor_reduce(den[:], pr.rearrange("t k g -> t g k"), axis=AX.X, op=ALU.add)
             nc.vector.reciprocal(den[:], den[:])
-            nc.vector.tensor_tensor(pr[:], pr[:], den[:].unsqueeze(1).to_broadcast([P, 4, GA]), ALU.mult)
-            three = small.tile([P, 4, GA, 3], BF16, name="three")
-            rest = small.tile([P, 4, GA], F32, name="rest")
-            split3(pr[:], three[:, :, :, 0], three[:, :, :, 1], three[:, :, :, 2], rest[:])
-            for pair in range(B // 2):
-                flipped = sm_ps.tile([ROWS, 2, 4, P], BF16, name="sm")
-                for b2 in range(2):
-                    b = 2 * pair + b2
-                    for kind in range(4):
-                        nc.tensor.transpose(flipped[:, b2, kind, :],
-                                            three[:, kind, b * G:(b + 1) * G, :].rearrange("t g j -> t (g j)"), ident16[:])
-                nc.scalar.copy(probs[:, 2 * pair:2 * pair + 2, :, :], flipped[:])
+            nc.vector.tensor_tensor(pr[:], pr[:], den[:].unsqueeze(1).to_broadcast([P, 4, GP]), ALU.mult)
+            three = small.tile([P, 3, GP, 3], BF16, name="three")
+            rest = small.tile([P, 3, GP], F32, name="rest")
+            split3(pr[:, 0:RELAY, :], three[:, :, :, 0], three[:, :, :, 1], three[:, :, :, 2], rest[:])
+            flipped = sm_ps.tile([ROWS, 2, 3, P], BF16, name="sm")
+            for b2 in range(2):
+                for kind in (NEXT, SELF, FIRST):
+                    nc.tensor.transpose(flipped[:, b2, kind, :],
+                                        three[:, kind, b2 * G:(b2 + 1) * G, :].rearrange("t g j -> t (g j)"), ident16[:])
+            nc.scalar.copy(probs[:, 2 * half:2 * half + 2, :, :], flipped[:])
 
         def spread(b, kind):
             pb = pb_ps.tile([P, L], F32, name="pb")
@@ -226,25 +235,28 @@ def tile_ner_b_kernel(tc, table, qw, qb, kw, vw, vb, ow, ob, ln_w, ln_b, ofc_w, 
                 nc.tensor.matmul(pb[:, c * P:(c + 1) * P], sel16[:, c, :], probs[:, b, kind, :], start=True, stop=True)
             return pb
 
-        def context(b):
-            v = vt[b]
+        own_t = {}
+
+        def context_own(b):
+            v, neg, ends = vt[b], vneg[b], vends[b]
             own = ctx_pool.tile([P, KB, L], F32, name="own")
-            nxt = ctx_pool.tile([P, KB, L], F32, name="nxt")
-            ctx16[b] = ctx_pool.tile([P, KB, L], BF16, name="ctx16")
             pb = spread(b, SELF)
             for i in range(KB):
-                nc.vector.tensor_tensor(own[:, i, :], pb[:], v[:, i, 0:L], ALU.mult)
-            pb = spread(b, NEXT)
-            for i in range(KB):
-                nc.vector.tensor_tensor(nxt[:, i, :], pb[:], v[:, i, 1:L + 1], ALU.mult)
+                nc.vector.scalar_tensor_tensor(own[:, i, :], v[:, i, 0:L], neg[:, i:i + 1], pb[:], ALU.add, ALU.mult)
             pb = spread(b, FIRST)
             for i in range(KB):
-                nc.vector.scalar_tensor_tensor(own[:, i, 1:L], pb[:, 1:L], v[:, i, 0:1], own[:, i, 1:L], ALU.mult, ALU.add)
-                nc.vector.scalar_tensor_tensor(own[:, i, 0:1], pb[:, 0:1], v[:, i, L - 1:L], own[:, i, 0:1], ALU.mult, ALU.add)
-            pb = spread(b, RELAY)
+                nc.vector.scalar_tensor_tensor(own[:, i, 1:L], pb[:, 1:L], ends[:, 0, i:i + 1], own[:, i, 1:L], ALU.mult, ALU.add)
+                nc.vector.scalar_tensor_tensor(own[:, i, 0:1], pb[:, 0:1], ends[:, 1, i:i + 1], own[:, i, 0:1], ALU.mult, ALU.add)
+            own_t[b] = own
+
+        def context_next(b):
+            v, neg, own = vt[b], vneg[b], own_t[b]
+            nxt = ctx_pool.tile([P, KB, L], F32, name="nxt")
+            ctx16[b] = ctx_pool.tile([P, KB, L], BF16, name="ctx16")
+            pb = spread(b, NEXT)
             for i in range(KB):
-                nc.vector.scalar_tensor_tensor(nxt[:, i, :], pb[:], vr[b][:, i:i + 1], nxt[:, i, :], ALU.mult, ALU.add)
-                nc.vector.tensor_tensor(ctx16[b][:, i, :], own[:, i, :], nxt[:, i, :], ALU.add)
+                nc.vector.scalar_tensor_tensor(nxt[:, i, :], v[:, i, 1:L + 1], neg[:, i:i + 1], pb[:], ALU.add, ALU.mult)
+                nc.vector.scalar_tensor_tensor(ctx16[b][:, i, :], nxt[:, i, :], vr[b][:, i:i + 1], own[:, i, :], ALU.add, ALU.add)
 
         def norm(b):
             a = ln_pool.tile([P, QN, D], F32, name="a")
@@ -286,21 +298,28 @@ def tile_ner_b_kernel(tc, table, qw, qb, kw, vw, vb, ow, ob, ln_w, ln_b, ofc_w, 
             nc.scalar.activation(res[:], ps[:], ACT.Identity, bias=ofcb_t[:, 0:1])
             nc.sync.dma_start(out[:, b * L:(b + 1) * L], res[:])
 
-        with tc.psum_pool(name="q_ps", bufs=3) as q_ps, tc.psum_pool(name="kv_ps", bufs=4) as kv_ps:
+        with tc.psum_pool(name="q_ps", bufs=3) as q_ps, tc.psum_pool(name="kv_ps", bufs=3) as kv_ps:
             keys(0)
             for b in range(B):
                 if b + 1 < B:
                     keys(b + 1)
                 scores(b)
-            for b in range(B):
                 values(b)
-        softmax()
+                if b == 1:
+                    softmax_exp(0)
+                if b == 2:
+                    softmax_norm(0)
         with tc.psum_pool(name="pb_ps", bufs=2) as pb_ps, tc.psum_pool(name="a_ps", bufs=2) as a_ps, \
                 tc.psum_pool(name="zt_ps", bufs=2) as zt_ps:
-            for step in range(B + 2):
-                if step < B:
-                    context(step)
-                if 0 <= step - 1 < B:
-                    norm(step - 1)
-                if 0 <= step - 2 < B:
-                    tags(step - 2)
+            for b in range(B + 2):
+                if b < B:
+                    context_own(b)
+                    if b == 0:
+                        softmax_exp(1)
+                    context_next(b)
+                    if b == 0:
+                        softmax_norm(1)
+                if 0 <= b - 1 < B:
+                    norm(b - 1)
+                if 0 <= b - 2 < B:
+                    tags(b - 2)

@@ -18,6 +18,8 @@ N = 2048
 L = 512
 B = N // L
 QN = L // P
+HQ = QN // 2
+LH = L // 2
 T = 128
 NH = 8
 HP = P // NH
@@ -102,7 +104,7 @@ def tile_ner_b_kernel(tc, table, qw, qb, kw, vw, vb, ow, ob, ln_w, ln_b, ofc_w, 
             nc.gpsimd.tensor_copy(sel16[:], sel32[:])
             zeros = held.tile([P, GP], F32, name="zeros")
             nc.gpsimd.memset(zeros[:], 0.0)
-            neghalf = held.tile([P, QN], F32, name="neghalf")
+            neghalf = held.tile([P, HQ], F32, name="neghalf")
             nc.gpsimd.memset(neghalf[:], -0.5)
 
             ones16 = held.tile([P, P], BF16, name="ones16")
@@ -127,7 +129,7 @@ def tile_ner_b_kernel(tc, table, qw, qb, kw, vw, vb, ow, ob, ln_w, ln_b, ofc_w, 
                     nc.vector.tensor_copy(e16[cb][:, b * L:(b + 1) * L], e32[:])
 
         ctx_pool = stack.enter_context(tc.tile_pool(name="ctx", bufs=2))
-        ln_pool = stack.enter_context(tc.tile_pool(name="ln", bufs=2))
+        ln_pool = stack.enter_context(tc.tile_pool(name="ln", bufs=3))
         y_pool = stack.enter_context(tc.tile_pool(name="y", bufs=2))
 
         def project(pool, w_t, b, i):
@@ -184,17 +186,16 @@ def tile_ner_b_kernel(tc, table, qw, qb, kw, vw, vb, ow, ob, ln_w, ln_b, ofc_w, 
                 ps = project(q_ps, wq, b, i)
                 bias = qb_t[:, i:i + 1]
                 nc.vector.scalar_tensor_tensor(tok0[:, i:i + 1], ps[:, 0:1], bias, k[:, i, L - 1:L], ALU.add, ALU.mult)
+                prod = {}
                 for kind, shift in ((SELF, 0), (NEXT, 1)):
-                    if i == 0:
-                        nc.vector.scalar_tensor_tensor(pt[:, kind, :], ps[:], bias, k[:, i, shift:shift + L], ALU.add, ALU.mult)
-                    else:
-                        prod = prod_pool.tile([P, L], F32, name=f"prod{kind}")
-                        nc.vector.scalar_tensor_tensor(prod[:], ps[:], bias, k[:, i, shift:shift + L], ALU.add, ALU.mult)
-                        nc.vector.tensor_tensor(pt[:, kind, :], pt[:, kind, :], prod[:], ALU.add)
+                    prod[kind] = pt[:, kind, :] if i == 0 else prod_pool.tile([P, L], F32, name=f"prod{kind}")[:]
+                    nc.vector.scalar_tensor_tensor(prod[kind], ps[:], bias, k[:, i, shift:shift + L], ALU.add, ALU.mult)
                 if i == 0:
                     nc.vector.tensor_scalar(pt[:, FIRST, 1:L], ps[:, 1:L], k[:, i, 0:1], cfix[b][:], ALU.mult, ALU.add)
                 else:
                     nc.vector.scalar_tensor_tensor(pt[:, FIRST, 1:L], ps[:, 1:L], k[:, i, 0:1], pt[:, FIRST, 1:L], ALU.mult, ALU.add)
+                    for kind in (SELF, NEXT):
+                        nc.vector.tensor_tensor(pt[:, kind, :], pt[:, kind, :], prod[kind], ALU.add)
             nc.vector.reduce_sum(pt[:, FIRST, 0:1], tok0[:], axis=AX.X)
             for kind in (NEXT, SELF, FIRST):
                 for c4 in range(QN):
@@ -254,49 +255,53 @@ def tile_ner_b_kernel(tc, table, qw, qb, kw, vw, vb, ow, ob, ln_w, ln_b, ofc_w, 
             nxt = ctx_pool.tile([P, KB, L], F32, name="nxt")
             ctx16[b] = ctx_pool.tile([P, KB, L], BF16, name="ctx16")
             pb = spread(b, NEXT)
-            for i in range(KB):
-                nc.vector.scalar_tensor_tensor(nxt[:, i, :], v[:, i, 1:L + 1], neg[:, i:i + 1], pb[:], ALU.add, ALU.mult)
-                nc.vector.scalar_tensor_tensor(ctx16[b][:, i, :], nxt[:, i, :], vr[b][:, i:i + 1], own[:, i, :], ALU.add, ALU.add)
+            for i in range(KB + 1):
+                if i < KB:
+                    nc.vector.scalar_tensor_tensor(nxt[:, i, :], v[:, i, 1:L + 1], neg[:, i:i + 1], pb[:], ALU.add, ALU.mult)
+                if i >= 1:
+                    nc.vector.scalar_tensor_tensor(ctx16[b][:, i - 1, :], nxt[:, i - 1, :], vr[b][:, i - 1:i], own[:, i - 1, :],
+                                                   ALU.add, ALU.add)
 
-        def norm(b):
-            a = ln_pool.tile([P, QN, D], F32, name="a")
-            asum = ln_pool.tile([P, QN], F32, name="asum")
-            for tb in range(QN):
+        def norm(b, h):
+            a = ln_pool.tile([P, HQ, D], F32, name="a")
+            asum = ln_pool.tile([P, HQ], F32, name="asum")
+            for tb in range(HQ):
+                t0 = (h * HQ + tb) * P
                 ps = a_ps.tile([P, D], F32, name="a_ps")
                 for i in range(KB):
-                    nc.tensor.matmul(ps[:], ctx16[b][:, i, tb * P:(tb + 1) * P], wo[:, i, :], start=(i == 0), stop=False)
+                    nc.tensor.matmul(ps[:], ctx16[b][:, i, t0:t0 + P], wo[:, i, :], start=(i == 0), stop=False)
                 nc.tensor.matmul(ps[:], ones16[:], ob16[:], start=False, stop=True)
                 nc.scalar.activation(a[:, tb, :], ps[:], ACT.Relu, accum_out=asum[:, tb:tb + 1])
-            negu = ln_pool.tile([P, QN], F32, name="negu")
+            negu = ln_pool.tile([P, HQ], F32, name="negu")
             nc.scalar.mul(negu[:], asum[:], -1.0 / D)
-            ssq = ln_pool.tile([P, QN], F32, name="ssq")
-            for tb in range(QN):
+            ssq = ln_pool.tile([P, HQ], F32, name="ssq")
+            for tb in range(HQ):
                 sq = ln_pool.tile([P, D], F32, name="sq")
                 nc.scalar.activation(sq[:], a[:, tb, :], ACT.Square, bias=negu[:, tb:tb + 1], accum_out=ssq[:, tb:tb + 1])
-            rstd = ln_pool.tile([P, QN], F32, name="rstd")
+            rstd = ln_pool.tile([P, HQ], F32, name="rstd")
             nc.gpsimd.tensor_scalar(rstd[:], ssq[:], 1.0 / D, EPS, ALU.mult, ALU.add)
             nc.gpsimd.tensor_tensor(rstd[:], rstd[:], neghalf[:], ALU.pow)
-            shift = ln_pool.tile([P, QN], F32, name="shift")
+            shift = ln_pool.tile([P, HQ], F32, name="shift")
             nc.gpsimd.tensor_tensor(shift[:], negu[:], rstd[:], ALU.mult)
-            z = ln_pool.tile([P, QN, D], F32, name="z")
-            for tb in range(QN):
+            z = ln_pool.tile([P, HQ, D], F32, name="z")
+            for tb in range(HQ):
                 nc.scalar.activation(z[:, tb, :], a[:, tb, :], ACT.Identity, bias=shift[:, tb:tb + 1], scale=rstd[:, tb:tb + 1])
-            z_t[b] = z
+            z_t[b, h] = z
 
-        def tags(b):
-            dealt_z = z_t[b].rearrange("t q (j i) -> t q i j", i=KB)
-            y16 = y_pool.tile([P, KB, L], BF16, name="y16")
+        def tags(b, h):
+            dealt_z = z_t[b, h].rearrange("t q (j i) -> t q i j", i=KB)
+            y16 = y_pool.tile([P, KB, LH], BF16, name="y16")
             for i in range(KB):
-                zt = zt_ps.tile([P, L], F32, name="zt")
-                for tb in range(QN):
+                zt = zt_ps.tile([P, LH], F32, name="zt")
+                for tb in range(HQ):
                     nc.tensor.transpose(zt[:, tb * P:(tb + 1) * P], dealt_z[:, tb, i, :], ident[:])
                 nc.scalar.activation(y16[:, i, :], zt[:], ACT.Identity, bias=lnb_t[:, i:i + 1], scale=lnw_t[:, i:i + 1])
-            ps = zt_ps.tile([T, L], F32, name="zt")
+            ps = zt_ps.tile([T, LH], F32, name="zt")
             for i in range(KB):
                 nc.tensor.matmul(ps[:], wf[:, i, :], y16[:, i, :], start=(i == 0), stop=(i == KB - 1))
-            res = y_pool.tile([T, L], F32, name="res")
+            res = y_pool.tile([T, LH], F32, name="res")
             nc.scalar.activation(res[:], ps[:], ACT.Identity, bias=ofcb_t[:, 0:1])
-            nc.sync.dma_start(out[:, b * L:(b + 1) * L], res[:])
+            nc.sync.dma_start(out[:, b * L + h * LH:b * L + (h + 1) * LH], res[:])
 
         with tc.psum_pool(name="q_ps", bufs=3) as q_ps, tc.psum_pool(name="kv_ps", bufs=3) as kv_ps:
             keys(0)
@@ -311,7 +316,7 @@ def tile_ner_b_kernel(tc, table, qw, qb, kw, vw, vb, ow, ob, ln_w, ln_b, ofc_w, 
                     softmax_norm(0)
         with tc.psum_pool(name="pb_ps", bufs=2) as pb_ps, tc.psum_pool(name="a_ps", bufs=2) as a_ps, \
                 tc.psum_pool(name="zt_ps", bufs=2) as zt_ps:
-            for b in range(B + 2):
+            for b in range(B + 1):
                 if b < B:
                     context_own(b)
                     if b == 0:
@@ -319,7 +324,8 @@ def tile_ner_b_kernel(tc, table, qw, qb, kw, vw, vb, ow, ob, ln_w, ln_b, ofc_w, 
                     context_next(b)
                     if b == 0:
                         softmax_norm(1)
-                if 0 <= b - 1 < B:
-                    norm(b - 1)
-                if 0 <= b - 2 < B:
-                    tags(b - 2)
+                if b >= 1:
+                    norm(b - 1, 0)
+                    norm(b - 1, 1)
+                    tags(b - 1, 0)
+                    tags(b - 1, 1)

@@ -281,11 +281,9 @@ def tile_ner_b_kernel(tc, table, qw, qb, kw, vw, vb, ow, ob, ln_w, ln_b, ofc_w, 
             rstd = ln_pool.tile([P, HQ], F32, name="rstd")
             nc.gpsimd.tensor_scalar(rstd[:], ssq[:], 1.0 / D, EPS, ALU.mult, ALU.add)
             nc.gpsimd.tensor_tensor(rstd[:], rstd[:], neghalf[:], ALU.pow)
-            shift = ln_pool.tile([P, HQ], F32, name="shift")
-            nc.gpsimd.tensor_tensor(shift[:], negu[:], rstd[:], ALU.mult)
             z = ln_pool.tile([P, HQ, D], F32, name="z")
             for tb in range(HQ):
-                nc.scalar.activation(z[:, tb, :], a[:, tb, :], ACT.Identity, bias=shift[:, tb:tb + 1], scale=rstd[:, tb:tb + 1])
+                nc.vector.tensor_scalar(z[:, tb, :], a[:, tb, :], negu[:, tb:tb + 1], rstd[:, tb:tb + 1], ALU.add, ALU.mult)
             z_t[b, h] = z
 
         def tags(b, h):

@@ -42,6 +42,8 @@ def tile_ner_b_kernel(tc, table, qw, qb, kw, vw, vb, ow, ob, ln_w, ln_b, ofc_w, 
         prod_pool = stack.enter_context(tc.tile_pool(name="prod", bufs=4))
         small = stack.enter_context(tc.tile_pool(name="small", bufs=2))
         sm_ps = stack.enter_context(tc.psum_pool(name="sm_ps", bufs=2))
+        ring_v = stack.enter_context(tc.psum_pool(name="ring_v", bufs=3))
+        ring_s = stack.enter_context(tc.psum_pool(name="ring_s", bufs=3))
 
         offsets = held.tile([P, N // 16], U16, name="offsets")
         nc.sync.dma_start(offsets[:], offs)
@@ -133,7 +135,7 @@ def tile_ner_b_kernel(tc, table, qw, qb, kw, vw, vb, ow, ob, ln_w, ln_b, ofc_w, 
         y_pool = stack.enter_context(tc.tile_pool(name="y", bufs=2))
 
         def project(pool, w_t, b, i):
-            ps = pool.tile([P, L], F32, name="ps")
+            ps = pool.tile([P, L], F32, name="ring")
             cols = w_t.rearrange("p k (j i) -> p k i j", i=KB)
             for cb in range(KB):
                 nc.tensor.matmul(ps[:], cols[:, cb, i, :], e16[cb][:, b * L:(b + 1) * L],
@@ -142,65 +144,91 @@ def tile_ner_b_kernel(tc, table, qw, qb, kw, vw, vb, ow, ob, ln_w, ln_b, ofc_w, 
 
         kt, cfix, vt, vneg, vends, vr, ctx16, z_t = {}, {}, {}, {}, {}, {}, {}, {}
 
-        def project_all(pool, w_t, b, name):
+        def open_projection(pool, name):
             x = pool.tile([P, KB, L + 1], F32, name=name)
             xsum = small.tile([P, KB], F32, name=name + "_sum")
-            for i in range(KB):
-                ps = project(kv_ps, w_t, b, i)
-                nc.scalar.activation(x[:, i, 0:L], ps[:], ACT.Copy, accum_out=xsum[:, i:i + 1])
-            negmean = held.tile([P, KB], F32, name=f"{name}_negmean{b}")
-            nc.scalar.mul(negmean[:], xsum[:], -1.0 / L)
-            return x, negmean
+            return x, xsum
 
-        def keys(b):
-            k, negmean = project_all(k_pool, wk, b, "kt")
+        def project_block(w_t, b, i, x, xsum):
+            ps = project(ring_s, w_t, b, i)
+            nc.scalar.activation(x[:, i, 0:L], ps[:], ACT.Copy, accum_out=xsum[:, i:i + 1])
+
+        def minus_mean(xsum, name):
+            negmean = held.tile([P, KB], F32, name=name)
+            nc.scalar.mul(negmean[:], xsum[:], -1.0 / L)
+            return negmean
+
+        ksum, vsum = {}, {}
+
+        def keys_open(b):
+            kt[b], ksum[b] = open_projection(k_pool, "kt")
+
+        def key_block(b, i):
+            project_block(wk, b, i, kt[b], ksum[b])
+
+        def keys_center(b):
+            negmean = minus_mean(ksum[b], f"kt_negmean{b}")
             for i in range(KB):
-                nc.scalar.activation(k[:, i, 0:L], k[:, i, 0:L], ACT.Identity, bias=negmean[:, i:i + 1])
+                nc.scalar.activation(kt[b][:, i, 0:L], kt[b][:, i, 0:L], ACT.Identity, bias=negmean[:, i:i + 1])
+
+        def keys_edge(b):
+            k = kt[b]
             nc.vector.tensor_copy(k[:, :, L:L + 1], k[:, :, 0:1])
             qbk = small.tile([P, KB], F32, name="qbk")
             nc.vector.tensor_tensor(qbk[:], k[:, :, 0:1].rearrange("p i o -> p (i o)"), qb_t[:], ALU.mult)
             cfix[b] = small.tile([P, 1], F32, name="cfix")
             nc.vector.reduce_sum(cfix[b][:], qbk[:], axis=AX.X)
-            kt[b] = k
 
-        def values(b):
-            v, negmean = project_all(v_pool, wv, b, "vt")
+        def values_open(b):
+            vt[b], vsum[b] = open_projection(v_pool, "vt")
+
+        def value_block(b, i):
+            project_block(wv, b, i, vt[b], vsum[b])
+
+        def values_edge(b):
+            v = vt[b]
+            negmean = minus_mean(vsum[b], f"vt_negmean{b}")
             nc.vector.tensor_copy(v[:, :, L:L + 1], v[:, :, 0:1])
             ends = held.tile([P, 2, KB], F32, name=f"ends{b}")
             nc.vector.tensor_tensor(ends[:, 0, :], v[:, :, 0:1].rearrange("p i o -> p (i o)"), negmean[:], ALU.add)
             nc.vector.tensor_tensor(ends[:, 1, :], v[:, :, L - 1:L].rearrange("p i o -> p (i o)"), negmean[:], ALU.add)
             relay = held.tile([P, KB], F32, name=f"relay{b}")
             nc.vector.tensor_tensor(relay[:], vb_t[:], negmean[:], ALU.subtract)
-            vt[b], vneg[b], vends[b], vr[b] = v, negmean, ends, relay
+            vneg[b], vends[b], vr[b] = negmean, ends, relay
 
-        sc, pr_t = {}, {}
+        sc, pr_t, three_t, part, tok0_t = {}, {}, {}, {}, {}
 
-        def scores(b):
-            k = kt[b]
+        def scores_open(b):
+            part[b] = part_pool.tile([P, 3, L], F32, name="part")
+            tok0_t[b] = small.tile([P, KB], F32, name="tok0")
+
+        def score_block(b, i):
+            k, pt, tok0 = kt[b], part[b], tok0_t[b]
+            ps = project(ring_v, wq, b, i)
+            bias = qb_t[:, i:i + 1]
+            nc.vector.scalar_tensor_tensor(tok0[:, i:i + 1], ps[:, 0:1], bias, k[:, i, L - 1:L], ALU.add, ALU.mult)
+            prod = {}
+            for kind, shift in ((SELF, 0), (NEXT, 1)):
+                prod[kind] = pt[:, kind, :] if i == 0 else prod_pool.tile([P, L], F32, name=f"prod{kind}")[:]
+                nc.vector.scalar_tensor_tensor(prod[kind], ps[:], bias, k[:, i, shift:shift + L], ALU.add, ALU.mult)
+            if i == 0:
+                nc.vector.tensor_scalar(pt[:, FIRST, 1:L], ps[:, 1:L], k[:, i, 0:1], cfix[b][:], ALU.mult, ALU.add)
+            else:
+                nc.vector.scalar_tensor_tensor(pt[:, FIRST, 1:L], ps[:, 1:L], k[:, i, 0:1], pt[:, FIRST, 1:L], ALU.mult, ALU.add)
+                for kind in (SELF, NEXT):
+                    nc.vector.tensor_tensor(pt[:, kind, :], pt[:, kind, :], prod[kind], ALU.add)
+
+        def scores_edge(b):
+            nc.vector.reduce_sum(part[b][:, FIRST, 0:1], tok0_t[b][:], axis=AX.X)
+
+        def head_sums(b):
             if b % 2 == 0:
                 sc[b // 2] = sm_ps.tile([P, 4, GP], F32, name="sm")
                 nc.tensor.matmul(sc[b // 2][:, RELAY, :], ident[:], zeros[:], start=True, stop=True)
-            pt = part_pool.tile([P, 3, L], F32, name="part")
-            tok0 = small.tile([P, KB], F32, name="tok0")
-            for i in range(KB):
-                ps = project(q_ps, wq, b, i)
-                bias = qb_t[:, i:i + 1]
-                nc.vector.scalar_tensor_tensor(tok0[:, i:i + 1], ps[:, 0:1], bias, k[:, i, L - 1:L], ALU.add, ALU.mult)
-                prod = {}
-                for kind, shift in ((SELF, 0), (NEXT, 1)):
-                    prod[kind] = pt[:, kind, :] if i == 0 else prod_pool.tile([P, L], F32, name=f"prod{kind}")[:]
-                    nc.vector.scalar_tensor_tensor(prod[kind], ps[:], bias, k[:, i, shift:shift + L], ALU.add, ALU.mult)
-                if i == 0:
-                    nc.vector.tensor_scalar(pt[:, FIRST, 1:L], ps[:, 1:L], k[:, i, 0:1], cfix[b][:], ALU.mult, ALU.add)
-                else:
-                    nc.vector.scalar_tensor_tensor(pt[:, FIRST, 1:L], ps[:, 1:L], k[:, i, 0:1], pt[:, FIRST, 1:L], ALU.mult, ALU.add)
-                    for kind in (SELF, NEXT):
-                        nc.vector.tensor_tensor(pt[:, kind, :], pt[:, kind, :], prod[kind], ALU.add)
-            nc.vector.reduce_sum(pt[:, FIRST, 0:1], tok0[:], axis=AX.X)
             for kind in (NEXT, SELF, FIRST):
                 for c4 in range(QN):
                     g = (b % 2) * G + c4 * NH
-                    nc.tensor.matmul(sc[b // 2][:, kind, g:g + NH], pt[:, kind, c4 * P:(c4 + 1) * P], headsel[:],
+                    nc.tensor.matmul(sc[b // 2][:, kind, g:g + NH], part[b][:, kind, c4 * P:(c4 + 1) * P], headsel[:],
                                      start=True, stop=True)
 
         probs = held.tile([ROWS, B, 3, P], BF16, name="probs")
@@ -223,6 +251,10 @@ def tile_ner_b_kernel(tc, table, qw, qb, kw, vw, vb, ow, ob, ln_w, ln_b, ofc_w, 
             three = small.tile([P, 3, GP, 3], BF16, name="three")
             rest = small.tile([P, 3, GP], F32, name="rest")
             split3(pr[:, 0:RELAY, :], three[:, :, :, 0], three[:, :, :, 1], three[:, :, :, 2], rest[:])
+            three_t[half] = three
+
+        def softmax_flip(half):
+            three = three_t[half]
             flipped = sm_ps.tile([ROWS, 2, 3, P], BF16, name="sm")
             for b2 in range(2):
                 for kind in (NEXT, SELF, FIRST):
@@ -230,50 +262,55 @@ def tile_ner_b_kernel(tc, table, qw, qb, kw, vw, vb, ow, ob, ln_w, ln_b, ofc_w, 
                                         three[:, kind, b2 * G:(b2 + 1) * G, :].rearrange("t g j -> t (g j)"), ident16[:])
             nc.scalar.copy(probs[:, 2 * half:2 * half + 2, :, :], flipped[:])
 
-        def spread(b, kind):
-            pb = pb_ps.tile([P, L], F32, name="pb")
-            for c in range(QN):
-                nc.tensor.matmul(pb[:, c * P:(c + 1) * P], sel16[:, c, :], probs[:, b, kind, :], start=True, stop=True)
-            return pb
+        pb_t, own_t, a_t, asum_t, negu_t, rstd_t, y_t = {}, {}, {}, {}, {}, {}, {}
 
-        own_t = {}
+        def spread(b, h, kind):
+            pb = ring_v.tile([P, LH], F32, name="ring")
+            for tb in range(HQ):
+                nc.tensor.matmul(pb[:, tb * P:(tb + 1) * P], sel16[:, h * HQ + tb, :], probs[:, b, kind, :], start=True, stop=True)
+            pb_t[b, h, kind] = pb
 
-        def context_own(b):
-            v, neg, ends = vt[b], vneg[b], vends[b]
-            own = ctx_pool.tile([P, KB, L], F32, name="own")
-            pb = spread(b, SELF)
+        def context_self(b, h):
+            v, neg, pb, t0 = vt[b], vneg[b], pb_t[b, h, SELF], h * LH
+            own = ctx_pool.tile([P, KB, LH], F32, name="own")
             for i in range(KB):
-                nc.vector.scalar_tensor_tensor(own[:, i, :], v[:, i, 0:L], neg[:, i:i + 1], pb[:], ALU.add, ALU.mult)
-            pb = spread(b, FIRST)
-            for i in range(KB):
-                nc.vector.scalar_tensor_tensor(own[:, i, 1:L], pb[:, 1:L], ends[:, 0, i:i + 1], own[:, i, 1:L], ALU.mult, ALU.add)
-                nc.vector.scalar_tensor_tensor(own[:, i, 0:1], pb[:, 0:1], ends[:, 1, i:i + 1], own[:, i, 0:1], ALU.mult, ALU.add)
-            own_t[b] = own
+                nc.vector.scalar_tensor_tensor(own[:, i, :], v[:, i, t0:t0 + LH], neg[:, i:i + 1], pb[:], ALU.add, ALU.mult)
+            own_t[b, h] = own
 
-        def context_next(b):
-            v, neg, own = vt[b], vneg[b], own_t[b]
-            nxt = ctx_pool.tile([P, KB, L], F32, name="nxt")
-            ctx16[b] = ctx_pool.tile([P, KB, L], BF16, name="ctx16")
-            pb = spread(b, NEXT)
+        def context_first(b, h):
+            own, ends, pb = own_t[b, h], vends[b], pb_t[b, h, FIRST]
+            skip = 1 if h == 0 else 0
+            for i in range(KB):
+                nc.vector.scalar_tensor_tensor(own[:, i, skip:LH], pb[:, skip:LH], ends[:, 0, i:i + 1], own[:, i, skip:LH],
+                                               ALU.mult, ALU.add)
+                if h == 0:
+                    nc.vector.scalar_tensor_tensor(own[:, i, 0:1], pb[:, 0:1], ends[:, 1, i:i + 1], own[:, i, 0:1], ALU.mult, ALU.add)
+
+        def context_next(b, h):
+            v, neg, own, pb, t0 = vt[b], vneg[b], own_t[b, h], pb_t[b, h, NEXT], h * LH
+            nxt = ctx_pool.tile([P, KB, LH], F32, name="nxt")
+            ctx16[b, h] = ctx_pool.tile([P, KB, LH], BF16, name="ctx16")
             for i in range(KB + 1):
                 if i < KB:
-                    nc.vector.scalar_tensor_tensor(nxt[:, i, :], v[:, i, 1:L + 1], neg[:, i:i + 1], pb[:], ALU.add, ALU.mult)
+                    nc.vector.scalar_tensor_tensor(nxt[:, i, :], v[:, i, t0 + 1:t0 + LH + 1], neg[:, i:i + 1], pb[:], ALU.add, ALU.mult)
                 if i >= 1:
-                    nc.vector.scalar_tensor_tensor(ctx16[b][:, i - 1, :], nxt[:, i - 1, :], vr[b][:, i - 1:i], own[:, i - 1, :],
+                    nc.vector.scalar_tensor_tensor(ctx16[b, h][:, i - 1, :], nxt[:, i - 1, :], vr[b][:, i - 1:i], own[:, i - 1, :],
                                                    ALU.add, ALU.add)
 
-        def norm(b, h):
-            a = ln_pool.tile([P, HQ, D], F32, name="a")
-            asum = ln_pool.tile([P, HQ], F32, name="asum")
+        def hidden(b, h):
+            a_t[b, h] = ln_pool.tile([P, HQ, D], F32, name="a")
+            asum_t[b, h] = ln_pool.tile([P, HQ], F32, name="asum")
             for tb in range(HQ):
-                t0 = (h * HQ + tb) * P
-                ps = a_ps.tile([P, D], F32, name="a_ps")
+                ps = ring_s.tile([P, D], F32, name="ring")
                 for i in range(KB):
-                    nc.tensor.matmul(ps[:], ctx16[b][:, i, t0:t0 + P], wo[:, i, :], start=(i == 0), stop=False)
+                    nc.tensor.matmul(ps[:], ctx16[b, h][:, i, tb * P:(tb + 1) * P], wo[:, i, :], start=(i == 0), stop=False)
                 nc.tensor.matmul(ps[:], ones16[:], ob16[:], start=False, stop=True)
-                nc.scalar.activation(a[:, tb, :], ps[:], ACT.Relu, accum_out=asum[:, tb:tb + 1])
+                nc.scalar.activation(a_t[b, h][:, tb, :], ps[:], ACT.Relu, accum_out=asum_t[b, h][:, tb:tb + 1])
+
+        def norm_stats(b, h):
+            a = a_t[b, h]
             negu = ln_pool.tile([P, HQ], F32, name="negu")
-            nc.scalar.mul(negu[:], asum[:], -1.0 / D)
+            nc.scalar.mul(negu[:], asum_t[b, h][:], -1.0 / D)
             ssq = ln_pool.tile([P, HQ], F32, name="ssq")
             for tb in range(HQ):
                 sq = ln_pool.tile([P, D], F32, name="sq")
@@ -281,49 +318,89 @@ def tile_ner_b_kernel(tc, table, qw, qb, kw, vw, vb, ow, ob, ln_w, ln_b, ofc_w, 
             rstd = ln_pool.tile([P, HQ], F32, name="rstd")
             nc.gpsimd.tensor_scalar(rstd[:], ssq[:], 1.0 / D, EPS, ALU.mult, ALU.add)
             nc.gpsimd.tensor_tensor(rstd[:], rstd[:], neghalf[:], ALU.pow)
+            negu_t[b, h], rstd_t[b, h] = negu, rstd
+
+        def norm_apply(b, h):
+            a, negu, rstd = a_t[b, h], negu_t[b, h], rstd_t[b, h]
             z = ln_pool.tile([P, HQ, D], F32, name="z")
             for tb in range(HQ):
                 nc.vector.tensor_scalar(z[:, tb, :], a[:, tb, :], negu[:, tb:tb + 1], rstd[:, tb:tb + 1], ALU.add, ALU.mult)
             z_t[b, h] = z
 
-        def tags(b, h):
+        def norm_flip(b, h):
             dealt_z = z_t[b, h].rearrange("t q (j i) -> t q i j", i=KB)
             y16 = y_pool.tile([P, KB, LH], BF16, name="y16")
             for i in range(KB):
-                zt = zt_ps.tile([P, LH], F32, name="zt")
+                zt = ring_s.tile([P, LH], F32, name="ring")
                 for tb in range(HQ):
                     nc.tensor.transpose(zt[:, tb * P:(tb + 1) * P], dealt_z[:, tb, i, :], ident[:])
                 nc.scalar.activation(y16[:, i, :], zt[:], ACT.Identity, bias=lnb_t[:, i:i + 1], scale=lnw_t[:, i:i + 1])
-            ps = zt_ps.tile([T, LH], F32, name="zt")
+            y_t[b, h] = y16
+
+        def tags(b, h):
+            ps = ring_s.tile([T, LH], F32, name="ring")
             for i in range(KB):
-                nc.tensor.matmul(ps[:], wf[:, i, :], y16[:, i, :], start=(i == 0), stop=(i == KB - 1))
+                nc.tensor.matmul(ps[:], wf[:, i, :], y_t[b, h][:, i, :], start=(i == 0), stop=(i == KB - 1))
             res = y_pool.tile([T, LH], F32, name="res")
             nc.scalar.activation(res[:], ps[:], ACT.Identity, bias=ofcb_t[:, 0:1])
             nc.sync.dma_start(out[:, b * L + h * LH:b * L + (h + 1) * LH], res[:])
 
-        with tc.psum_pool(name="q_ps", bufs=3) as q_ps, tc.psum_pool(name="kv_ps", bufs=3) as kv_ps:
-            keys(0)
-            for b in range(B):
-                if b + 1 < B:
-                    keys(b + 1)
-                scores(b)
-                values(b)
-                if b == 1:
+        keys_open(0)
+        for i in range(KB):
+            key_block(0, i)
+        keys_center(0)
+        keys_edge(0)
+        for b in range(B):
+            scores_open(b)
+            values_open(b)
+            others = [(value_block, b, i) for i in range(KB)]
+            if b + 1 < B:
+                keys_open(b + 1)
+                others = [(key_block, b + 1, i) for i in range(KB)] + others
+            share = len(others) // KB
+            for i in range(KB):
+                score_block(b, i)
+                for block, block_b, block_i in others[i * share:(i + 1) * share]:
+                    block(block_b, block_i)
+                if i == 0 and b >= 1:
+                    head_sums(b - 1)
+                if i == 1 and b >= 1:
+                    values_edge(b - 1)
+                if i == 1 and b + 1 < B:
+                    keys_center(b + 1)
+                if b == 2 and i == 1:
                     softmax_exp(0)
-                if b == 2:
+                if b == 2 and i == 2:
                     softmax_norm(0)
-        with tc.psum_pool(name="pb_ps", bufs=2) as pb_ps, tc.psum_pool(name="a_ps", bufs=2) as a_ps, \
-                tc.psum_pool(name="zt_ps", bufs=2) as zt_ps:
-            for b in range(B + 1):
-                if b < B:
-                    context_own(b)
-                    if b == 0:
-                        softmax_exp(1)
-                    context_next(b)
-                    if b == 0:
-                        softmax_norm(1)
-                if b >= 1:
-                    norm(b - 1, 0)
-                    norm(b - 1, 1)
-                    tags(b - 1, 0)
-                    tags(b - 1, 1)
+                if b == 3 and i == 0:
+                    softmax_flip(0)
+            scores_edge(b)
+            if b + 1 < B:
+                keys_edge(b + 1)
+        spread(0, 0, SELF)
+        spread(0, 0, FIRST)
+        head_sums(B - 1)
+        values_edge(B - 1)
+
+        def stage(step, u, *args):
+            if 0 <= u < 2 * B:
+                step(u // 2, u % 2, *args)
+
+        for u in range(2 * B + 4):
+            stage(spread, u, NEXT)
+            stage(context_self, u)
+            stage(hidden, u - 1)
+            stage(spread, u + 1, SELF)
+            stage(context_first, u)
+            stage(norm_flip, u - 3)
+            stage(spread, u + 1, FIRST)
+            stage(context_next, u)
+            stage(norm_stats, u - 1)
+            stage(tags, u - 3)
+            stage(norm_apply, u - 2)
+            if u == 0:
+                softmax_exp(1)
+            if u == 1:
+                softmax_norm(1)
+            if u == 2:
+                softmax_flip(1)

@@ -70,17 +70,22 @@ def tile_ner_b_kernel(tc, table, qw, qb, kw, vw, vb, ow, ob, ln_w, ln_b, ofc_w, 
             nc.vector.tensor_copy(lo, rest)
 
         with tc.tile_pool(name="table", bufs=1) as table_pool, tc.tile_pool(name="start", bufs=1) as start_pool:
+            wk = held.tile([P, KB, D], BF16, name="wk")
+            wq = held.tile([P, KB, D], BF16, name="wq")
+            wv = held.tile([P, KB, D], BF16, name="wv")
+
+            def load_weights(w_t, w):
+                nc.sync.dma_start(w_t[:], w.rearrange("(k p) m -> p k m", p=P))
+
             tables = []
             for cb in range(KB):
                 t = table_pool.tile([P, S], F32, name=f"table_{cb}")
                 nc.sync.dma_start(t[:], table[cb * P:(cb + 1) * P, :])
                 tables.append(t)
-
-            wk = held.tile([P, KB, D], BF16, name="wk")
-            wq = held.tile([P, KB, D], BF16, name="wq")
-            wv = held.tile([P, KB, D], BF16, name="wv")
-            for w_t, w in ((wk, kw), (wq, qw), (wv, vw)):
-                nc.sync.dma_start(w_t[:], w.rearrange("(k p) m -> p k m", p=P))
+                if cb == 0:
+                    load_weights(wk, kw)
+                    load_weights(wq, qw)
+            load_weights(wv, vw)
             wo = held.tile([P, KB, D], BF16, name="wo")
             nc.sync.dma_start(wo[:], ow.rearrange("(p i) m -> p i m", i=KB))
             wf = held.tile([P, KB, T], BF16, name="wf")

@@ -55,10 +55,15 @@ def tile_ner_b_kernel(tc, table, qw, qb, kw, vw, vb, ow, ob, ln_w, ln_b, ofc_w, 
             nc.scalar.dma_start(t[:], vec.rearrange("(p i) o -> p (i o)", i=KB))
             return t
 
+        def cut(vec, name):
+            t = held.tile([P, KB], F32, name=name)
+            nc.scalar.dma_start(t[:], vec.rearrange("(i p) o -> p (i o)", p=P))
+            return t
+
         qb_t = dealt(qb, "qb_t")
         vb_t = dealt(vb, "vb_t")
-        lnw_t = dealt(ln_w, "lnw_t")
-        lnb_t = dealt(ln_b, "lnb_t")
+        lnw_t = cut(ln_w, "lnw_t")
+        lnb_t = cut(ln_b, "lnb_t")
         ofcb_t = held.tile([P, 1], F32, name="ofcb_t")
         nc.scalar.dma_start(ofcb_t[:], ofc_b)
 
@@ -89,7 +94,7 @@ def tile_ner_b_kernel(tc, table, qw, qb, kw, vw, vb, ow, ob, ln_w, ln_b, ofc_w, 
             wo = held.tile([P, KB, D], BF16, name="wo")
             nc.sync.dma_start(wo[:], ow.rearrange("(p i) m -> p i m", i=KB))
             wf = held.tile([P, KB, T], BF16, name="wf")
-            nc.sync.dma_start(wf[:], ofc_w.rearrange("(p i) t -> p i t", i=KB))
+            nc.sync.dma_start(wf[:], ofc_w.rearrange("(i p) t -> p i t", p=P))
 
             ident = held.tile([P, P], F32, name="ident")
             make_identity(nc, ident[:])
@@ -333,12 +338,12 @@ def tile_ner_b_kernel(tc, table, qw, qb, kw, vw, vb, ow, ob, ln_w, ln_b, ofc_w, 
             z_t[b, h] = z
 
         def norm_flip(b, h):
-            dealt_z = z_t[b, h].rearrange("t q (j i) -> t q i j", i=KB)
+            z = z_t[b, h]
             y16 = y_pool.tile([P, KB, LH], BF16, name="y16")
             for i in range(KB):
                 zt = ring_s.tile([P, LH], F32, name="ring")
                 for tb in range(HQ):
-                    nc.tensor.transpose(zt[:, tb * P:(tb + 1) * P], dealt_z[:, tb, i, :], ident[:])
+                    nc.tensor.transpose(zt[:, tb * P:(tb + 1) * P], z[:, tb, i * P:(i + 1) * P], ident[:])
                 nc.scalar.activation(y16[:, i, :], zt[:], ACT.Identity, bias=lnb_t[:, i:i + 1], scale=lnw_t[:, i:i + 1])
             y_t[b, h] = y16
 

@@ -355,6 +355,17 @@ def tile_ner_b_kernel(tc, table, qw, qb, kw, vw, vb, ow, ob, ln_w, ln_b, ofc_w, 
             nc.scalar.activation(res[:], ps[:], ACT.Identity, bias=ofcb_t[:, 0:1])
             nc.sync.dma_start(out[:, b * L + h * LH:b * L + (h + 1) * LH], res[:])
 
+        def values_of_step(b):
+            late = b - 1 if b > B // 2 else b
+            return late if b != B // 2 else None
+
+        def value_blocks(b):
+            vb_seq = values_of_step(b)
+            if vb_seq is None:
+                return []
+            values_open(vb_seq)
+            return [(value_block, vb_seq, i) for i in range(KB)]
+
         keys_open(0)
         for i in range(KB):
             key_block(0, i)
@@ -362,20 +373,18 @@ def tile_ner_b_kernel(tc, table, qw, qb, kw, vw, vb, ow, ob, ln_w, ln_b, ofc_w, 
         keys_edge(0)
         for b in range(B):
             scores_open(b)
-            values_open(b)
-            others = [(value_block, b, i) for i in range(KB)]
+            others = value_blocks(b)
             if b + 1 < B:
                 keys_open(b + 1)
                 others = [(key_block, b + 1, i) for i in range(KB)] + others
-            share = len(others) // KB
             for i in range(KB):
                 score_block(b, i)
-                for block, block_b, block_i in others[i * share:(i + 1) * share]:
+                for block, block_b, block_i in others[2 * i:2 * i + 2]:
                     block(block_b, block_i)
                 if i == 0 and b >= 1:
                     head_sums(b - 1)
-                if i == 1 and b >= 1:
-                    values_edge(b - 1)
+                if i == 1 and b >= 1 and values_of_step(b - 1) is not None:
+                    values_edge(values_of_step(b - 1))
                 if i == 1 and b + 1 < B:
                     keys_center(b + 1)
                 if b == 2 and i == 1:
@@ -390,7 +399,9 @@ def tile_ner_b_kernel(tc, table, qw, qb, kw, vw, vb, ow, ob, ln_w, ln_b, ofc_w, 
         spread(0, 0, SELF)
         spread(0, 0, FIRST)
         head_sums(B - 1)
-        values_edge(B - 1)
+        values_edge(values_of_step(B - 1))
+        for block, block_b, block_i in value_blocks(B):
+            block(block_b, block_i)
 
         def stage(step, u, *args):
             if 0 <= u < 2 * B:
@@ -409,6 +420,7 @@ def tile_ner_b_kernel(tc, table, qw, qb, kw, vw, vb, ow, ob, ln_w, ln_b, ofc_w, 
             stage(tags, u - 3)
             stage(norm_apply, u - 2)
             if u == 0:
+                values_edge(values_of_step(B))
                 softmax_exp(1)
             if u == 1:
                 softmax_norm(1)

@@ -356,11 +356,9 @@ def tile_ner_b_kernel(tc, table, qw, qb, kw, vw, vb, ow, ob, ln_w, ln_b, ofc_w, 
             nc.sync.dma_start(out[:, b * L + h * LH:b * L + (h + 1) * LH], res[:])
 
         def values_of_step(b):
-            late = b - 1 if b > B // 2 else b
-            return late if b != B // 2 else None
+            return b - (B - 1) if b >= B - 1 else None
 
-        def value_blocks(b):
-            vb_seq = values_of_step(b)
+        def value_blocks(vb_seq):
             if vb_seq is None:
                 return []
             values_open(vb_seq)
@@ -373,7 +371,7 @@ def tile_ner_b_kernel(tc, table, qw, qb, kw, vw, vb, ow, ob, ln_w, ln_b, ofc_w, 
         keys_edge(0)
         for b in range(B):
             scores_open(b)
-            others = value_blocks(b)
+            others = value_blocks(values_of_step(b))
             if b + 1 < B:
                 keys_open(b + 1)
                 others = [(key_block, b + 1, i) for i in range(KB)] + others
@@ -383,8 +381,6 @@ def tile_ner_b_kernel(tc, table, qw, qb, kw, vw, vb, ow, ob, ln_w, ln_b, ofc_w, 
                     block(block_b, block_i)
                 if i == 0 and b >= 1:
                     head_sums(b - 1)
-                if i == 1 and b >= 1 and values_of_step(b - 1) is not None:
-                    values_edge(values_of_step(b - 1))
                 if i == 1 and b + 1 < B:
                     keys_center(b + 1)
                 if b == 2 and i == 1:
@@ -400,13 +396,16 @@ def tile_ner_b_kernel(tc, table, qw, qb, kw, vw, vb, ow, ob, ln_w, ln_b, ofc_w, 
         spread(0, 0, FIRST)
         head_sums(B - 1)
         values_edge(values_of_step(B - 1))
-        for block, block_b, block_i in value_blocks(B):
+        for block, block_b, block_i in value_blocks(values_of_step(B)):
             block(block_b, block_i)
 
         def stage(step, u, *args):
             if 0 <= u < 2 * B:
                 step(u // 2, u % 2, *args)
 
+        others = []
+        for b in range(values_of_step(B) + 1, B):
+            others += value_blocks(b)
         for u in range(2 * B + 4):
             stage(spread, u, NEXT)
             stage(context_self, u)
@@ -416,11 +415,14 @@ def tile_ner_b_kernel(tc, table, qw, qb, kw, vw, vb, ow, ob, ln_w, ln_b, ofc_w, 
             stage(norm_flip, u - 3)
             stage(spread, u + 1, FIRST)
             stage(context_next, u)
+            for block, block_b, block_i in others[2 * u:2 * u + 2]:
+                block(block_b, block_i)
             stage(norm_stats, u - 1)
             stage(tags, u - 3)
             stage(norm_apply, u - 2)
+            if u % 2 == 0 and u // 2 + 1 < B:
+                values_edge(u // 2 + 1)
             if u == 0:
-                values_edge(values_of_step(B))
                 softmax_exp(1)
             if u == 1:
                 softmax_norm(1)

@@ -379,15 +379,15 @@ def tile_ner_b_kernel(tc, table, qw, qb, kw, vw, vb, ow, ob, ln_w, ln_b, ofc_w, 
                 score_block(b, i)
                 for block, block_b, block_i in others[2 * i:2 * i + 2]:
                     block(block_b, block_i)
-                if i == 0 and b >= 1:
+                if i == 1 and b >= 1:
                     head_sums(b - 1)
                 if i == 1 and b + 1 < B:
                     keys_center(b + 1)
-                if b == 2 and i == 1:
-                    softmax_exp(0)
                 if b == 2 and i == 2:
+                    softmax_exp(0)
+                if b == 2 and i == 3:
                     softmax_norm(0)
-                if b == 3 and i == 0:
+                if b == 3 and i == 2:
                     softmax_flip(0)
             scores_edge(b)
             if b + 1 < B:

@@ -189,6 +189,18 @@ def tile_ner_b_kernel(tc, table, qw, qb, kw, vw, vb, ow, ob, ln_w, ln_b, ofc_w, 
             cfix[b] = small.tile([P, 1], F32, name="cfix")
             nc.vector.reduce_sum(cfix[b][:], qbk[:], axis=AX.X)
 
+        def first_keys():
+            keys_open(0)
+            k = kt[0]
+            for i in range(KB):
+                ps = project(ring_s, wk, 0, i)
+                nc.vector.tensor_scalar(k[:, i, 0:L], ps[:], 1.0, None, ALU.mult, ALU.add, accum_out=ksum[0][:, i:i + 1])
+            negmean = held.tile([P, KB], F32, name="kt_negmean0")
+            nc.vector.tensor_scalar_mul(negmean[:], ksum[0][:], -1.0 / L)
+            for i in range(KB):
+                nc.vector.tensor_scalar_add(k[:, i, 0:L], k[:, i, 0:L], negmean[:, i:i + 1])
+            keys_edge(0)
+
         def values_open(b):
             vt[b], vsum[b] = open_projection(v_pool, "vt")
 
@@ -364,11 +376,7 @@ def tile_ner_b_kernel(tc, table, qw, qb, kw, vw, vb, ow, ob, ln_w, ln_b, ofc_w, 
             values_open(vb_seq)
             return [(value_block, vb_seq, i) for i in range(KB)]
 
-        keys_open(0)
-        for i in range(KB):
-            key_block(0, i)
-        keys_center(0)
-        keys_edge(0)
+        first_keys()
         for b in range(B):
             scores_open(b)
             others = value_blocks(values_of_step(b))

@@ -45,6 +45,11 @@ def tile_ner_b_kernel(tc, table, qw, qb, kw, vw, vb, ow, ob, ln_w, ln_b, ofc_w, 
         ring_v = stack.enter_context(tc.psum_pool(name="ring_v", bufs=3))
         ring_s = stack.enter_context(tc.psum_pool(name="ring_s", bufs=3))
 
+        zeros = held.tile([P, P], F32, name="zeros")
+        nc.gpsimd.memset(zeros[:], 0.0)
+        ones16 = held.tile([P, P], BF16, name="ones16")
+        nc.scalar.activation(ones16[:], zeros[:], ACT.Exp)
+
         offsets = held.tile([P, N // 16], U16, name="offsets")
         nc.sync.dma_start(offsets[:], offs)
 
@@ -74,82 +79,18 @@ def tile_ner_b_kernel(tc, table, qw, qb, kw, vw, vb, ow, ob, ln_w, ln_b, ofc_w, 
             nc.vector.tensor_tensor(rest, rest, mid, ALU.subtract)
             nc.vector.tensor_copy(lo, rest)
 
-        with tc.tile_pool(name="table", bufs=1) as table_pool, tc.tile_pool(name="start", bufs=1) as start_pool:
-            wk = held.tile([P, KB, D], BF16, name="wk")
-            wq = held.tile([P, KB, D], BF16, name="wq")
-            wv = held.tile([P, KB, D], BF16, name="wv")
+        wk = held.tile([P, KB, D], BF16, name="wk")
+        wq = held.tile([P, KB, D], BF16, name="wq")
+        wv = held.tile([P, KB, D], BF16, name="wv")
 
-            def load_weights(w_t, w):
-                nc.sync.dma_start(w_t[:], w.rearrange("(k p) m -> p k m", p=P))
-
-            tables = []
-            for cb in range(KB):
-                t = table_pool.tile([P, S], F32, name=f"table_{cb}")
-                nc.sync.dma_start(t[:], table[cb * P:(cb + 1) * P, :])
-                tables.append(t)
-                if cb == 0:
-                    load_weights(wk, kw)
-                    load_weights(wq, qw)
-            load_weights(wv, vw)
-            wo = held.tile([P, KB, D], BF16, name="wo")
-            nc.sync.dma_start(wo[:], ow.rearrange("(p i) m -> p i m", i=KB))
-            wf = held.tile([P, KB, T], BF16, name="wf")
-            nc.sync.dma_start(wf[:], ofc_w.rearrange("(i p) t -> p i t", p=P))
-
-            ident = held.tile([P, P], F32, name="ident")
-            make_identity(nc, ident[:])
-            ident16 = held.tile([P, P], BF16, name="ident16")
-            nc.gpsimd.tensor_copy(ident16[:], ident[:])
-            headsel = held.tile([P, NH], F32, name="headsel")
-            nc.gpsimd.memset(headsel[:], 0.125)
-            nc.gpsimd.affine_select(out=headsel[:], in_=headsel[:], compare_op=ALU.is_ge, fill=0.0,
-                                    base=0, pattern=[[-HP, NH]], channel_multiplier=1)
-            nc.gpsimd.affine_select(out=headsel[:], in_=headsel[:], compare_op=ALU.is_ge, fill=0.0,
-                                    base=HP - 1, pattern=[[HP, NH]], channel_multiplier=-1)
-            sel32 = start_pool.tile([ROWS, QN, P], F32, name="sel32")
-            nc.gpsimd.memset(sel32[:], 1.0)
-            nc.gpsimd.affine_select(out=sel32[:], in_=sel32[:], compare_op=ALU.is_ge, fill=0.0,
-                                    base=0, pattern=[[-3 * NH, QN], [-3, NH], [0, HP]], channel_multiplier=1)
-            nc.gpsimd.affine_select(out=sel32[:], in_=sel32[:], compare_op=ALU.is_ge, fill=0.0,
-                                    base=2, pattern=[[3 * NH, QN], [3, NH], [0, HP]], channel_multiplier=-1)
-            sel16 = held.tile([ROWS, QN, P], BF16, name="sel16")
-            nc.gpsimd.tensor_copy(sel16[:], sel32[:])
-            zeros = held.tile([P, GP], F32, name="zeros")
-            nc.gpsimd.memset(zeros[:], 0.0)
-            neghalf = held.tile([P, HQ], F32, name="neghalf")
-            nc.gpsimd.memset(neghalf[:], -0.5)
-
-            ones16 = held.tile([P, P], BF16, name="ones16")
-            nc.gpsimd.memset(ones16[:], 1.0)
-            ob3 = start_pool.tile([P, D], F32, name="ob3")
-            nc.gpsimd.memset(ob3[:], 0.0)
-            for row in (0, 32, 64):
-                nc.scalar.dma_start(ob3[row:row + 1, :], ob.rearrange("m o -> o m"))
-            ob_parts = start_pool.tile([P, 3, D], BF16, name="ob_parts")
-            ob_rest = start_pool.tile([P, D], F32, name="ob_rest")
-            split3(ob3[:], ob_parts[:, 0, :], ob_parts[:, 1, :], ob_parts[:, 2, :], ob_rest[:])
-            ob16 = held.tile([P, D], BF16, name="ob16")
-            nc.vector.tensor_copy(ob16[0:32, :], ob_parts[0:32, 0, :])
-            nc.vector.tensor_copy(ob16[32:64, :], ob_parts[32:64, 1, :])
-            nc.vector.tensor_copy(ob16[64:128, :], ob_parts[64:128, 2, :])
-
-            for cb in range(KB):
-                for b in range(B):
-                    e32 = start_pool.tile([P, L], F32, name="e32", bufs=4)
-                    piece = offsets[:, b * (L // 16):(b + 1) * (L // 16)]
-                    nc.scalar.activation(e32[:], tables[cb][:].indirect(piece), ACT.Copy)
-                    nc.vector.tensor_copy(e16[cb][:, b * L:(b + 1) * L], e32[:])
-
-        ctx_pool = stack.enter_context(tc.tile_pool(name="ctx", bufs=2))
-        ln_pool = stack.enter_context(tc.tile_pool(name="ln", bufs=3))
-        y_pool = stack.enter_context(tc.tile_pool(name="y", bufs=2))
+        def contract(ps, w_t, b, i, cb):
+            cols = w_t.rearrange("p k (j i) -> p k i j", i=KB)
+            nc.tensor.matmul(ps[:], cols[:, cb, i, :], e16[cb][:, b * L:(b + 1) * L], start=(cb == 0), stop=(cb == KB - 1))
 
         def project(pool, w_t, b, i):
             ps = pool.tile([P, L], F32, name="ring")
-            cols = w_t.rearrange("p k (j i) -> p k i j", i=KB)
             for cb in range(KB):
-                nc.tensor.matmul(ps[:], cols[:, cb, i, :], e16[cb][:, b * L:(b + 1) * L],
-                                 start=(cb == 0), stop=(cb == KB - 1))
+                contract(ps, w_t, b, i, cb)
             return ps
 
         kt, cfix, vt, vneg, vends, vr, ctx16, z_t = {}, {}, {}, {}, {}, {}, {}, {}
@@ -189,17 +130,97 @@ def tile_ner_b_kernel(tc, table, qw, qb, kw, vw, vb, ow, ob, ln_w, ln_b, ofc_w, 
             cfix[b] = small.tile([P, 1], F32, name="cfix")
             nc.vector.reduce_sum(cfix[b][:], qbk[:], axis=AX.X)
 
-        def first_keys():
+        def first_keys(blocks):
             keys_open(0)
             k = kt[0]
             for i in range(KB):
-                ps = project(ring_s, wk, 0, i)
-                nc.vector.tensor_scalar(k[:, i, 0:L], ps[:], 1.0, None, ALU.mult, ALU.add, accum_out=ksum[0][:, i:i + 1])
+                nc.vector.tensor_scalar(k[:, i, 0:L], blocks[i][:], 1.0, None, ALU.mult, ALU.add, accum_out=ksum[0][:, i:i + 1])
             negmean = held.tile([P, KB], F32, name="kt_negmean0")
             nc.vector.tensor_scalar_mul(negmean[:], ksum[0][:], -1.0 / L)
             for i in range(KB):
                 nc.vector.tensor_scalar_add(k[:, i, 0:L], k[:, i, 0:L], negmean[:, i:i + 1])
             keys_edge(0)
+
+        first_k = [pool.tile([P, L], F32, name="ring") for pool in (ring_s, ring_s, ring_s, ring_v)]
+        first_q = [ring_v.tile([P, L], F32, name="ring"), ring_v.tile([P, L], F32, name="ring"),
+                   sm_ps.tile([P, L], F32, name="sm"), sm_ps.tile([P, L], F32, name="sm")]
+
+        def first_contract(cb):
+            for w_t, blocks in ((wk, first_k), (wq, first_q)):
+                for i in range(KB):
+                    contract(blocks[i], w_t, 0, i, cb)
+
+        with tc.tile_pool(name="table", bufs=1) as table_pool, tc.tile_pool(name="start", bufs=1) as start_pool:
+            def load_weights(w_t, w):
+                nc.sync.dma_start(w_t[:], w.rearrange("(k p) m -> p k m", p=P))
+
+            tables = []
+            for cb in range(KB):
+                t = table_pool.tile([P, S], F32, name=f"table_{cb}")
+                nc.sync.dma_start(t[:], table[cb * P:(cb + 1) * P, :])
+                tables.append(t)
+                if cb == 0:
+                    load_weights(wk, kw)
+                if cb == 1:
+                    load_weights(wq, qw)
+            load_weights(wv, vw)
+            wo = held.tile([P, KB, D], BF16, name="wo")
+            nc.sync.dma_start(wo[:], ow.rearrange("(p i) m -> p i m", i=KB))
+            wf = held.tile([P, KB, T], BF16, name="wf")
+            nc.sync.dma_start(wf[:], ofc_w.rearrange("(i p) t -> p i t", p=P))
+
+            ident = held.tile([P, P], F32, name="ident")
+            make_identity(nc, ident[:])
+            ident16 = held.tile([P, P], BF16, name="ident16")
+            nc.gpsimd.tensor_copy(ident16[:], ident[:])
+            headsel = held.tile([P, NH], F32, name="headsel")
+            nc.gpsimd.memset(headsel[:], 0.125)
+            nc.gpsimd.affine_select(out=headsel[:], in_=headsel[:], compare_op=ALU.is_ge, fill=0.0,
+                                    base=0, pattern=[[-HP, NH]], channel_multiplier=1)
+            nc.gpsimd.affine_select(out=headsel[:], in_=headsel[:], compare_op=ALU.is_ge, fill=0.0,
+                                    base=HP - 1, pattern=[[HP, NH]], channel_multiplier=-1)
+            sel32 = start_pool.tile([ROWS, QN, P], F32, name="sel32")
+            nc.gpsimd.memset(sel32[:], 1.0)
+            nc.gpsimd.affine_select(out=sel32[:], in_=sel32[:], compare_op=ALU.is_ge, fill=0.0,
+                                    base=0, pattern=[[-3 * NH, QN], [-3, NH], [0, HP]], channel_multiplier=1)
+            nc.gpsimd.affine_select(out=sel32[:], in_=sel32[:], compare_op=ALU.is_ge, fill=0.0,
+                                    base=2, pattern=[[3 * NH, QN], [3, NH], [0, HP]], channel_multiplier=-1)
+            sel16 = held.tile([ROWS, QN, P], BF16, name="sel16")
+            nc.gpsimd.tensor_copy(sel16[:], sel32[:])
+            neghalf = held.tile([P, HQ], F32, name="neghalf")
+            nc.gpsimd.memset(neghalf[:], -0.5)
+
+            ob3 = start_pool.tile([P, D], F32, name="ob3")
+            nc.gpsimd.memset(ob3[:], 0.0)
+            for row in (0, 32, 64):
+                nc.scalar.dma_start(ob3[row:row + 1, :], ob.rearrange("m o -> o m"))
+            ob_parts = start_pool.tile([P, 3, D], BF16, name="ob_parts")
+            ob_rest = start_pool.tile([P, D], F32, name="ob_rest")
+            split3(ob3[:], ob_parts[:, 0, :], ob_parts[:, 1, :], ob_parts[:, 2, :], ob_rest[:])
+            ob16 = held.tile([P, D], BF16, name="ob16")
+            nc.vector.tensor_copy(ob16[0:32, :], ob_parts[0:32, 0, :])
+            nc.vector.tensor_copy(ob16[32:64, :], ob_parts[32:64, 1, :])
+            nc.vector.tensor_copy(ob16[64:128, :], ob_parts[64:128, 2, :])
+
+            def look_up(cb, b):
+                e32 = start_pool.tile([P, L], F32, name="e32", bufs=4)
+                piece = offsets[:, b * (L // 16):(b + 1) * (L // 16)]
+                nc.scalar.activation(e32[:], tables[cb][:].indirect(piece), ACT.Copy)
+                rounder = nc.vector if b == 0 else nc.gpsimd
+                rounder.tensor_copy(e16[cb][:, b * L:(b + 1) * L], e32[:])
+
+            pieces = [(cb, b) for cb in range(KB) for b in range(B)]
+            pieces.remove((KB - 1, 0))
+            pieces = pieces[:-B] + [(KB - 1, 0)] + pieces[-B:]
+            for cb, b in pieces:
+                look_up(cb, b)
+                if b == 0:
+                    first_contract(cb)
+            first_keys(first_k)
+
+        ctx_pool = stack.enter_context(tc.tile_pool(name="ctx", bufs=2))
+        ln_pool = stack.enter_context(tc.tile_pool(name="ln", bufs=3))
+        y_pool = stack.enter_context(tc.tile_pool(name="y", bufs=2))
 
         def values_open(b):
             vt[b], vsum[b] = open_projection(v_pool, "vt")
@@ -226,7 +247,7 @@ def tile_ner_b_kernel(tc, table, qw, qb, kw, vw, vb, ow, ob, ln_w, ln_b, ofc_w, 
 
         def score_block(b, i):
             k, pt, tok0 = kt[b], part[b], tok0_t[b]
-            ps = project(ring_v, wq, b, i)
+            ps = first_q[i] if b == 0 else project(ring_v, wq, b, i)
             bias = qb_t[:, i:i + 1]
             nc.vector.scalar_tensor_tensor(tok0[:, i:i + 1], ps[:, 0:1], bias, k[:, i, L - 1:L], ALU.add, ALU.mult)
             prod = {}
@@ -246,7 +267,7 @@ def tile_ner_b_kernel(tc, table, qw, qb, kw, vw, vb, ow, ob, ln_w, ln_b, ofc_w, 
         def head_sums(b):
             if b % 2 == 0:
                 sc[b // 2] = sm_ps.tile([P, 4, GP], F32, name="sm")
-                nc.tensor.matmul(sc[b // 2][:, RELAY, :], ident[:], zeros[:], start=True, stop=True)
+                nc.tensor.matmul(sc[b // 2][:, RELAY, :], ident[:], zeros[:, 0:GP], start=True, stop=True)
             for kind in (NEXT, SELF, FIRST):
                 for c4 in range(QN):
                     g = (b % 2) * G + c4 * NH
@@ -376,7 +397,6 @@ def tile_ner_b_kernel(tc, table, qw, qb, kw, vw, vb, ow, ob, ln_w, ln_b, ofc_w, 
             values_open(vb_seq)
             return [(value_block, vb_seq, i) for i in range(KB)]
 
-        first_keys()
         for b in range(B):
             scores_open(b)
             others = value_blocks(values_of_step(b))

@@ -22,6 +22,7 @@ HQ = QN // 2
 LH = L // 2
 T = 128
 NH = 8
+HD = D // NH
 HP = P // NH
 G = QN * NH
 GP = 2 * G
@@ -93,7 +94,7 @@ def tile_ner_b_kernel(tc, table, qw, qb, kw, vw, vb, ow, ob, ln_w, ln_b, ofc_w, 
                 contract(ps, w_t, b, i, cb)
             return ps
 
-        kt, cfix, vt, vneg, vends, vr, ctx16, z_t = {}, {}, {}, {}, {}, {}, {}, {}
+        kt, vt, vneg, vends, vr, ctx16, z_t = {}, {}, {}, {}, {}, {}, {}
 
         def open_projection(pool, name):
             x = pool.tile([P, KB, L + 1], F32, name=name)
@@ -125,10 +126,6 @@ def tile_ner_b_kernel(tc, table, qw, qb, kw, vw, vb, ow, ob, ln_w, ln_b, ofc_w, 
         def keys_edge(b):
             k = kt[b]
             nc.vector.tensor_copy(k[:, :, L:L + 1], k[:, :, 0:1])
-            qbk = small.tile([P, KB], F32, name="qbk")
-            nc.vector.tensor_tensor(qbk[:], k[:, :, 0:1].rearrange("p i o -> p (i o)"), qb_t[:], ALU.mult)
-            cfix[b] = small.tile([P, 1], F32, name="cfix")
-            nc.vector.reduce_sum(cfix[b][:], qbk[:], axis=AX.X)
 
         def first_keys(blocks):
             keys_open(0)
@@ -141,14 +138,8 @@ def tile_ner_b_kernel(tc, table, qw, qb, kw, vw, vb, ow, ob, ln_w, ln_b, ofc_w, 
                 nc.vector.tensor_scalar_add(k[:, i, 0:L], k[:, i, 0:L], negmean[:, i:i + 1])
             keys_edge(0)
 
-        first_k = [pool.tile([P, L], F32, name="ring") for pool in (ring_s, ring_s, ring_s, ring_v)]
-        first_q = [ring_v.tile([P, L], F32, name="ring"), ring_v.tile([P, L], F32, name="ring"),
-                   sm_ps.tile([P, L], F32, name="sm"), sm_ps.tile([P, L], F32, name="sm")]
-
-        def first_contract(cb):
-            for w_t, blocks in ((wk, first_k), (wq, first_q)):
-                for i in range(KB):
-                    contract(blocks[i], w_t, 0, i, cb)
+        q_ends = held.tile([P, B, 2, KB], F32, name="q_ends")
+        qw_flip = held.tile([P, KB, D], BF16, name="qw_flip")
 
         with tc.tile_pool(name="table", bufs=1) as table_pool, tc.tile_pool(name="start", bufs=1) as start_pool:
             def load_weights(w_t, w):
@@ -174,11 +165,16 @@ def tile_ner_b_kernel(tc, table, qw, qb, kw, vw, vb, ow, ob, ln_w, ln_b, ofc_w, 
             ident16 = held.tile([P, P], BF16, name="ident16")
             nc.gpsimd.tensor_copy(ident16[:], ident[:])
             headsel = held.tile([P, NH], F32, name="headsel")
-            nc.gpsimd.memset(headsel[:], 0.125)
+            nc.gpsimd.memset(headsel[:], 1.0)
             nc.gpsimd.affine_select(out=headsel[:], in_=headsel[:], compare_op=ALU.is_ge, fill=0.0,
                                     base=0, pattern=[[-HP, NH]], channel_multiplier=1)
             nc.gpsimd.affine_select(out=headsel[:], in_=headsel[:], compare_op=ALU.is_ge, fill=0.0,
                                     base=HP - 1, pattern=[[HP, NH]], channel_multiplier=-1)
+            headsel16 = held.tile([P, NH], BF16, name="headsel16")
+            nc.gpsimd.tensor_copy(headsel16[:], headsel[:])
+            token0 = held.tile([P, P], BF16, name="token0")
+            nc.gpsimd.memset(token0[:], 0.0)
+            nc.gpsimd.memset(token0[:, 0:1], 1.0)
             sel32 = start_pool.tile([ROWS, QN, P], F32, name="sel32")
             nc.gpsimd.memset(sel32[:], 1.0)
             nc.gpsimd.affine_select(out=sel32[:], in_=sel32[:], compare_op=ALU.is_ge, fill=0.0,
@@ -201,6 +197,22 @@ def tile_ner_b_kernel(tc, table, qw, qb, kw, vw, vb, ow, ob, ln_w, ln_b, ofc_w, 
             nc.vector.tensor_copy(ob16[0:32, :], ob_parts[0:32, 0, :])
             nc.vector.tensor_copy(ob16[32:64, :], ob_parts[32:64, 1, :])
             nc.vector.tensor_copy(ob16[64:128, :], ob_parts[64:128, 2, :])
+
+            cols = wq.rearrange("p k (j i) -> p k i j", i=KB)
+            for i in range(KB):
+                flip = sm_ps.tile([P, D], BF16, name="sm")
+                for cb in range(KB):
+                    nc.tensor.transpose(flip[:, cb * P:(cb + 1) * P], cols[:, cb, i, :], ident16[:])
+                nc.vector.tensor_copy(qw_flip[:, i, :], flip[:])
+
+            first_k = [pool.tile([P, L], F32, name="ring") for pool in (ring_s, ring_s, ring_s, ring_v)]
+            first_q = [ring_v.tile([P, L], F32, name="ring"), ring_v.tile([P, L], F32, name="ring"),
+                       sm_ps.tile([P, L], F32, name="sm"), sm_ps.tile([P, L], F32, name="sm")]
+
+            def first_contract(cb):
+                for w_t, blocks in ((wk, first_k), (wq, first_q)):
+                    for i in range(KB):
+                        contract(blocks[i], w_t, 0, i, cb)
 
             def look_up(cb, b):
                 e32 = start_pool.tile([P, L], F32, name="e32", bufs=4)
@@ -239,49 +251,121 @@ def tile_ner_b_kernel(tc, table, qw, qb, kw, vw, vb, ow, ob, ln_w, ln_b, ofc_w, 
             nc.vector.tensor_tensor(relay[:], vb_t[:], negmean[:], ALU.subtract)
             vneg[b], vends[b], vr[b] = negmean, ends, relay
 
-        sc, pr_t, three_t, part, tok0_t = {}, {}, {}, {}, {}
+        sc, first_parts, pr_t, three_t, part, pair_keys = {}, {}, {}, {}, {}, {}
 
         def scores_open(b):
-            part[b] = part_pool.tile([P, 3, L], F32, name="part")
-            tok0_t[b] = small.tile([P, KB], F32, name="tok0")
+            part[b] = part_pool.tile([P, 2, L], F32, name="part")
 
         def score_block(b, i):
-            k, pt, tok0 = kt[b], part[b], tok0_t[b]
+            k, pt = kt[b], part[b]
             ps = first_q[i] if b == 0 else project(ring_v, wq, b, i)
-            bias = qb_t[:, i:i + 1]
-            nc.vector.scalar_tensor_tensor(tok0[:, i:i + 1], ps[:, 0:1], bias, k[:, i, L - 1:L], ALU.add, ALU.mult)
-            prod = {}
+            prod = pt if i == 0 else prod_pool.tile([P, 2, L], F32, name="prod")
             for kind, shift in ((SELF, 0), (NEXT, 1)):
-                prod[kind] = pt[:, kind, :] if i == 0 else prod_pool.tile([P, L], F32, name=f"prod{kind}")[:]
-                nc.vector.scalar_tensor_tensor(prod[kind], ps[:], bias, k[:, i, shift:shift + L], ALU.add, ALU.mult)
-            if i == 0:
-                nc.vector.tensor_scalar(pt[:, FIRST, 1:L], ps[:, 1:L], k[:, i, 0:1], cfix[b][:], ALU.mult, ALU.add)
-            else:
-                nc.vector.scalar_tensor_tensor(pt[:, FIRST, 1:L], ps[:, 1:L], k[:, i, 0:1], pt[:, FIRST, 1:L], ALU.mult, ALU.add)
-                for kind in (SELF, NEXT):
-                    nc.vector.tensor_tensor(pt[:, kind, :], pt[:, kind, :], prod[kind], ALU.add)
+                nc.vector.scalar_tensor_tensor(prod[:, kind, :], ps[:], qb_t[:, i:i + 1], k[:, i, shift:shift + L], ALU.add, ALU.mult)
+            if i > 0:
+                nc.vector.tensor_tensor(pt[:], pt[:], prod[:], ALU.add)
 
-        def scores_edge(b):
-            nc.vector.reduce_sum(part[b][:, FIRST, 0:1], tok0_t[b][:], axis=AX.X)
+        products = {}
+
+        def products_flip(b):
+            for kind in (NEXT, SELF):
+                ps = sm_ps.tile([P, QN, P], F32, name="sm")
+                for c4 in range(QN):
+                    nc.tensor.transpose(ps[:, c4, :], part[b][:, kind, c4 * P:(c4 + 1) * P], ident[:])
+                products[b, kind] = ps
 
         def head_sums(b):
             if b % 2 == 0:
-                sc[b // 2] = sm_ps.tile([P, 4, GP], F32, name="sm")
-                nc.tensor.matmul(sc[b // 2][:, RELAY, :], ident[:], zeros[:, 0:GP], start=True, stop=True)
-            for kind in (NEXT, SELF, FIRST):
-                for c4 in range(QN):
-                    g = (b % 2) * G + c4 * NH
-                    nc.tensor.matmul(sc[b // 2][:, kind, g:g + NH], part[b][:, kind, c4 * P:(c4 + 1) * P], headsel[:],
-                                     start=True, stop=True)
+                sc[b // 2] = small.tile([P, 2, GP], F32, name="sc")
+            for kind in (NEXT, SELF):
+                nc.vector.tensor_reduce(sc[b // 2][:, kind, (b % 2) * G:(b % 2 + 1) * G],
+                                        products[b, kind].rearrange("t c (h r) -> t (c h) r", r=HP), axis=AX.X, op=ALU.add)
+
+        FK, DK = 0, 1
+
+        def first_queries():
+            ps = sm_ps.tile([P, KB, B], F32, name="sm")
+            cols = wq.rearrange("p k (j i) -> p k i j", i=KB)
+            for i in range(KB):
+                for cb in range(KB):
+                    nc.tensor.matmul(ps[:, i, :], cols[:, cb, i, :], e16[cb][:, 0:N:L], start=(cb == 0), stop=(cb == KB - 1))
+            nc.vector.tensor_tensor(q_ends[:, :, DK, :], ps.rearrange("p i b -> p b i"), qb_t[:].unsqueeze(1).to_broadcast([P, B, KB]), ALU.add)
+            nc.vector.tensor_copy(q_ends[:, :, FK, :], qb_t[:].unsqueeze(1).to_broadcast([P, B, KB]))
+
+        def split3_small(src, parts, rest):
+            nc.gpsimd.tensor_copy(parts[0], src)
+            nc.gpsimd.tensor_tensor(rest, src, parts[0], ALU.subtract)
+            nc.gpsimd.tensor_copy(parts[1], rest)
+            nc.gpsimd.tensor_tensor(rest, rest, parts[1], ALU.subtract)
+            nc.gpsimd.tensor_copy(parts[2], rest)
+
+        def pair_key(b):
+            if b % 2 == 0:
+                pair_keys[b // 2] = small.tile([P, 2, 2, KB], F32, name="pair_key")
+            k, ends = kt[b], pair_keys[b // 2]
+            first, last = (k[:, :, t:t + 1].rearrange("p i o -> p (i o)") for t in (0, L - 1))
+            nc.gpsimd.tensor_copy(ends[:, b % 2, FK, :], first)
+            nc.gpsimd.tensor_tensor(ends[:, b % 2, DK, :], last, first, ALU.subtract)
+
+        w_ps, w_parts = {}, {}
+
+        def first_weights(half):
+            ends = pair_keys[half]
+            parts = small.tile([P, KB, 2, 3], BF16, name="key_parts")
+            rest = small.tile([P, KB, 2], F32, name="key_rest")
+            split3_small(ends[:, :, FK, :].rearrange("p b i -> p i b"), [parts[:, :, :, j] for j in range(3)], rest[:])
+            by_head = small.tile([P, KB, 2, 3 * NH], BF16, name="by_head")
+            nc.gpsimd.tensor_tensor(by_head.rearrange("p i b (j h) -> p (i b j) h", h=NH),
+                                    parts.rearrange("p i b j -> p (i b j)").unsqueeze(2).to_broadcast([P, KB * 6, NH]),
+                                    headsel16[:].unsqueeze(1).to_broadcast([P, KB * 6, NH]), ALU.mult)
+            ps = sm_ps.tile([P, 2, KB, 3 * NH], F32, name="sm")
+            for cb in range(KB):
+                for i in range(KB):
+                    nc.tensor.matmul(ps[:, :, cb, :], qw_flip[:, i, cb * P:(cb + 1) * P], by_head[:, i, :, :],
+                                     start=(i == 0), stop=(i == KB - 1))
+            w_ps[half] = ps
+            prods = small.tile([P, 4, KB], F32, name="key_prods")
+            nc.gpsimd.tensor_tensor(prods[:], ends.rearrange("p b s i -> p (b s) i"),
+                                    q_ends[:, 2 * half:2 * half + 2, :, :].rearrange("p b s i -> p (b s) i"), ALU.mult)
+            sums = small.tile([P, 4, 2], F32, name="key_sums")
+            nc.gpsimd.tensor_tensor(sums[:], prods[:, :, 0:2], prods[:, :, 2:4], ALU.add)
+            nc.gpsimd.tensor_tensor(sums[:, :, 0:1], sums[:, :, 0:1], sums[:, :, 1:2], ALU.add)
+            w32 = small.tile([P, 12, NH], F32, name="w32")
+            nc.gpsimd.tensor_tensor(w32[:, 8:12, :], sums[:, :, 0:1].to_broadcast([P, 4, NH]),
+                                    headsel[:].unsqueeze(1).to_broadcast([P, 4, NH]), ALU.mult)
+            nc.vector.tensor_reduce(w32[:, 0:8, :], ps.rearrange("p b c (j h) -> p (b c) h j", h=NH), axis=AX.X, op=ALU.add)
+            w_rest = small.tile([P, 12, NH], F32, name="w_rest")
+            w_parts[half] = small.tile([P, 3, 12, NH], BF16, name="w_parts")
+            split3_small(w32[:], [w_parts[half][:, j, :, :] for j in range(3)], w_rest[:])
+
+        def first_scores(b):
+            half, b2 = b // 2, b % 2
+            if b2 == 0:
+                first_parts[half] = sm_ps.tile([P, 3, GP], F32, name="sm")
+            w3 = w_parts[half]
+            for c4 in range(QN):
+                g = b2 * G + c4 * NH
+                dst = first_parts[half][:, :, g:g + NH]
+                for cb in range(KB):
+                    nc.tensor.matmul(dst, e16[cb][:, b * L + c4 * P:b * L + (c4 + 1) * P], w3[:, :, b2 * KB + cb, :],
+                                     start=(cb == 0), stop=False)
+                nc.tensor.matmul(dst, ones16[:], w3[:, :, 8 + 2 * b2 + FK, :], start=False, stop=(c4 > 0))
+                if c4 == 0:
+                    nc.tensor.matmul(dst, token0[:], w3[:, :, 8 + 2 * b2 + DK, :], start=False, stop=True)
 
         probs = held.tile([ROWS, B, 3, P], BF16, name="probs")
 
         def softmax_exp(half):
-            top = small.tile([P, GP], F32, name="top")
-            nc.vector.tensor_reduce(top[:], sc[half].rearrange("t k g -> t g k"), axis=AX.X, op=ALU.max)
+            sums = sc[half]
             pr = small.tile([P, 4, GP], F32, name="pr")
-            nc.vector.tensor_tensor(pr[:], sc[half][:], top[:].unsqueeze(1).to_broadcast([P, 4, GP]), ALU.subtract)
-            nc.scalar.activation(pr[:], pr[:], ACT.Exp)
+            nc.vector.tensor_reduce(pr[:, FIRST, :], first_parts[half].rearrange("t j g -> t g j"), axis=AX.X, op=ALU.add)
+            top = small.tile([P, GP], F32, name="top")
+            nc.vector.tensor_tensor(top[:], sums[:, NEXT, :], pr[:, FIRST, :], ALU.max)
+            nc.vector.scalar_tensor_tensor(top[:], sums[:, SELF, :], 0.0, top[:], ALU.max, ALU.max)
+            nc.vector.tensor_tensor(pr[:, NEXT:FIRST, :], sums[:], top[:].unsqueeze(1).to_broadcast([P, 2, GP]), ALU.subtract)
+            nc.vector.tensor_tensor(pr[:, FIRST, :], pr[:, FIRST, :], top[:], ALU.subtract)
+            nc.vector.tensor_scalar_mul(pr[:, RELAY, :], top[:], -1.0)
+            nc.scalar.activation(pr[:], pr[:], ACT.Exp, scale=HD ** -0.5)
             pr_t[half] = pr
 
         def softmax_norm(half):
@@ -397,6 +481,7 @@ def tile_ner_b_kernel(tc, table, qw, qb, kw, vw, vb, ow, ob, ln_w, ln_b, ofc_w, 
             values_open(vb_seq)
             return [(value_block, vb_seq, i) for i in range(KB)]
 
+        pair_key(0)
         for b in range(B):
             scores_open(b)
             others = value_blocks(values_of_step(b))
@@ -407,21 +492,33 @@ def tile_ner_b_kernel(tc, table, qw, qb, kw, vw, vb, ow, ob, ln_w, ln_b, ofc_w, 
                 score_block(b, i)
                 for block, block_b, block_i in others[2 * i:2 * i + 2]:
                     block(block_b, block_i)
+                if b == 1 and i == 0:
+                    first_queries()
+                if b % 2 == 1 and i == 0:
+                    first_weights(b // 2)
                 if i == 1 and b >= 1:
+                    products_flip(b - 1)
+                if i == 2 and b >= 1:
                     head_sums(b - 1)
                 if i == 1 and b + 1 < B:
                     keys_center(b + 1)
                 if b == 2 and i == 2:
-                    softmax_exp(0)
+                    first_scores(0)
+                    first_scores(1)
                 if b == 2 and i == 3:
+                    softmax_exp(0)
+                if b == 3 and i == 0:
                     softmax_norm(0)
                 if b == 3 and i == 2:
                     softmax_flip(0)
-            scores_edge(b)
             if b + 1 < B:
                 keys_edge(b + 1)
+                pair_key(b + 1)
         spread(0, 0, SELF)
         spread(0, 0, FIRST)
+        products_flip(B - 1)
+        first_scores(B - 2)
+        first_scores(B - 1)
         head_sums(B - 1)
         values_edge(values_of_step(B - 1))
         for block, block_b, block_i in value_blocks(values_of_step(B)):

@@ -88,10 +88,12 @@ def tile_ner_b_kernel(tc, table, qw, qb, kw, vw, vb, ow, ob, ln_w, ln_b, ofc_w, 
             cols = w_t.rearrange("p k (j i) -> p k i j", i=KB)
             nc.tensor.matmul(ps[:], cols[:, cb, i, :], e16[cb][:, b * L:(b + 1) * L], start=(cb == 0), stop=(cb == KB - 1))
 
-        def project(pool, w_t, b, i):
+        def project(pool, w_t, b, i, turns=()):
             ps = pool.tile([P, L], F32, name="ring")
             for cb in range(KB):
                 contract(ps, w_t, b, i, cb)
+                if turns:
+                    turns[cb]()
             return ps
 
         kt, vt, vneg, vends, vr, ctx16, z_t = {}, {}, {}, {}, {}, {}, {}
@@ -101,8 +103,8 @@ def tile_ner_b_kernel(tc, table, qw, qb, kw, vw, vb, ow, ob, ln_w, ln_b, ofc_w, 
             xsum = small.tile([P, KB], F32, name=name + "_sum")
             return x, xsum
 
-        def project_block(w_t, b, i, x, xsum):
-            ps = project(ring_s, w_t, b, i)
+        def project_block(w_t, b, i, x, xsum, turns):
+            ps = project(ring_s, w_t, b, i, turns)
             nc.scalar.activation(x[:, i, 0:L], ps[:], ACT.Copy, accum_out=xsum[:, i:i + 1])
 
         def minus_mean(xsum, name):
@@ -115,8 +117,8 @@ def tile_ner_b_kernel(tc, table, qw, qb, kw, vw, vb, ow, ob, ln_w, ln_b, ofc_w, 
         def keys_open(b):
             kt[b], ksum[b] = open_projection(k_pool, "kt")
 
-        def key_block(b, i):
-            project_block(wk, b, i, kt[b], ksum[b])
+        def key_block(b, i, turns=()):
+            project_block(wk, b, i, kt[b], ksum[b], turns)
 
         def keys_center(b):
             negmean = minus_mean(ksum[b], f"kt_negmean{b}")
@@ -237,8 +239,8 @@ def tile_ner_b_kernel(tc, table, qw, qb, kw, vw, vb, ow, ob, ln_w, ln_b, ofc_w, 
         def values_open(b):
             vt[b], vsum[b] = open_projection(v_pool, "vt")
 
-        def value_block(b, i):
-            project_block(wv, b, i, vt[b], vsum[b])
+        def value_block(b, i, turns=()):
+            project_block(wv, b, i, vt[b], vsum[b], turns)
 
         def values_edge(b):
             v = vt[b]
@@ -267,12 +269,14 @@ def tile_ner_b_kernel(tc, table, qw, qb, kw, vw, vb, ow, ob, ln_w, ln_b, ofc_w, 
 
         products = {}
 
-        def products_flip(b):
-            for kind in (NEXT, SELF):
-                ps = sm_ps.tile([P, QN, P], F32, name="sm")
-                for c4 in range(QN):
-                    nc.tensor.transpose(ps[:, c4, :], part[b][:, kind, c4 * P:(c4 + 1) * P], ident[:])
-                products[b, kind] = ps
+        def products_turns(b, kind):
+            def turn(c4):
+                def go():
+                    if c4 == 0:
+                        products[b, kind] = sm_ps.tile([P, QN, P], F32, name="sm")
+                    nc.tensor.transpose(products[b, kind][:, c4, :], part[b][:, kind, c4 * P:(c4 + 1) * P], ident[:])
+                return go
+            return [turn(c4) for c4 in range(QN)]
 
         def head_sums(b):
             if b % 2 == 0:
@@ -424,13 +428,15 @@ def tile_ner_b_kernel(tc, table, qw, qb, kw, vw, vb, ow, ob, ln_w, ln_b, ofc_w, 
                     nc.vector.scalar_tensor_tensor(ctx16[b, h][:, i - 1, :], nxt[:, i - 1, :], vr[b][:, i - 1:i], own[:, i - 1, :],
                                                    ALU.add, ALU.add)
 
-        def hidden(b, h):
+        def hidden(b, h, turns=()):
             a_t[b, h] = ln_pool.tile([P, HQ, D], F32, name="a")
             asum_t[b, h] = ln_pool.tile([P, HQ], F32, name="asum")
             for tb in range(HQ):
                 ps = ring_s.tile([P, D], F32, name="ring")
                 for i in range(KB):
                     nc.tensor.matmul(ps[:], ctx16[b, h][:, i, tb * P:(tb + 1) * P], wo[:, i, :], start=(i == 0), stop=False)
+                    if turns:
+                        turns[tb * KB + i]()
                 nc.tensor.matmul(ps[:], ones16[:], ob16[:], start=False, stop=True)
                 nc.scalar.activation(a_t[b, h][:, tb, :], ps[:], ACT.Relu, accum_out=asum_t[b, h][:, tb:tb + 1])
 
@@ -454,15 +460,22 @@ def tile_ner_b_kernel(tc, table, qw, qb, kw, vw, vb, ow, ob, ln_w, ln_b, ofc_w, 
                 nc.vector.tensor_scalar(z[:, tb, :], a[:, tb, :], negu[:, tb:tb + 1], rstd[:, tb:tb + 1], ALU.add, ALU.mult)
             z_t[b, h] = z
 
-        def norm_flip(b, h):
+        def norm_turns(b, h):
             z = z_t[b, h]
             y16 = y_pool.tile([P, KB, LH], BF16, name="y16")
-            for i in range(KB):
-                zt = ring_s.tile([P, LH], F32, name="ring")
-                for tb in range(HQ):
-                    nc.tensor.transpose(zt[:, tb * P:(tb + 1) * P], z[:, tb, i * P:(i + 1) * P], ident[:])
-                nc.scalar.activation(y16[:, i, :], zt[:], ACT.Identity, bias=lnb_t[:, i:i + 1], scale=lnw_t[:, i:i + 1])
             y_t[b, h] = y16
+            zt = {}
+
+            def turn(i, tb):
+                def go():
+                    if i % 2 == 0 and tb == 0:
+                        zt[i // 2] = ring_s.tile([P, 2, LH], F32, name="ring")
+                    nc.tensor.transpose(zt[i // 2][:, i % 2, tb * P:(tb + 1) * P], z[:, tb, i * P:(i + 1) * P], ident[:])
+                    if i % 2 == 1 and tb == HQ - 1:
+                        for j in (i - 1, i):
+                            nc.scalar.activation(y16[:, j, :], zt[i // 2][:, j % 2, :], ACT.Identity, bias=lnb_t[:, j:j + 1], scale=lnw_t[:, j:j + 1])
+                return go
+            return [turn(i, tb) for i in range(KB) for tb in range(HQ)]
 
         def tags(b, h):
             ps = ring_s.tile([T, LH], F32, name="ring")
@@ -490,14 +503,12 @@ def tile_ner_b_kernel(tc, table, qw, qb, kw, vw, vb, ow, ob, ln_w, ln_b, ofc_w, 
                 others = [(key_block, b + 1, i) for i in range(KB)] + others
             for i in range(KB):
                 score_block(b, i)
-                for block, block_b, block_i in others[2 * i:2 * i + 2]:
-                    block(block_b, block_i)
+                for (block, block_b, block_i), kind in zip(others[2 * i:2 * i + 2], (NEXT, SELF)):
+                    block(block_b, block_i, products_turns(b - 1, kind) if i == 1 and b >= 1 else ())
                 if b == 1 and i == 0:
                     first_queries()
-                if b % 2 == 1 and i == 0:
+                if b % 2 == 1 and i == 2:
                     first_weights(b // 2)
-                if i == 1 and b >= 1:
-                    products_flip(b - 1)
                 if i == 2 and b >= 1:
                     head_sums(b - 1)
                 if i == 1 and b + 1 < B:
@@ -509,20 +520,17 @@ def tile_ner_b_kernel(tc, table, qw, qb, kw, vw, vb, ow, ob, ln_w, ln_b, ofc_w, 
                     softmax_exp(0)
                 if b == 3 and i == 0:
                     softmax_norm(0)
-                if b == 3 and i == 2:
+                if b == 3 and i == 3:
                     softmax_flip(0)
             if b + 1 < B:
                 keys_edge(b + 1)
                 pair_key(b + 1)
         spread(0, 0, SELF)
         spread(0, 0, FIRST)
-        products_flip(B - 1)
-        first_scores(B - 2)
-        first_scores(B - 1)
-        head_sums(B - 1)
         values_edge(values_of_step(B - 1))
         for block, block_b, block_i in value_blocks(values_of_step(B)):
-            block(block_b, block_i)
+            block(block_b, block_i, products_turns(B - 1, (NEXT, SELF)[block_i]) if block_i < 2 else ())
+        head_sums(B - 1)
 
         def stage(step, u, *args):
             if 0 <= u < 2 * B:
@@ -534,10 +542,14 @@ def tile_ner_b_kernel(tc, table, qw, qb, kw, vw, vb, ow, ob, ln_w, ln_b, ofc_w, 
         for u in range(2 * B + 4):
             stage(spread, u, NEXT)
             stage(context_self, u)
-            stage(hidden, u - 1)
+            turns = norm_turns((u - 3) // 2, (u - 3) % 2) if 0 <= u - 3 < 2 * B else ()
+            if 0 <= u - 1 < 2 * B:
+                hidden((u - 1) // 2, (u - 1) % 2, turns)
+            else:
+                for turn in turns:
+                    turn()
             stage(spread, u + 1, SELF)
             stage(context_first, u)
-            stage(norm_flip, u - 3)
             stage(spread, u + 1, FIRST)
             stage(context_next, u)
             for block, block_b, block_i in others[2 * u:2 * u + 2]:
@@ -548,8 +560,10 @@ def tile_ner_b_kernel(tc, table, qw, qb, kw, vw, vb, ow, ob, ln_w, ln_b, ofc_w, 
             if u % 2 == 0 and u // 2 + 1 < B:
                 values_edge(u // 2 + 1)
             if u == 0:
-                softmax_exp(1)
+                first_scores(B - 2)
+                first_scores(B - 1)
             if u == 1:
+                softmax_exp(1)
                 softmax_norm(1)
             if u == 2:
                 softmax_flip(1)

@@ -120,11 +120,6 @@ def tile_ner_b_kernel(tc, table, qw, qb, kw, vw, vb, ow, ob, ln_w, ln_b, ofc_w, 
         def key_block(b, i, turns=()):
             project_block(wk, b, i, kt[b], ksum[b], turns)
 
-        def keys_center(b):
-            negmean = minus_mean(ksum[b], f"kt_negmean{b}")
-            for i in range(KB):
-                nc.scalar.activation(kt[b][:, i, 0:L], kt[b][:, i, 0:L], ACT.Identity, bias=negmean[:, i:i + 1])
-
         def keys_edge(b):
             k = kt[b]
             nc.vector.tensor_copy(k[:, :, L:L + 1], k[:, :, 0:1])
@@ -134,13 +129,9 @@ def tile_ner_b_kernel(tc, table, qw, qb, kw, vw, vb, ow, ob, ln_w, ln_b, ofc_w, 
             k = kt[0]
             for i in range(KB):
                 nc.vector.tensor_scalar(k[:, i, 0:L], blocks[i][:], 1.0, None, ALU.mult, ALU.add, accum_out=ksum[0][:, i:i + 1])
-            negmean = held.tile([P, KB], F32, name="kt_negmean0")
-            nc.vector.tensor_scalar_mul(negmean[:], ksum[0][:], -1.0 / L)
-            for i in range(KB):
-                nc.vector.tensor_scalar_add(k[:, i, 0:L], k[:, i, 0:L], negmean[:, i:i + 1])
             keys_edge(0)
 
-        q_ends = held.tile([P, B, 2, KB], F32, name="q_ends")
+        q_ends = held.tile([P, B, 3, KB], F32, name="q_ends")
         qw_flip = held.tile([P, KB, D], BF16, name="qw_flip")
 
         with tc.tile_pool(name="table", bufs=1) as table_pool, tc.tile_pool(name="start", bufs=1) as start_pool:
@@ -211,25 +202,26 @@ def tile_ner_b_kernel(tc, table, qw, qb, kw, vw, vb, ow, ob, ln_w, ln_b, ofc_w, 
             first_q = [ring_v.tile([P, L], F32, name="ring"), ring_v.tile([P, L], F32, name="ring"),
                        sm_ps.tile([P, L], F32, name="sm"), sm_ps.tile([P, L], F32, name="sm")]
 
-            def first_contract(cb):
+            def first_contract(cb, t0, t1):
                 for w_t, blocks in ((wk, first_k), (wq, first_q)):
+                    cols = w_t.rearrange("p k (j i) -> p k i j", i=KB)
                     for i in range(KB):
-                        contract(blocks[i], w_t, 0, i, cb)
+                        nc.tensor.matmul(blocks[i][:, t0:t1], cols[:, cb, i, :], e16[cb][:, t0:t1],
+                                         start=(cb == 0), stop=(cb == KB - 1 and t1 == L))
 
-            def look_up(cb, b):
+            def look_up(cb, t0, t1):
                 e32 = start_pool.tile([P, L], F32, name="e32", bufs=4)
-                piece = offsets[:, b * (L // 16):(b + 1) * (L // 16)]
-                nc.scalar.activation(e32[:], tables[cb][:].indirect(piece), ACT.Copy)
-                rounder = nc.vector if b == 0 else nc.gpsimd
-                rounder.tensor_copy(e16[cb][:, b * L:(b + 1) * L], e32[:])
+                nc.scalar.activation(e32[:, 0:t1 - t0], tables[cb][:].indirect(offsets[:, t0 // 16:t1 // 16]), ACT.Copy)
+                rounder = nc.vector if t1 <= L else nc.gpsimd
+                rounder.tensor_copy(e16[cb][:, t0:t1], e32[:, 0:t1 - t0])
 
-            pieces = [(cb, b) for cb in range(KB) for b in range(B)]
-            pieces.remove((KB - 1, 0))
-            pieces = pieces[:-B] + [(KB - 1, 0)] + pieces[-B:]
-            for cb, b in pieces:
-                look_up(cb, b)
-                if b == 0:
-                    first_contract(cb)
+            pieces = [(cb, b * L, (b + 1) * L) for cb in range(KB) for b in range(B)]
+            pieces.remove((KB - 1, 0, L))
+            pieces = pieces[:-B] + [(KB - 1, 0, LH), (KB - 1, LH, L)] + pieces[-B:]
+            for cb, t0, t1 in pieces:
+                look_up(cb, t0, t1)
+                if t1 <= L:
+                    first_contract(cb, t0, t1)
             first_keys(first_k)
 
         ctx_pool = stack.enter_context(tc.tile_pool(name="ctx", bufs=2))
@@ -285,7 +277,9 @@ def tile_ner_b_kernel(tc, table, qw, qb, kw, vw, vb, ow, ob, ln_w, ln_b, ofc_w, 
                 nc.vector.tensor_reduce(sc[b // 2][:, kind, (b % 2) * G:(b % 2 + 1) * G],
                                         products[b, kind].rearrange("t c (h r) -> t (c h) r", r=HP), axis=AX.X, op=ALU.add)
 
-        FK, DK = 0, 1
+        FK, RK, DK = 0, 1, 2
+        NK = 3
+        W_COLS = 2 * 2 * KB
 
         def first_queries():
             ps = sm_ps.tile([P, KB, B], F32, name="sm")
@@ -293,8 +287,9 @@ def tile_ner_b_kernel(tc, table, qw, qb, kw, vw, vb, ow, ob, ln_w, ln_b, ofc_w, 
             for i in range(KB):
                 for cb in range(KB):
                     nc.tensor.matmul(ps[:, i, :], cols[:, cb, i, :], e16[cb][:, 0:N:L], start=(cb == 0), stop=(cb == KB - 1))
+            for s in (FK, RK):
+                nc.vector.tensor_copy(q_ends[:, :, s, :], qb_t[:].unsqueeze(1).to_broadcast([P, B, KB]))
             nc.vector.tensor_tensor(q_ends[:, :, DK, :], ps.rearrange("p i b -> p b i"), qb_t[:].unsqueeze(1).to_broadcast([P, B, KB]), ALU.add)
-            nc.vector.tensor_copy(q_ends[:, :, FK, :], qb_t[:].unsqueeze(1).to_broadcast([P, B, KB]))
 
         def split3_small(src, parts, rest):
             nc.gpsimd.tensor_copy(parts[0], src)
@@ -305,70 +300,69 @@ def tile_ner_b_kernel(tc, table, qw, qb, kw, vw, vb, ow, ob, ln_w, ln_b, ofc_w, 
 
         def pair_key(b):
             if b % 2 == 0:
-                pair_keys[b // 2] = small.tile([P, 2, 2, KB], F32, name="pair_key")
+                pair_keys[b // 2] = small.tile([P, 2, NK, KB], F32, name="pair_key")
             k, ends = kt[b], pair_keys[b // 2]
             first, last = (k[:, :, t:t + 1].rearrange("p i o -> p (i o)") for t in (0, L - 1))
             nc.gpsimd.tensor_copy(ends[:, b % 2, FK, :], first)
+            nc.gpsimd.tensor_scalar(ends[:, b % 2, RK, :], ksum[b][:], 1.0 / L, 0.0, ALU.mult, ALU.add)
             nc.gpsimd.tensor_tensor(ends[:, b % 2, DK, :], last, first, ALU.subtract)
 
-        w_ps, w_parts = {}, {}
+        w_parts = {}
 
         def first_weights(half):
             ends = pair_keys[half]
-            parts = small.tile([P, KB, 2, 3], BF16, name="key_parts")
-            rest = small.tile([P, KB, 2], F32, name="key_rest")
-            split3_small(ends[:, :, FK, :].rearrange("p b i -> p i b"), [parts[:, :, :, j] for j in range(3)], rest[:])
-            by_head = small.tile([P, KB, 2, 3 * NH], BF16, name="by_head")
-            nc.gpsimd.tensor_tensor(by_head.rearrange("p i b (j h) -> p (i b j) h", h=NH),
-                                    parts.rearrange("p i b j -> p (i b j)").unsqueeze(2).to_broadcast([P, KB * 6, NH]),
-                                    headsel16[:].unsqueeze(1).to_broadcast([P, KB * 6, NH]), ALU.mult)
-            ps = sm_ps.tile([P, 2, KB, 3 * NH], F32, name="sm")
+            parts = small.tile([P, KB, 2, 2, 3], BF16, name="key_parts")
+            rest = small.tile([P, KB, 2, 2], F32, name="key_rest")
+            split3_small(ends[:, :, FK:DK, :].rearrange("p b s i -> p i b s"), [parts[:, :, :, :, j] for j in range(3)], rest[:])
+            by_head = small.tile([P, KB, 4, 3 * NH], BF16, name="by_head")
+            nc.gpsimd.tensor_tensor(by_head.rearrange("p i x (j h) -> p (i x j) h", h=NH),
+                                    parts.rearrange("p i b s j -> p (i b s j)").unsqueeze(2).to_broadcast([P, KB * 12, NH]),
+                                    headsel16[:].unsqueeze(1).to_broadcast([P, KB * 12, NH]), ALU.mult)
+            ps = sm_ps.tile([P, 4, KB, 3 * NH], F32, name="sm")
             for cb in range(KB):
                 for i in range(KB):
                     nc.tensor.matmul(ps[:, :, cb, :], qw_flip[:, i, cb * P:(cb + 1) * P], by_head[:, i, :, :],
                                      start=(i == 0), stop=(i == KB - 1))
-            w_ps[half] = ps
-            prods = small.tile([P, 4, KB], F32, name="key_prods")
+            prods = small.tile([P, 2 * NK, KB], F32, name="key_prods")
             nc.gpsimd.tensor_tensor(prods[:], ends.rearrange("p b s i -> p (b s) i"),
                                     q_ends[:, 2 * half:2 * half + 2, :, :].rearrange("p b s i -> p (b s) i"), ALU.mult)
-            sums = small.tile([P, 4, 2], F32, name="key_sums")
+            sums = small.tile([P, 2 * NK, 2], F32, name="key_sums")
             nc.gpsimd.tensor_tensor(sums[:], prods[:, :, 0:2], prods[:, :, 2:4], ALU.add)
             nc.gpsimd.tensor_tensor(sums[:, :, 0:1], sums[:, :, 0:1], sums[:, :, 1:2], ALU.add)
-            w32 = small.tile([P, 12, NH], F32, name="w32")
-            nc.gpsimd.tensor_tensor(w32[:, 8:12, :], sums[:, :, 0:1].to_broadcast([P, 4, NH]),
-                                    headsel[:].unsqueeze(1).to_broadcast([P, 4, NH]), ALU.mult)
-            nc.vector.tensor_reduce(w32[:, 0:8, :], ps.rearrange("p b c (j h) -> p (b c) h j", h=NH), axis=AX.X, op=ALU.add)
-            w_rest = small.tile([P, 12, NH], F32, name="w_rest")
-            w_parts[half] = small.tile([P, 3, 12, NH], BF16, name="w_parts")
+            w32 = small.tile([P, W_COLS + 2 * NK, NH], F32, name="w32")
+            nc.gpsimd.tensor_tensor(w32[:, W_COLS:W_COLS + 2 * NK, :], sums[:, :, 0:1].to_broadcast([P, 2 * NK, NH]),
+                                    headsel[:].unsqueeze(1).to_broadcast([P, 2 * NK, NH]), ALU.mult)
+            nc.vector.tensor_reduce(w32[:, 0:W_COLS, :], ps.rearrange("p x c (j h) -> p (x c) h j", h=NH), axis=AX.X, op=ALU.add)
+            w_rest = small.tile([P, W_COLS + 2 * NK, NH], F32, name="w_rest")
+            w_parts[half] = small.tile([P, 3, W_COLS + 2 * NK, NH], BF16, name="w_parts")
             split3_small(w32[:], [w_parts[half][:, j, :, :] for j in range(3)], w_rest[:])
 
         def first_scores(b):
             half, b2 = b // 2, b % 2
             if b2 == 0:
-                first_parts[half] = sm_ps.tile([P, 3, GP], F32, name="sm")
+                first_parts[half] = sm_ps.tile([P, 3, 2, GP], F32, name="sm")
             w3 = w_parts[half]
+            dst = first_parts[half][:, :, :, b2 * G:(b2 + 1) * G].rearrange("t j s (c h) -> t j s c h", c=QN)
+            for s in (FK, RK):
+                share = w3[:, :, W_COLS + NK * b2 + s, :].unsqueeze(2).to_broadcast([P, 3, QN, NH])
+                nc.tensor.matmul(dst[:, :, s, :, :], ones16[:], share, start=(s == FK), stop=False)
             for c4 in range(QN):
-                g = b2 * G + c4 * NH
-                dst = first_parts[half][:, :, g:g + NH]
                 for cb in range(KB):
-                    nc.tensor.matmul(dst, e16[cb][:, b * L + c4 * P:b * L + (c4 + 1) * P], w3[:, :, b2 * KB + cb, :],
-                                     start=(cb == 0), stop=False)
-                nc.tensor.matmul(dst, ones16[:], w3[:, :, 8 + 2 * b2 + FK, :], start=False, stop=(c4 > 0))
-                if c4 == 0:
-                    nc.tensor.matmul(dst, token0[:], w3[:, :, 8 + 2 * b2 + DK, :], start=False, stop=True)
+                    keys = w3[:, :, b2 * 2 * KB + cb:(b2 + 1) * 2 * KB:KB, :]
+                    nc.tensor.matmul(dst[:, :, :, c4, :], e16[cb][:, b * L + c4 * P:b * L + (c4 + 1) * P], keys, start=False, stop=False)
+            nc.tensor.matmul(dst[:, :, FK, 0, :], token0[:], w3[:, :, W_COLS + NK * b2 + DK, :], start=False, stop=True)
 
         probs = held.tile([ROWS, B, 3, P], BF16, name="probs")
 
         def softmax_exp(half):
             sums = sc[half]
             pr = small.tile([P, 4, GP], F32, name="pr")
-            nc.vector.tensor_reduce(pr[:, FIRST, :], first_parts[half].rearrange("t j g -> t g j"), axis=AX.X, op=ALU.add)
-            top = small.tile([P, GP], F32, name="top")
-            nc.vector.tensor_tensor(top[:], sums[:, NEXT, :], pr[:, FIRST, :], ALU.max)
-            nc.vector.scalar_tensor_tensor(top[:], sums[:, SELF, :], 0.0, top[:], ALU.max, ALU.max)
-            nc.vector.tensor_tensor(pr[:, NEXT:FIRST, :], sums[:], top[:].unsqueeze(1).to_broadcast([P, 2, GP]), ALU.subtract)
-            nc.vector.tensor_tensor(pr[:, FIRST, :], pr[:, FIRST, :], top[:], ALU.subtract)
-            nc.vector.tensor_scalar_mul(pr[:, RELAY, :], top[:], -1.0)
+            nc.vector.tensor_reduce(pr[:, FIRST:, :], first_parts[half].rearrange("t j s g -> t (s g) j"), axis=AX.X, op=ALU.add)
+            top = small.tile([P, 2, GP], F32, name="top")
+            nc.vector.tensor_tensor(top[:], sums[:], pr[:, FIRST:, :], ALU.max)
+            nc.vector.tensor_tensor(top[:, 0, :], top[:, 0, :], top[:, 1, :], ALU.max)
+            for scores, kind in ((sums[:], NEXT), (pr[:, FIRST:, :], FIRST)):
+                nc.vector.tensor_tensor(pr[:, kind:kind + 2, :], scores, top[:, 0:1, :].to_broadcast([P, 2, GP]), ALU.subtract)
             nc.scalar.activation(pr[:], pr[:], ACT.Exp, scale=HD ** -0.5)
             pr_t[half] = pr
 
@@ -393,19 +387,21 @@ def tile_ner_b_kernel(tc, table, qw, qb, kw, vw, vb, ow, ob, ln_w, ln_b, ofc_w, 
                                         three[:, kind, b2 * G:(b2 + 1) * G, :].rearrange("t g j -> t (g j)"), ident16[:])
             nc.scalar.copy(probs[:, 2 * half:2 * half + 2, :, :], flipped[:])
 
-        pb_t, own_t, a_t, asum_t, negu_t, rstd_t, y_t = {}, {}, {}, {}, {}, {}, {}
+        pb_t, own_t, a_t, asum_t, mean_t, rstd_t, y_t = {}, {}, {}, {}, {}, {}, {}
 
-        def spread(b, h, kind):
-            pb = ring_v.tile([P, LH], F32, name="ring")
+        def spread(b, h, *kinds):
+            pb = ring_v.tile([P, len(kinds), LH], F32, name="ring")
             for tb in range(HQ):
-                nc.tensor.matmul(pb[:, tb * P:(tb + 1) * P], sel16[:, h * HQ + tb, :], probs[:, b, kind, :], start=True, stop=True)
-            pb_t[b, h, kind] = pb
+                nc.tensor.matmul(pb[:, :, tb * P:(tb + 1) * P], sel16[:, h * HQ + tb, :], probs[:, b, kinds[0]:kinds[-1] + 1, :],
+                                 start=True, stop=True)
+            for k, kind in enumerate(kinds):
+                pb_t[b, h, kind] = pb[:, k, :]
 
         def context_self(b, h):
             v, neg, pb, t0 = vt[b], vneg[b], pb_t[b, h, SELF], h * LH
             own = ctx_pool.tile([P, KB, LH], F32, name="own")
             for i in range(KB):
-                nc.vector.scalar_tensor_tensor(own[:, i, :], v[:, i, t0:t0 + LH], neg[:, i:i + 1], pb[:], ALU.add, ALU.mult)
+                nc.vector.scalar_tensor_tensor(own[:, i, :], v[:, i, t0:t0 + LH], neg[:, i:i + 1], pb, ALU.add, ALU.mult)
             own_t[b, h] = own
 
         def context_first(b, h):
@@ -423,7 +419,7 @@ def tile_ner_b_kernel(tc, table, qw, qb, kw, vw, vb, ow, ob, ln_w, ln_b, ofc_w, 
             ctx16[b, h] = ctx_pool.tile([P, KB, LH], BF16, name="ctx16")
             for i in range(KB + 1):
                 if i < KB:
-                    nc.vector.scalar_tensor_tensor(nxt[:, i, :], v[:, i, t0 + 1:t0 + LH + 1], neg[:, i:i + 1], pb[:], ALU.add, ALU.mult)
+                    nc.vector.scalar_tensor_tensor(nxt[:, i, :], v[:, i, t0 + 1:t0 + LH + 1], neg[:, i:i + 1], pb, ALU.add, ALU.mult)
                 if i >= 1:
                     nc.vector.scalar_tensor_tensor(ctx16[b, h][:, i - 1, :], nxt[:, i - 1, :], vr[b][:, i - 1:i], own[:, i - 1, :],
                                                    ALU.add, ALU.add)
@@ -442,22 +438,32 @@ def tile_ner_b_kernel(tc, table, qw, qb, kw, vw, vb, ow, ob, ln_w, ln_b, ofc_w, 
 
         def norm_stats(b, h):
             a = a_t[b, h]
-            negu = ln_pool.tile([P, HQ], F32, name="negu")
-            nc.scalar.mul(negu[:], asum_t[b, h][:], -1.0 / D)
-            ssq = ln_pool.tile([P, HQ], F32, name="ssq")
-            for tb in range(HQ):
-                sq = ln_pool.tile([P, D], F32, name="sq")
-                nc.scalar.activation(sq[:], a[:, tb, :], ACT.Square, bias=negu[:, tb:tb + 1], accum_out=ssq[:, tb:tb + 1])
             rstd = ln_pool.tile([P, HQ], F32, name="rstd")
-            nc.gpsimd.tensor_scalar(rstd[:], ssq[:], 1.0 / D, EPS, ALU.mult, ALU.add)
+            if (b, h) == (B - 1, 1):
+                stats = ln_pool.tile([P, HQ, 6], F32, name="stats")
+                mv = ln_pool.tile([P, HQ, 2], F32, name="mv")
+                for tb in range(HQ):
+                    nc.vector.bn_stats(stats[:, tb, :], a[:, tb, :])
+                    nc.vector.bn_aggr(mv[:, tb, :], stats[:, tb, :])
+                mean_t[b, h] = [mv[:, tb, 0:1] for tb in range(HQ)], ALU.subtract
+                nc.gpsimd.tensor_scalar(rstd[:], mv[:, :, 1], 1.0, EPS, ALU.mult, ALU.add)
+            else:
+                negu = ln_pool.tile([P, HQ], F32, name="negu")
+                nc.scalar.mul(negu[:], asum_t[b, h][:], -1.0 / D)
+                ssq = ln_pool.tile([P, HQ], F32, name="ssq")
+                for tb in range(HQ):
+                    sq = ln_pool.tile([P, D], F32, name="sq")
+                    nc.scalar.activation(sq[:], a[:, tb, :], ACT.Square, bias=negu[:, tb:tb + 1], accum_out=ssq[:, tb:tb + 1])
+                mean_t[b, h] = [negu[:, tb:tb + 1] for tb in range(HQ)], ALU.add
+                nc.gpsimd.tensor_scalar(rstd[:], ssq[:], 1.0 / D, EPS, ALU.mult, ALU.add)
             nc.gpsimd.tensor_tensor(rstd[:], rstd[:], neghalf[:], ALU.pow)
-            negu_t[b, h], rstd_t[b, h] = negu, rstd
+            rstd_t[b, h] = rstd
 
         def norm_apply(b, h):
-            a, negu, rstd = a_t[b, h], negu_t[b, h], rstd_t[b, h]
+            a, (mean, op), rstd = a_t[b, h], mean_t[b, h], rstd_t[b, h]
             z = ln_pool.tile([P, HQ, D], F32, name="z")
             for tb in range(HQ):
-                nc.vector.tensor_scalar(z[:, tb, :], a[:, tb, :], negu[:, tb:tb + 1], rstd[:, tb:tb + 1], ALU.add, ALU.mult)
+                nc.vector.tensor_scalar(z[:, tb, :], a[:, tb, :], mean[tb], rstd[:, tb:tb + 1], op, ALU.mult)
             z_t[b, h] = z
 
         def norm_turns(b, h):
@@ -473,7 +479,11 @@ def tile_ner_b_kernel(tc, table, qw, qb, kw, vw, vb, ow, ob, ln_w, ln_b, ofc_w, 
                     nc.tensor.transpose(zt[i // 2][:, i % 2, tb * P:(tb + 1) * P], z[:, tb, i * P:(i + 1) * P], ident[:])
                     if i % 2 == 1 and tb == HQ - 1:
                         for j in (i - 1, i):
-                            nc.scalar.activation(y16[:, j, :], zt[i // 2][:, j % 2, :], ACT.Identity, bias=lnb_t[:, j:j + 1], scale=lnw_t[:, j:j + 1])
+                            y, x, weight, bias = y16[:, j, :], zt[i // 2][:, j % 2, :], lnw_t[:, j:j + 1], lnb_t[:, j:j + 1]
+                            if (b, h) == (B - 1, 1) and j % 2 == 1:
+                                nc.vector.tensor_scalar(y, x, weight, bias, ALU.mult, ALU.add)
+                            else:
+                                nc.scalar.activation(y, x, ACT.Identity, bias=bias, scale=weight)
                 return go
             return [turn(i, tb) for i in range(KB) for tb in range(HQ)]
 
@@ -511,8 +521,6 @@ def tile_ner_b_kernel(tc, table, qw, qb, kw, vw, vb, ow, ob, ln_w, ln_b, ofc_w, 
                     first_weights(b // 2)
                 if i == 2 and b >= 1:
                     head_sums(b - 1)
-                if i == 1 and b + 1 < B:
-                    keys_center(b + 1)
                 if b == 2 and i == 2:
                     first_scores(0)
                     first_scores(1)
@@ -525,8 +533,7 @@ def tile_ner_b_kernel(tc, table, qw, qb, kw, vw, vb, ow, ob, ln_w, ln_b, ofc_w, 
             if b + 1 < B:
                 keys_edge(b + 1)
                 pair_key(b + 1)
-        spread(0, 0, SELF)
-        spread(0, 0, FIRST)
+        spread(0, 0, SELF, FIRST)
         values_edge(values_of_step(B - 1))
         for block, block_b, block_i in value_blocks(values_of_step(B)):
             block(block_b, block_i, products_turns(B - 1, (NEXT, SELF)[block_i]) if block_i < 2 else ())
@@ -548,9 +555,8 @@ def tile_ner_b_kernel(tc, table, qw, qb, kw, vw, vb, ow, ob, ln_w, ln_b, ofc_w, 
             else:
                 for turn in turns:
                     turn()
-            stage(spread, u + 1, SELF)
+            stage(spread, u + 1, SELF, FIRST)
             stage(context_first, u)
-            stage(spread, u + 1, FIRST)
             stage(context_next, u)
             for block, block_b, block_i in others[2 * u:2 * u + 2]:
                 block(block_b, block_i)

@@ -176,8 +176,8 @@ def tile_ner_b_kernel(tc, table, qw, qb, kw, vw, vb, ow, ob, ln_w, ln_b, ofc_w, 
                                     base=2, pattern=[[3 * NH, QN], [3, NH], [0, HP]], channel_multiplier=-1)
             sel16 = held.tile([ROWS, QN, P], BF16, name="sel16")
             nc.gpsimd.tensor_copy(sel16[:], sel32[:])
-            neghalf = held.tile([P, HQ], F32, name="neghalf")
-            nc.gpsimd.memset(neghalf[:], -0.5)
+            eps = held.tile([P, 1], F32, name="eps")
+            nc.gpsimd.memset(eps[:], EPS)
 
             ob3 = start_pool.tile([P, D], F32, name="ob3")
             nc.gpsimd.memset(ob3[:], 0.0)
@@ -239,8 +239,9 @@ def tile_ner_b_kernel(tc, table, qw, qb, kw, vw, vb, ow, ob, ln_w, ln_b, ofc_w, 
             negmean = minus_mean(vsum[b], f"vt_negmean{b}")
             nc.vector.tensor_copy(v[:, :, L:L + 1], v[:, :, 0:1])
             ends = held.tile([P, 2, KB], F32, name=f"ends{b}")
-            nc.vector.tensor_tensor(ends[:, 0, :], v[:, :, 0:1].rearrange("p i o -> p (i o)"), negmean[:], ALU.add)
-            nc.vector.tensor_tensor(ends[:, 1, :], v[:, :, L - 1:L].rearrange("p i o -> p (i o)"), negmean[:], ALU.add)
+            first, last = (v[:, :, t:t + 1].rearrange("p i o -> p (i o)") for t in (0, L - 1))
+            nc.vector.tensor_tensor(ends[:, 0, :], first, negmean[:], ALU.add)
+            nc.vector.tensor_tensor(ends[:, 1, :], last, first, ALU.subtract)
             relay = held.tile([P, KB], F32, name=f"relay{b}")
             nc.vector.tensor_tensor(relay[:], vb_t[:], negmean[:], ALU.subtract)
             vneg[b], vends[b], vr[b] = negmean, ends, relay
@@ -387,7 +388,7 @@ def tile_ner_b_kernel(tc, table, qw, qb, kw, vw, vb, ow, ob, ln_w, ln_b, ofc_w, 
                                         three[:, kind, b2 * G:(b2 + 1) * G, :].rearrange("t g j -> t (g j)"), ident16[:])
             nc.scalar.copy(probs[:, 2 * half:2 * half + 2, :, :], flipped[:])
 
-        pb_t, own_t, a_t, asum_t, mean_t, rstd_t, y_t = {}, {}, {}, {}, {}, {}, {}
+        pb_t, own_t, a_t, asum_t, mean_t, std_t, y_t = {}, {}, {}, {}, {}, {}, {}
 
         def spread(b, h, *kinds):
             pb = ring_v.tile([P, len(kinds), LH], F32, name="ring")
@@ -406,12 +407,11 @@ def tile_ner_b_kernel(tc, table, qw, qb, kw, vw, vb, ow, ob, ln_w, ln_b, ofc_w, 
 
         def context_first(b, h):
             own, ends, pb = own_t[b, h], vends[b], pb_t[b, h, FIRST]
-            skip = 1 if h == 0 else 0
             for i in range(KB):
-                nc.vector.scalar_tensor_tensor(own[:, i, skip:LH], pb[:, skip:LH], ends[:, 0, i:i + 1], own[:, i, skip:LH],
-                                               ALU.mult, ALU.add)
-                if h == 0:
-                    nc.vector.scalar_tensor_tensor(own[:, i, 0:1], pb[:, 0:1], ends[:, 1, i:i + 1], own[:, i, 0:1], ALU.mult, ALU.add)
+                nc.vector.scalar_tensor_tensor(own[:, i, :], pb, ends[:, 0, i:i + 1], own[:, i, :], ALU.mult, ALU.add)
+            if h == 0:
+                own0 = own[:, :, 0:1].rearrange("p i o -> p (i o)")
+                nc.vector.scalar_tensor_tensor(own0, ends[:, 1, :], pb[:, 0:1], own0, ALU.mult, ALU.add)
 
         def context_next(b, h):
             v, neg, own, pb, t0 = vt[b], vneg[b], own_t[b, h], pb_t[b, h, NEXT], h * LH
@@ -438,7 +438,7 @@ def tile_ner_b_kernel(tc, table, qw, qb, kw, vw, vb, ow, ob, ln_w, ln_b, ofc_w, 
 
         def norm_stats(b, h):
             a = a_t[b, h]
-            rstd = ln_pool.tile([P, HQ], F32, name="rstd")
+            std = ln_pool.tile([P, HQ], F32, name="std")
             if (b, h) == (B - 1, 1):
                 stats = ln_pool.tile([P, HQ, 6], F32, name="stats")
                 mv = ln_pool.tile([P, HQ, 2], F32, name="mv")
@@ -446,7 +446,7 @@ def tile_ner_b_kernel(tc, table, qw, qb, kw, vw, vb, ow, ob, ln_w, ln_b, ofc_w, 
                     nc.vector.bn_stats(stats[:, tb, :], a[:, tb, :])
                     nc.vector.bn_aggr(mv[:, tb, :], stats[:, tb, :])
                 mean_t[b, h] = [mv[:, tb, 0:1] for tb in range(HQ)], ALU.subtract
-                nc.gpsimd.tensor_scalar(rstd[:], mv[:, :, 1], 1.0, EPS, ALU.mult, ALU.add)
+                nc.scalar.activation(std[:], mv[:, :, 1], ACT.Sqrt, bias=eps[:, 0:1])
             else:
                 negu = ln_pool.tile([P, HQ], F32, name="negu")
                 nc.scalar.mul(negu[:], asum_t[b, h][:], -1.0 / D)
@@ -455,12 +455,13 @@ def tile_ner_b_kernel(tc, table, qw, qb, kw, vw, vb, ow, ob, ln_w, ln_b, ofc_w, 
                     sq = ln_pool.tile([P, D], F32, name="sq")
                     nc.scalar.activation(sq[:], a[:, tb, :], ACT.Square, bias=negu[:, tb:tb + 1], accum_out=ssq[:, tb:tb + 1])
                 mean_t[b, h] = [negu[:, tb:tb + 1] for tb in range(HQ)], ALU.add
-                nc.gpsimd.tensor_scalar(rstd[:], ssq[:], 1.0 / D, EPS, ALU.mult, ALU.add)
-            nc.gpsimd.tensor_tensor(rstd[:], rstd[:], neghalf[:], ALU.pow)
-            rstd_t[b, h] = rstd
+                nc.scalar.activation(std[:], ssq[:], ACT.Sqrt, bias=eps[:, 0:1], scale=1.0 / D)
+            std_t[b, h] = std
 
         def norm_apply(b, h):
-            a, (mean, op), rstd = a_t[b, h], mean_t[b, h], rstd_t[b, h]
+            a, (mean, op) = a_t[b, h], mean_t[b, h]
+            rstd = ln_pool.tile([P, HQ], F32, name="rstd")
+            nc.vector.reciprocal(rstd[:], std_t[b, h][:])
             z = ln_pool.tile([P, HQ, D], F32, name="z")
             for tb in range(HQ):
                 nc.vector.tensor_scalar(z[:, tb, :], a[:, tb, :], mean[tb], rstd[:, tb:tb + 1], op, ALU.mult)
@@ -560,6 +561,9 @@ def tile_ner_b_kernel(tc, table, qw, qb, kw, vw, vb, ow, ob, ln_w, ln_b, ofc_w, 
             stage(context_next, u)
             for block, block_b, block_i in others[2 * u:2 * u + 2]:
                 block(block_b, block_i)
+            if u == 1:
+                softmax_exp(1)
+                softmax_norm(1)
             stage(norm_stats, u - 1)
             stage(tags, u - 3)
             stage(norm_apply, u - 2)
@@ -568,8 +572,5 @@ def tile_ner_b_kernel(tc, table, qw, qb, kw, vw, vb, ow, ob, ln_w, ln_b, ofc_w, 
             if u == 0:
                 first_scores(B - 2)
                 first_scores(B - 1)
-            if u == 1:
-                softmax_exp(1)
-                softmax_norm(1)
             if u == 2:
                 softmax_flip(1)

from contextlib import ExitStack

import concourse.mybir as mybir
from concourse.masks import make_identity

F32 = mybir.dt.float32
BF16 = mybir.dt.bfloat16
U16 = mybir.dt.uint16
ALU = mybir.AluOpType
ACT = mybir.ActivationFunctionType
AX = mybir.AxisListType

P = 128
D = 512
KB = D // P
S = 4096
N = 2048
L = 512
B = N // L
QN = L // P
HQ = QN // 2
LH = L // 2
T = 128
NH = 8
HD = D // NH
HP = P // NH
G = QN * NH
GP = 2 * G
ROWS = 3 * G
EPS = 1e-12
NEXT, SELF, FIRST, RELAY = 0, 1, 2, 3

FLOPS = 2 * N * (4 * D * D + D * T)


def tile_ner_b_kernel(tc, table, qw, qb, kw, vw, vb, ow, ob, ln_w, ln_b, ofc_w, ofc_b, offs, out):
    nc = tc.nc
    with ExitStack() as stack:
        held = stack.enter_context(tc.tile_pool(name="held", bufs=1))
        k_pool = stack.enter_context(tc.tile_pool(name="k", bufs=2))
        v_pool = stack.enter_context(tc.tile_pool(name="v", bufs=B))
        part_pool = stack.enter_context(tc.tile_pool(name="part", bufs=2))
        prod_pool = stack.enter_context(tc.tile_pool(name="prod", bufs=4))
        small = stack.enter_context(tc.tile_pool(name="small", bufs=2))
        sm_ps = stack.enter_context(tc.psum_pool(name="sm_ps", bufs=2))
        ring_v = stack.enter_context(tc.psum_pool(name="ring_v", bufs=3))
        ring_s = stack.enter_context(tc.psum_pool(name="ring_s", bufs=3))

        zeros = held.tile([P, P], F32, name="zeros")
        nc.gpsimd.memset(zeros[:], 0.0)
        ones16 = held.tile([P, P], BF16, name="ones16")
        nc.scalar.activation(ones16[:], zeros[:], ACT.Exp)

        offsets = held.tile([P, N // 16], U16, name="offsets")
        nc.sync.dma_start(offsets[:], offs)

        e16 = [held.tile([P, N], BF16, name=f"e16_{cb}") for cb in range(KB)]

        def dealt(vec, name):
            t = held.tile([P, KB], F32, name=name)
            nc.scalar.dma_start(t[:], vec.rearrange("(p i) o -> p (i o)", i=KB))
            return t

        def cut(vec, name):
            t = held.tile([P, KB], F32, name=name)
            nc.scalar.dma_start(t[:], vec.rearrange("(i p) o -> p (i o)", p=P))
            return t

        qb_t = dealt(qb, "qb_t")
        vb_t = dealt(vb, "vb_t")
        lnw_t = cut(ln_w, "lnw_t")
        lnb_t = cut(ln_b, "lnb_t")
        ofcb_t = held.tile([P, 1], F32, name="ofcb_t")
        nc.scalar.dma_start(ofcb_t[:], ofc_b)

        def split3(src, hi, mid, lo, rest):
            nc.vector.tensor_copy(hi, src)
            nc.vector.tensor_tensor(rest, src, hi, ALU.subtract)
            nc.vector.tensor_copy(mid, rest)
            nc.vector.tensor_tensor(rest, rest, mid, ALU.subtract)
            nc.vector.tensor_copy(lo, rest)

        wk = held.tile([P, KB, D], BF16, name="wk")
        wq = held.tile([P, KB, D], BF16, name="wq")
        wv = held.tile([P, KB, D], BF16, name="wv")

        def contract(ps, w_t, b, i, cb):
            cols = w_t.rearrange("p k (j i) -> p k i j", i=KB)
            nc.tensor.matmul(ps[:], cols[:, cb, i, :], e16[cb][:, b * L:(b + 1) * L], start=(cb == 0), stop=(cb == KB - 1))

        def project(pool, w_t, b, i, turns=()):
            ps = pool.tile([P, L], F32, name="ring")
            for cb in range(KB):
                contract(ps, w_t, b, i, cb)
                if turns:
                    turns[cb]()
            return ps

        kt, vt, vneg, vends, vr, ctx16, z_t = {}, {}, {}, {}, {}, {}, {}

        def open_projection(pool, name):
            x = pool.tile([P, KB, L + 1], F32, name=name)
            xsum = small.tile([P, KB], F32, name=name + "_sum")
            return x, xsum

        def project_block(w_t, b, i, x, xsum, turns):
            ps = project(ring_s, w_t, b, i, turns)
            nc.scalar.activation(x[:, i, 0:L], ps[:], ACT.Copy, accum_out=xsum[:, i:i + 1])

        def minus_mean(xsum, name):
            negmean = held.tile([P, KB], F32, name=name)
            nc.scalar.mul(negmean[:], xsum[:], -1.0 / L)
            return negmean

        ksum, vsum = {}, {}

        def keys_open(b):
            kt[b], ksum[b] = open_projection(k_pool, "kt")

        def key_block(b, i, turns=()):
            project_block(wk, b, i, kt[b], ksum[b], turns)

        def keys_edge(b):
            k = kt[b]
            nc.vector.tensor_copy(k[:, :, L:L + 1], k[:, :, 0:1])

        def first_keys(blocks):
            keys_open(0)
            k = kt[0]
            for i in range(KB):
                nc.vector.tensor_scalar(k[:, i, 0:L], blocks[i][:], 1.0, None, ALU.mult, ALU.add, accum_out=ksum[0][:, i:i + 1])
            keys_edge(0)

        q_ends = held.tile([P, B, 3, KB], F32, name="q_ends")
        qw_flip = held.tile([P, KB, D], BF16, name="qw_flip")

        with tc.tile_pool(name="table", bufs=1) as table_pool, tc.tile_pool(name="start", bufs=1) as start_pool:
            def load_weights(w_t, w):
                nc.sync.dma_start(w_t[:], w.rearrange("(k p) m -> p k m", p=P))

            tables = []
            for cb in range(KB):
                t = table_pool.tile([P, S], F32, name=f"table_{cb}")
                nc.sync.dma_start(t[:], table[cb * P:(cb + 1) * P, :])
                tables.append(t)
                if cb == 0:
                    load_weights(wk, kw)
                if cb == 1:
                    load_weights(wq, qw)
            load_weights(wv, vw)
            wo = held.tile([P, KB, D], BF16, name="wo")
            nc.sync.dma_start(wo[:], ow.rearrange("(p i) m -> p i m", i=KB))
            wf = held.tile([P, KB, T], BF16, name="wf")
            nc.sync.dma_start(wf[:], ofc_w.rearrange("(i p) t -> p i t", p=P))

            ident = held.tile([P, P], F32, name="ident")
            make_identity(nc, ident[:])
            ident16 = held.tile([P, P], BF16, name="ident16")
            nc.gpsimd.tensor_copy(ident16[:], ident[:])
            headsel = held.tile([P, NH], F32, name="headsel")
            nc.gpsimd.memset(headsel[:], 1.0)
            nc.gpsimd.affine_select(out=headsel[:], in_=headsel[:], compare_op=ALU.is_ge, fill=0.0,
                                    base=0, pattern=[[-HP, NH]], channel_multiplier=1)
            nc.gpsimd.affine_select(out=headsel[:], in_=headsel[:], compare_op=ALU.is_ge, fill=0.0,
                                    base=HP - 1, pattern=[[HP, NH]], channel_multiplier=-1)
            headsel16 = held.tile([P, NH], BF16, name="headsel16")
            nc.gpsimd.tensor_copy(headsel16[:], headsel[:])
            token0 = held.tile([P, P], BF16, name="token0")
            nc.gpsimd.memset(token0[:], 0.0)
            nc.gpsimd.memset(token0[:, 0:1], 1.0)
            sel32 = start_pool.tile([ROWS, QN, P], F32, name="sel32")
            nc.gpsimd.memset(sel32[:], 1.0)
            nc.gpsimd.affine_select(out=sel32[:], in_=sel32[:], compare_op=ALU.is_ge, fill=0.0,
                                    base=0, pattern=[[-3 * NH, QN], [-3, NH], [0, HP]], channel_multiplier=1)
            nc.gpsimd.affine_select(out=sel32[:], in_=sel32[:], compare_op=ALU.is_ge, fill=0.0,
                                    base=2, pattern=[[3 * NH, QN], [3, NH], [0, HP]], channel_multiplier=-1)
            sel16 = held.tile([ROWS, QN, P], BF16, name="sel16")
            nc.gpsimd.tensor_copy(sel16[:], sel32[:])
            eps = held.tile([P, 1], F32, name="eps")
            nc.gpsimd.memset(eps[:], EPS)

            ob3 = start_pool.tile([P, D], F32, name="ob3")
            nc.gpsimd.memset(ob3[:], 0.0)
            for row in (0, 32, 64):
                nc.scalar.dma_start(ob3[row:row + 1, :], ob.rearrange("m o -> o m"))
            ob_parts = start_pool.tile([P, 3, D], BF16, name="ob_parts")
            ob_rest = start_pool.tile([P, D], F32, name="ob_rest")
            split3(ob3[:], ob_parts[:, 0, :], ob_parts[:, 1, :], ob_parts[:, 2, :], ob_rest[:])
            ob16 = held.tile([P, D], BF16, name="ob16")
            nc.vector.tensor_copy(ob16[0:32, :], ob_parts[0:32, 0, :])
            nc.vector.tensor_copy(ob16[32:64, :], ob_parts[32:64, 1, :])
            nc.vector.tensor_copy(ob16[64:128, :], ob_parts[64:128, 2, :])

            cols = wq.rearrange("p k (j i) -> p k i j", i=KB)
            for i in range(KB):
                flip = sm_ps.tile([P, D], BF16, name="sm")
                for cb in range(KB):
                    nc.tensor.transpose(flip[:, cb * P:(cb + 1) * P], cols[:, cb, i, :], ident16[:])
                nc.vector.tensor_copy(qw_flip[:, i, :], flip[:])

            first_k = [pool.tile([P, L], F32, name="ring") for pool in (ring_s, ring_s, ring_s, ring_v)]
            first_q = [ring_v.tile([P, L], F32, name="ring"), ring_v.tile([P, L], F32, name="ring"),
                       sm_ps.tile([P, L], F32, name="sm"), sm_ps.tile([P, L], F32, name="sm")]

            def first_contract(cb, t0, t1):
                for w_t, blocks in ((wk, first_k), (wq, first_q)):
                    cols = w_t.rearrange("p k (j i) -> p k i j", i=KB)
                    for i in range(KB):
                        nc.tensor.matmul(blocks[i][:, t0:t1], cols[:, cb, i, :], e16[cb][:, t0:t1],
                                         start=(cb == 0), stop=(cb == KB - 1 and t1 == L))

            def look_up(cb, t0, t1):
                e32 = start_pool.tile([P, L], F32, name="e32", bufs=4)
                nc.scalar.activation(e32[:, 0:t1 - t0], tables[cb][:].indirect(offsets[:, t0 // 16:t1 // 16]), ACT.Copy)
                rounder = nc.vector if t1 <= L else nc.gpsimd
                rounder.tensor_copy(e16[cb][:, t0:t1], e32[:, 0:t1 - t0])

            pieces = [(cb, b * L, (b + 1) * L) for cb in range(KB) for b in range(B)]
            pieces.remove((KB - 1, 0, L))
            pieces = pieces[:-B] + [(KB - 1, 0, LH), (KB - 1, LH, L)] + pieces[-B:]
            for cb, t0, t1 in pieces:
                look_up(cb, t0, t1)
                if t1 <= L:
                    first_contract(cb, t0, t1)
            first_keys(first_k)

        ctx_pool = stack.enter_context(tc.tile_pool(name="ctx", bufs=2))
        ln_pool = stack.enter_context(tc.tile_pool(name="ln", bufs=3))
        y_pool = stack.enter_context(tc.tile_pool(name="y", bufs=2))

        def values_open(b):
            vt[b], vsum[b] = open_projection(v_pool, "vt")

        def value_block(b, i, turns=()):
            project_block(wv, b, i, vt[b], vsum[b], turns)

        def values_edge(b):
            v = vt[b]
            negmean = minus_mean(vsum[b], f"vt_negmean{b}")
            nc.vector.tensor_copy(v[:, :, L:L + 1], v[:, :, 0:1])
            ends = held.tile([P, 2, KB], F32, name=f"ends{b}")
            first, last = (v[:, :, t:t + 1].rearrange("p i o -> p (i o)") for t in (0, L - 1))
            nc.vector.tensor_tensor(ends[:, 0, :], first, negmean[:], ALU.add)
            nc.vector.tensor_tensor(ends[:, 1, :], last, first, ALU.subtract)
            relay = held.tile([P, KB], F32, name=f"relay{b}")
            nc.vector.tensor_tensor(relay[:], vb_t[:], negmean[:], ALU.subtract)
            vneg[b], vends[b], vr[b] = negmean, ends, relay

        sc, first_parts, pr_t, three_t, part, pair_keys = {}, {}, {}, {}, {}, {}

        def scores_open(b):
            part[b] = part_pool.tile([P, 2, L], F32, name="part")

        def score_block(b, i):
            k, pt = kt[b], part[b]
            ps = first_q[i] if b == 0 else project(ring_v, wq, b, i)
            prod = pt if i == 0 else prod_pool.tile([P, 2, L], F32, name="prod")
            for kind, shift in ((SELF, 0), (NEXT, 1)):
                nc.vector.scalar_tensor_tensor(prod[:, kind, :], ps[:], qb_t[:, i:i + 1], k[:, i, shift:shift + L], ALU.add, ALU.mult)
            if i > 0:
                nc.vector.tensor_tensor(pt[:], pt[:], prod[:], ALU.add)

        products = {}

        def products_turns(b, kind):
            def turn(c4):
                def go():
                    if c4 == 0:
                        products[b, kind] = sm_ps.tile([P, QN, P], F32, name="sm")
                    nc.tensor.transpose(products[b, kind][:, c4, :], part[b][:, kind, c4 * P:(c4 + 1) * P], ident[:])
                return go
            return [turn(c4) for c4 in range(QN)]

        def head_sums(b):
            if b % 2 == 0:
                sc[b // 2] = small.tile([P, 2, GP], F32, name="sc")
            for kind in (NEXT, SELF):
                nc.vector.tensor_reduce(sc[b // 2][:, kind, (b % 2) * G:(b % 2 + 1) * G],
                                        products[b, kind].rearrange("t c (h r) -> t (c h) r", r=HP), axis=AX.X, op=ALU.add)

        FK, RK, DK = 0, 1, 2
        NK = 3
        W_COLS = 2 * 2 * KB

        def first_queries():
            ps = sm_ps.tile([P, KB, B], F32, name="sm")
            cols = wq.rearrange("p k (j i) -> p k i j", i=KB)
            for i in range(KB):
                for cb in range(KB):
                    nc.tensor.matmul(ps[:, i, :], cols[:, cb, i, :], e16[cb][:, 0:N:L], start=(cb == 0), stop=(cb == KB - 1))
            for s in (FK, RK):
                nc.vector.tensor_copy(q_ends[:, :, s, :], qb_t[:].unsqueeze(1).to_broadcast([P, B, KB]))
            nc.vector.tensor_tensor(q_ends[:, :, DK, :], ps.rearrange("p i b -> p b i"), qb_t[:].unsqueeze(1).to_broadcast([P, B, KB]), ALU.add)

        def split3_small(src, parts, rest):
            nc.gpsimd.tensor_copy(parts[0], src)
            nc.gpsimd.tensor_tensor(rest, src, parts[0], ALU.subtract)
            nc.gpsimd.tensor_copy(parts[1], rest)
            nc.gpsimd.tensor_tensor(rest, rest, parts[1], ALU.subtract)
            nc.gpsimd.tensor_copy(parts[2], rest)

        def pair_key(b):
            if b % 2 == 0:
                pair_keys[b // 2] = small.tile([P, 2, NK, KB], F32, name="pair_key")
            k, ends = kt[b], pair_keys[b // 2]
            first, last = (k[:, :, t:t + 1].rearrange("p i o -> p (i o)") for t in (0, L - 1))
            nc.gpsimd.tensor_copy(ends[:, b % 2, FK, :], first)
            nc.gpsimd.tensor_scalar(ends[:, b % 2, RK, :], ksum[b][:], 1.0 / L, 0.0, ALU.mult, ALU.add)
            nc.gpsimd.tensor_tensor(ends[:, b % 2, DK, :], last, first, ALU.subtract)

        w_parts = {}

        def first_weights(half):
            ends = pair_keys[half]
            parts = small.tile([P, KB, 2, 2, 3], BF16, name="key_parts")
            rest = small.tile([P, KB, 2, 2], F32, name="key_rest")
            split3_small(ends[:, :, FK:DK, :].rearrange("p b s i -> p i b s"), [parts[:, :, :, :, j] for j in range(3)], rest[:])
            by_head = small.tile([P, KB, 4, 3 * NH], BF16, name="by_head")
            nc.gpsimd.tensor_tensor(by_head.rearrange("p i x (j h) -> p (i x j) h", h=NH),
                                    parts.rearrange("p i b s j -> p (i b s j)").unsqueeze(2).to_broadcast([P, KB * 12, NH]),
                                    headsel16[:].unsqueeze(1).to_broadcast([P, KB * 12, NH]), ALU.mult)
            ps = sm_ps.tile([P, 4, KB, 3 * NH], F32, name="sm")
            for cb in range(KB):
                for i in range(KB):
                    nc.tensor.matmul(ps[:, :, cb, :], qw_flip[:, i, cb * P:(cb + 1) * P], by_head[:, i, :, :],
                                     start=(i == 0), stop=(i == KB - 1))
            prods = small.tile([P, 2 * NK, KB], F32, name="key_prods")
            nc.gpsimd.tensor_tensor(prods[:], ends.rearrange("p b s i -> p (b s) i"),
                                    q_ends[:, 2 * half:2 * half + 2, :, :].rearrange("p b s i -> p (b s) i"), ALU.mult)
            sums = small.tile([P, 2 * NK, 2], F32, name="key_sums")
            nc.gpsimd.tensor_tensor(sums[:], prods[:, :, 0:2], prods[:, :, 2:4], ALU.add)
            nc.gpsimd.tensor_tensor(sums[:, :, 0:1], sums[:, :, 0:1], sums[:, :, 1:2], ALU.add)
            w32 = small.tile([P, W_COLS + 2 * NK, NH], F32, name="w32")
            nc.gpsimd.tensor_tensor(w32[:, W_COLS:W_COLS + 2 * NK, :], sums[:, :, 0:1].to_broadcast([P, 2 * NK, NH]),
                                    headsel[:].unsqueeze(1).to_broadcast([P, 2 * NK, NH]), ALU.mult)
            nc.vector.tensor_reduce(w32[:, 0:W_COLS, :], ps.rearrange("p x c (j h) -> p (x c) h j", h=NH), axis=AX.X, op=ALU.add)
            w_rest = small.tile([P, W_COLS + 2 * NK, NH], F32, name="w_rest")
            w_parts[half] = small.tile([P, 3, W_COLS + 2 * NK, NH], BF16, name="w_parts")
            split3_small(w32[:], [w_parts[half][:, j, :, :] for j in range(3)], w_rest[:])

        def first_scores(b):
            half, b2 = b // 2, b % 2
            if b2 == 0:
                first_parts[half] = sm_ps.tile([P, 3, 2, GP], F32, name="sm")
            w3 = w_parts[half]
            dst = first_parts[half][:, :, :, b2 * G:(b2 + 1) * G].rearrange("t j s (c h) -> t j s c h", c=QN)
            for s in (FK, RK):
                share = w3[:, :, W_COLS + NK * b2 + s, :].unsqueeze(2).to_broadcast([P, 3, QN, NH])
                nc.tensor.matmul(dst[:, :, s, :, :], ones16[:], share, start=(s == FK), stop=False)
            for c4 in range(QN):
                for cb in range(KB):
                    keys = w3[:, :, b2 * 2 * KB + cb:(b2 + 1) * 2 * KB:KB, :]
                    nc.tensor.matmul(dst[:, :, :, c4, :], e16[cb][:, b * L + c4 * P:b * L + (c4 + 1) * P], keys, start=False, stop=False)
            nc.tensor.matmul(dst[:, :, FK, 0, :], token0[:], w3[:, :, W_COLS + NK * b2 + DK, :], start=False, stop=True)

        probs = held.tile([ROWS, B, 3, P], BF16, name="probs")

        def softmax_exp(half):
            sums = sc[half]
            pr = small.tile([P, 4, GP], F32, name="pr")
            nc.vector.tensor_reduce(pr[:, FIRST:, :], first_parts[half].rearrange("t j s g -> t (s g) j"), axis=AX.X, op=ALU.add)
            top = small.tile([P, 2, GP], F32, name="top")
            nc.vector.tensor_tensor(top[:], sums[:], pr[:, FIRST:, :], ALU.max)
            nc.vector.tensor_tensor(top[:, 0, :], top[:, 0, :], top[:, 1, :], ALU.max)
            for scores, kind in ((sums[:], NEXT), (pr[:, FIRST:, :], FIRST)):
                nc.vector.tensor_tensor(pr[:, kind:kind + 2, :], scores, top[:, 0:1, :].to_broadcast([P, 2, GP]), ALU.subtract)
            nc.scalar.activation(pr[:], pr[:], ACT.Exp, scale=HD ** -0.5)
            pr_t[half] = pr

        def softmax_norm(half):
            pr = pr_t[half]
            nc.vector.tensor_scalar_mul(pr[:, SELF, :], pr[:, SELF, :], 2.0)
            den = small.tile([P, GP], F32, name="den")
            nc.vector.tensor_reduce(den[:], pr.rearrange("t k g -> t g k"), axis=AX.X, op=ALU.add)
            nc.vector.reciprocal(den[:], den[:])
            nc.vector.tensor_tensor(pr[:], pr[:], den[:].unsqueeze(1).to_broadcast([P, 4, GP]), ALU.mult)
            three = small.tile([P, 3, GP, 3], BF16, name="three")
            rest = small.tile([P, 3, GP], F32, name="rest")
            split3(pr[:, 0:RELAY, :], three[:, :, :, 0], three[:, :, :, 1], three[:, :, :, 2], rest[:])
            three_t[half] = three

        def softmax_flip(half):
            three = three_t[half]
            flipped = sm_ps.tile([ROWS, 2, 3, P], BF16, name="sm")
            for b2 in range(2):
                for kind in (NEXT, SELF, FIRST):
                    nc.tensor.transpose(flipped[:, b2, kind, :],
                                        three[:, kind, b2 * G:(b2 + 1) * G, :].rearrange("t g j -> t (g j)"), ident16[:])
            nc.scalar.copy(probs[:, 2 * half:2 * half + 2, :, :], flipped[:])

        pb_t, own_t, a_t, asum_t, mean_t, std_t, y_t = {}, {}, {}, {}, {}, {}, {}

        def spread(b, h, *kinds):
            pb = ring_v.tile([P, len(kinds), LH], F32, name="ring")
            for tb in range(HQ):
                nc.tensor.matmul(pb[:, :, tb * P:(tb + 1) * P], sel16[:, h * HQ + tb, :], probs[:, b, kinds[0]:kinds[-1] + 1, :],
                                 start=True, stop=True)
            for k, kind in enumerate(kinds):
                pb_t[b, h, kind] = pb[:, k, :]

        def context_self(b, h):
            v, neg, pb, t0 = vt[b], vneg[b], pb_t[b, h, SELF], h * LH
            own = ctx_pool.tile([P, KB, LH], F32, name="own")
            for i in range(KB):
                nc.vector.scalar_tensor_tensor(own[:, i, :], v[:, i, t0:t0 + LH], neg[:, i:i + 1], pb, ALU.add, ALU.mult)
            own_t[b, h] = own

        def context_first(b, h):
            own, ends, pb = own_t[b, h], vends[b], pb_t[b, h, FIRST]
            for i in range(KB):
                nc.vector.scalar_tensor_tensor(own[:, i, :], pb, ends[:, 0, i:i + 1], own[:, i, :], ALU.mult, ALU.add)
            if h == 0:
                own0 = own[:, :, 0:1].rearrange("p i o -> p (i o)")
                nc.vector.scalar_tensor_tensor(own0, ends[:, 1, :], pb[:, 0:1], own0, ALU.mult, ALU.add)

        def context_next(b, h):
            v, neg, own, pb, t0 = vt[b], vneg[b], own_t[b, h], pb_t[b, h, NEXT], h * LH
            nxt = ctx_pool.tile([P, KB, LH], F32, name="nxt")
            ctx16[b, h] = ctx_pool.tile([P, KB, LH], BF16, name="ctx16")
            for i in range(KB + 1):
                if i < KB:
                    nc.vector.scalar_tensor_tensor(nxt[:, i, :], v[:, i, t0 + 1:t0 + LH + 1], neg[:, i:i + 1], pb, ALU.add, ALU.mult)
                if i >= 1:
                    nc.vector.scalar_tensor_tensor(ctx16[b, h][:, i - 1, :], nxt[:, i - 1, :], vr[b][:, i - 1:i], own[:, i - 1, :],
                                                   ALU.add, ALU.add)

        def hidden(b, h, turns=()):
            a_t[b, h] = ln_pool.tile([P, HQ, D], F32, name="a")
            asum_t[b, h] = ln_pool.tile([P, HQ], F32, name="asum")
            for tb in range(HQ):
                ps = ring_s.tile([P, D], F32, name="ring")
                for i in range(KB):
                    nc.tensor.matmul(ps[:], ctx16[b, h][:, i, tb * P:(tb + 1) * P], wo[:, i, :], start=(i == 0), stop=False)
                    if turns:
                        turns[tb * KB + i]()
                nc.tensor.matmul(ps[:], ones16[:], ob16[:], start=False, stop=True)
                nc.scalar.activation(a_t[b, h][:, tb, :], ps[:], ACT.Relu, accum_out=asum_t[b, h][:, tb:tb + 1])

        def norm_stats(b, h):
            a = a_t[b, h]
            std = ln_pool.tile([P, HQ], F32, name="std")
            if (b, h) == (B - 1, 1):
                stats = ln_pool.tile([P, HQ, 6], F32, name="stats")
                mv = ln_pool.tile([P, HQ, 2], F32, name="mv")
                for tb in range(HQ):
                    nc.vector.bn_stats(stats[:, tb, :], a[:, tb, :])
                    nc.vector.bn_aggr(mv[:, tb, :], stats[:, tb, :])
                mean_t[b, h] = [mv[:, tb, 0:1] for tb in range(HQ)], ALU.subtract
                nc.scalar.activation(std[:], mv[:, :, 1], ACT.Sqrt, bias=eps[:, 0:1])
            else:
                negu = ln_pool.tile([P, HQ], F32, name="negu")
                nc.scalar.mul(negu[:], asum_t[b, h][:], -1.0 / D)
                ssq = ln_pool.tile([P, HQ], F32, name="ssq")
                for tb in range(HQ):
                    sq = ln_pool.tile([P, D], F32, name="sq")
                    nc.scalar.activation(sq[:], a[:, tb, :], ACT.Square, bias=negu[:, tb:tb + 1], accum_out=ssq[:, tb:tb + 1])
                mean_t[b, h] = [negu[:, tb:tb + 1] for tb in range(HQ)], ALU.add
                nc.scalar.activation(std[:], ssq[:], ACT.Sqrt, bias=eps[:, 0:1], scale=1.0 / D)
            std_t[b, h] = std

        def norm_apply(b, h):
            a, (mean, op) = a_t[b, h], mean_t[b, h]
            rstd = ln_pool.tile([P, HQ], F32, name="rstd")
            nc.vector.reciprocal(rstd[:], std_t[b, h][:])
            z = ln_pool.tile([P, HQ, D], F32, name="z")
            for tb in range(HQ):
                nc.vector.tensor_scalar(z[:, tb, :], a[:, tb, :], mean[tb], rstd[:, tb:tb + 1], op, ALU.mult)
            z_t[b, h] = z

        def norm_turns(b, h):
            z = z_t[b, h]
            y16 = y_pool.tile([P, KB, LH], BF16, name="y16")
            y_t[b, h] = y16
            zt = {}

            def turn(i, tb):
                def go():
                    if i % 2 == 0 and tb == 0:
                        zt[i // 2] = ring_s.tile([P, 2, LH], F32, name="ring")
                    nc.tensor.transpose(zt[i // 2][:, i % 2, tb * P:(tb + 1) * P], z[:, tb, i * P:(i + 1) * P], ident[:])
                    if i % 2 == 1 and tb == HQ - 1:
                        for j in (i - 1, i):
                            y, x, weight, bias = y16[:, j, :], zt[i // 2][:, j % 2, :], lnw_t[:, j:j + 1], lnb_t[:, j:j + 1]
                            if (b, h) == (B - 1, 1) and j % 2 == 1:
                                nc.vector.tensor_scalar(y, x, weight, bias, ALU.mult, ALU.add)
                            else:
                                nc.scalar.activation(y, x, ACT.Identity, bias=bias, scale=weight)
                return go
            return [turn(i, tb) for i in range(KB) for tb in range(HQ)]

        def tags(b, h):
            ps = ring_s.tile([T, LH], F32, name="ring")
            for i in range(KB):
                nc.tensor.matmul(ps[:], wf[:, i, :], y_t[b, h][:, i, :], start=(i == 0), stop=(i == KB - 1))
            res = y_pool.tile([T, LH], F32, name="res")
            nc.scalar.activation(res[:], ps[:], ACT.Identity, bias=ofcb_t[:, 0:1])
            nc.sync.dma_start(out[:, b * L + h * LH:b * L + (h + 1) * LH], res[:])

        def values_of_step(b):
            return b - (B - 1) if b >= B - 1 else None

        def value_blocks(vb_seq):
            if vb_seq is None:
                return []
            values_open(vb_seq)
            return [(value_block, vb_seq, i) for i in range(KB)]

        pair_key(0)
        for b in range(B):
            scores_open(b)
            others = value_blocks(values_of_step(b))
            if b + 1 < B:
                keys_open(b + 1)
                others = [(key_block, b + 1, i) for i in range(KB)] + others
            for i in range(KB):
                score_block(b, i)
                for (block, block_b, block_i), kind in zip(others[2 * i:2 * i + 2], (NEXT, SELF)):
                    block(block_b, block_i, products_turns(b - 1, kind) if i == 1 and b >= 1 else ())
                if b == 1 and i == 0:
                    first_queries()
                if b % 2 == 1 and i == 2:
                    first_weights(b // 2)
                if i == 2 and b >= 1:
                    head_sums(b - 1)
                if b == 2 and i == 2:
                    first_scores(0)
                    first_scores(1)
                if b == 2 and i == 3:
                    softmax_exp(0)
                if b == 3 and i == 0:
                    softmax_norm(0)
                if b == 3 and i == 3:
                    softmax_flip(0)
            if b + 1 < B:
                keys_edge(b + 1)
                pair_key(b + 1)
        spread(0, 0, SELF, FIRST)
        values_edge(values_of_step(B - 1))
        for block, block_b, block_i in value_blocks(values_of_step(B)):
            block(block_b, block_i, products_turns(B - 1, (NEXT, SELF)[block_i]) if block_i < 2 else ())
        head_sums(B - 1)

        def stage(step, u, *args):
            if 0 <= u < 2 * B:
                step(u // 2, u % 2, *args)

        others = []
        for b in range(values_of_step(B) + 1, B):
            others += value_blocks(b)
        for u in range(2 * B + 4):
            stage(spread, u, NEXT)
            stage(context_self, u)
            turns = norm_turns((u - 3) // 2, (u - 3) % 2) if 0 <= u - 3 < 2 * B else ()
            if 0 <= u - 1 < 2 * B:
                hidden((u - 1) // 2, (u - 1) % 2, turns)
            else:
                for turn in turns:
                    turn()
            stage(spread, u + 1, SELF, FIRST)
            stage(context_first, u)
            stage(context_next, u)
            for block, block_b, block_i in others[2 * u:2 * u + 2]:
                block(block_b, block_i)
            if u == 1:
                softmax_exp(1)
                softmax_norm(1)
            stage(norm_stats, u - 1)
            stage(tags, u - 3)
            stage(norm_apply, u - 2)
            if u % 2 == 0 and u // 2 + 1 < B:
                values_edge(u // 2 + 1)
            if u == 0:
                first_scores(B - 2)
                first_scores(B - 1)
            if u == 2:
                softmax_flip(1)
